import numpy as np
import ml_dtypes


def mxq(x, axis, fmt="e4m3"):
    dtype, down = {"e4m3": (ml_dtypes.float8_e4m3fn, 7), "e5m2": (ml_dtypes.float8_e5m2, 14)}[fmt]
    v = np.moveaxis(np.asarray(x, np.float32).astype(ml_dtypes.bfloat16).astype(np.float64), axis, -1)
    blocks = v.reshape(v.shape[:-1] + (-1, 32))
    amax = np.abs(blocks).max(-1, keepdims=True)
    byte = np.maximum(np.where(amax > 0, np.frexp(amax)[1] - 1 + 127, 0) - down, 1)
    scale = np.exp2(byte - 127.0)
    codes = (blocks / scale).astype(np.float32).astype(dtype).astype(np.float64)
    return np.moveaxis((codes * scale).reshape(v.shape), -1, axis)


WIDE = False


def mx_kscale(k):
    if not WIDE:
        return np.ones(k)
    levels = np.array([10, -10, 5, -5, 0])
    a = np.random.permutation(np.resize(levels, k // 512 * 4)).reshape(k // 512, 4)
    idx = np.arange(k)
    return np.exp2(a[idx // 512, idx % 128 // 32])


BF16 = ml_dtypes.bfloat16


def bf(x):
    return np.asarray(x, np.float32).astype(BF16)


def f64(x):
    return np.asarray(x).astype(np.float64)


E2M1 = np.array([0.0, 0.5, 1.0, 1.5, 2.0, 3.0, 4.0, 6.0, -0.0, -0.5, -1.0, -1.5, -2.0, -3.0, -4.0, -6.0])


def pack_weight(w, fmt):
    k, n = w.shape
    w = f64(bf(w)).reshape(k // 32, 32, n)
    amax = np.abs(w).max(1)
    if fmt == "e4m3":
        byte = np.frexp(amax)[1] - 1 + 127 - 7
    else:
        mant, ex = np.frexp(amax / 6.0)
        byte = np.where(mant > 0.5, ex, ex - 1) + 127
    byte = np.clip(np.where(amax > 0, byte, 1), 1, 254)
    scaled = (w * np.exp2(127.0 - byte)[:, None, :]).reshape(k, n).astype(np.float32)
    by_word = np.ascontiguousarray(scaled.reshape(k // 512, 128, 4, n).transpose(0, 1, 3, 2))
    if fmt == "e4m3":
        words = by_word.astype(ml_dtypes.float8_e4m3fn).view(np.uint8)
    else:
        c = by_word.astype(ml_dtypes.float4_e2m1fn).view(np.uint8) & 0xF
        words = c[..., 0::2] | (c[..., 1::2] << 4)
    return np.ascontiguousarray(words), np.ascontiguousarray(byte.astype(np.uint8).reshape(k // 512, 16, n))


def unpack_weight(words, scales, fmt):
    g, p, n, _ = words.shape
    if fmt == "e4m3":
        vals = np.ascontiguousarray(words).view(ml_dtypes.float8_e4m3fn).astype(np.float64)
    else:
        nib = np.empty((g, p, n, 4), np.uint8)
        nib[..., 0::2] = words & 0xF
        nib[..., 1::2] = words >> 4
        vals = E2M1[nib]
    vals = vals * np.repeat(np.exp2(scales.astype(np.float64) - 127.0), 8, axis=1)[..., None]
    return vals.transpose(0, 1, 3, 2).reshape(g * 512, n)


B, N, D, H, HD, S, DO = 1, 128, 8192, 16, 64, 11, 1024
E = H * HD
D4 = [0.4829629131445341, 0.8365163037378079, 0.2241438680420134, -0.1294095225512604]
T = len(D4)


def elu1(u):
    return np.where(u > 0.0, u, np.exp(np.minimum(u, 0.0)) - 1.0) + 1.0


def softplus(u):
    return np.log(1.0 + np.exp(u))


def shifted(t, o):
    if o == 0:
        return t
    return np.concatenate([np.zeros((B, H, o, HD)), t[:, :, :N - o, :]], axis=2)


def setup_inputs():
    s = mx_kscale(D)
    lg = np.random.standard_normal((B, H, N, S)) * 1.4
    g = np.exp(lg - lg.max(-1, keepdims=True))
    x = bf(np.random.standard_normal((B, N, D)) * s)
    w = np.random.standard_normal((3 * E, D)) * 0.6 / np.sqrt(D) / s
    words, scales = pack_weight(w.T, "e4m3")
    return {"x": x,
            "W_qkv_words": words,
            "W_qkv_scales": scales,
            "b_qkv": bf(np.random.standard_normal(3 * E) * 0.1),
            "gains": bf(g / g.sum(-1, keepdims=True)),
            "pos_bias": bf(np.random.standard_normal((S * T, H)) * 0.5),
            "identity_bypass": bf(-1.0 + 0.5 * np.random.standard_normal(H))}


def reference(x, W_qkv_words, W_qkv_scales, b_qkv, gains, pos_bias, identity_bypass):
    qkv = (mxq(f64(x), 2, "e4m3") @ unpack_weight(W_qkv_words, W_qkv_scales, "e4m3")) + f64(b_qkv)
    q, k, v = [t.reshape(B, N, H, HD).transpose(0, 2, 1, 3) for t in np.split(qkv, 3, axis=-1)]
    g, pb = f64(gains), f64(pos_bias)
    acc = np.zeros((B, H, N, HD))
    z = np.zeros((B, H, N, 1))
    tap = 0
    for j in range(S):
        d = 1 << j
        g_j = g[..., j][..., None]
        for tau, c in enumerate(D4):
            o = d * tau
            bias = pb[tap].reshape(1, H, 1, 1)
            tap += 1
            if o != 0 and o >= N:
                continue
            k_s, v_s = shifted(k, o), shifted(v, o)
            feat = elu1(np.sum(q * k_s, -1, keepdims=True) + bias)
            acc = acc + (g_j * c) * feat * v_s
            z = z + g_j * abs(c) * feat
    p = softplus(f64(identity_bypass)).reshape(1, H, 1, 1)
    local = elu1(np.sum(q * k, -1, keepdims=True))
    acc = acc + p * local * v
    z = z + p * local
    res = acc / (z + 1e-06)
    return res.transpose(0, 2, 1, 3).reshape(B, N, E)

@@ -1,0 +1,558 @@
+from contextlib import ExitStack
+
+import concourse.mybir as mybir
+from concourse.masks import make_identity
+
+F32 = mybir.dt.float32
+BF16 = mybir.dt.bfloat16
+I32 = mybir.dt.int32
+U32 = mybir.dt.uint32
+U8 = mybir.dt.uint8
+FP8X4 = mybir.dt.float8_e4m3fn_x4
+ALU = mybir.AluOpType
+ACT = mybir.ActivationFunctionType
+AXIS_X = mybir.AxisListType.X
+
+P = 128
+TOKENS = 128
+D_MODEL = 8192
+HEADS = 16
+HEAD_DIM = 64
+EMB = HEADS * HEAD_DIM
+SCALES = 11
+TAPS = 4
+D4 = [0.4829629131445341, 0.8365163037378079, 0.2241438680420134, -0.1294095225512604]
+EPS = 1e-06
+
+K_PASS = 512
+PASSES = D_MODEL // K_PASS
+BANK = 512
+PLANES = 4
+
+GROUP = 8
+GROUPS = TOKENS // GROUP
+SLOTS = P // GROUP
+PAD = TOKENS - GROUP
+
+FLOPS = 2 * TOKENS * D_MODEL * 3 * EMB
+
+
+def taps_of(taus):
+    return [(j, tau, tau << j) for j in range(SCALES) for tau in taus if (tau << j) < TOKENS]
+
+
+LAYER_TAUS = [(1, 3), (2,)]
+
+
+W_BUFS = 7
+
+
+def tile_dwarfattention_pa_k_kernel(
+    tc, x, W_qkv_words, W_qkv_scales, b_qkv, gains, pos_bias, identity_bypass, out
+):
+    nc = tc.nc
+    n_pb = SCALES * TAPS * HEADS
+    with ExitStack() as stack:
+        stack.enter_context(tc.manual_schedule())
+        keep = stack.enter_context(tc.tile_pool(name="keep", bufs=1))
+        wpool = stack.enter_context(tc.tile_pool(name="weights", bufs=W_BUFS))
+        accs = stack.enter_context(tc.psum_pool(name="accs", bufs=4))
+        work = stack.enter_context(tc.psum_pool(name="work", bufs=4))
+
+        ident_f = keep.tile([P, P], F32)
+        ident_b = keep.tile([P, P], BF16)
+        ones_b = keep.tile([P, P], BF16)
+        ones_f = keep.tile([P, 2], F32)
+        minus_one = keep.tile([P, 1], F32)
+        half_mask = keep.tile([P, 2], F32)
+        x_codes = keep.tile([P, PASSES * TOKENS], U32, align_bytes=64)
+        x_scales = keep.tile([P, PASSES * TOKENS], U8, align_bytes=64)
+        w_planes = keep.tile([P, PASSES // PLANES, 3 * EMB], U8, align_bytes=64)
+        bias_all = keep.tile([P, 3 * EMB], BF16)
+        bias_tab = [keep.tile([P, HEADS, TOKENS], F32, name="bias_tab%d" % i) for i in range(2)]
+        gain_tab = [keep.tile([P, HEADS, TOKENS], F32, name="gain_tab%d" % i) for i in range(2)]
+        sign_tab = keep.tile([P, TOKENS], F32)
+        diag_bias = keep.tile([P, HEADS, SCALES + 1], F32)
+        diag_gain = keep.tile([P, HEADS, SCALES + 1], F32)
+        z_fixed = keep.tile([P, HEADS], F32)
+        at_all = keep.tile([P, HEADS, TOKENS], F32)
+        qk_same = keep.tile([P, HEADS], F32)
+        w_diag = keep.tile([P, HEADS], F32)
+        z_all = keep.tile([P, HEADS], F32)
+        z_inv = keep.tile([P, HEADS], F32)
+        w_diag_n = keep.tile([P, HEADS], F32)
+
+        w_words = W_qkv_words.rearrange("g p n t -> p g (n t)").bitcast(I32)
+        w_loads = [(g0, 2, 0, 3 * BANK) for g0 in range(0, PASSES, 2)]
+        w_loads += [(g0, 4, 3 * BANK, BANK) for g0 in range(0, PASSES, 4)]
+        first_v_load = len(w_loads)
+        g0 = 0
+        while g0 < PASSES:
+            n_g = min(2, max(1, (PASSES - g0) // 2))
+            w_loads.append((g0, n_g, 2 * EMB, 2 * BANK))
+            g0 += n_g
+        w_tiles = []
+
+        def load_weights_up_to(n):
+            for g0, n_g, col0, n_cols in w_loads[len(w_tiles) : n]:
+                w = wpool.tile([P, n_g, n_cols], U32, tag="w", align_bytes=64)
+                nc.sync.dma_start(out=w[:].bitcast(I32), in_=w_words[:, g0 : g0 + n_g, col0 : col0 + n_cols])
+                w_tiles.append(w)
+
+        def mx_passes(first, last, banks):
+            for t in range(first, last):
+                g0, n_g, col0, n_cols = w_loads[t]
+                for gi in range(n_g):
+                    g = g0 + gi
+                    for i, bank in enumerate(banks):
+                        nc.tensor.matmul_mx(
+                            out=bank[:],
+                            lhsT=x_codes[:, TOKENS * g : TOKENS * (g + 1)].bitcast(FP8X4),
+                            lhsT_scale=x_scales[:, TOKENS * g : TOKENS * (g + 1)],
+                            rhs=w_tiles[t][:, gi, BANK * i : BANK * (i + 1)].bitcast(FP8X4),
+                            rhs_scale=w_planes[
+                                4 * (g % PLANES) : P, g // PLANES, col0 + BANK * i : col0 + BANK * (i + 1)
+                            ],
+                            start=(g == 0),
+                            stop=(g == PASSES - 1),
+                        )
+                load_weights_up_to(t + 1 + W_BUFS)
+
+        def elu_plus_one(dst, u, tmp):
+            nc.scalar.activation(out=dst, in_=u, func=ACT.Exp)
+            nc.vector.tensor_scalar(out=tmp, in0=u, scalar1=0.0, scalar2=1.0, op0=ALU.max, op1=ALU.add)
+            nc.vector.tensor_tensor(out=dst, in0=dst, in1=tmp, op=ALU.min)
+
+        with tc.tile_pool(name="setup", bufs=1) as setup:
+            small_row = setup.tile([P, n_pb + HEADS], BF16)
+            nc.vector.memset(small_row[:], 0.0)
+            nc.scalar.dma_start(out=small_row[0:1, 0:n_pb], in_=pos_bias.rearrange("(o r) h -> o (r h)", o=1))
+            nc.scalar.dma_start(out=small_row[0:1, n_pb:], in_=identity_bypass.rearrange("(o h) -> o h", o=1))
+            gains_hg = setup.tile([P, 2, GROUP * SCALES], BF16)
+            nc.scalar.dma_start(
+                out=gains_hg[:],
+                in_=gains.rearrange("o h (g a) j -> (o h g) (a j)", a=GROUP).rearrange("(t p) e -> p t e", p=P),
+            )
+            nc.vector.memset(w_planes[:].rearrange("p a n -> p (a n)").bitcast(I32), 0)
+            make_identity(nc, ident_f[:])
+            make_identity(nc, ident_b[:])
+            nc.gpsimd.memset(ones_b[:], 1.0)
+            nc.gpsimd.memset(ones_f[:], 1.0)
+            nc.gpsimd.memset(minus_one[:], -1.0)
+            nc.gpsimd.memset(half_mask[:], 0.0)
+            nc.gpsimd.memset(half_mask[0:HEAD_DIM, 0:1], 1.0)
+            nc.gpsimd.memset(half_mask[HEAD_DIM:P, 1:2], 1.0)
+
+            x_sb = setup.tile([P, D_MODEL], BF16)
+            x_rows = x.rearrange("o n k -> (o n) k")
+            for c in range(4):
+                cols = slice(c * D_MODEL // 4, (c + 1) * D_MODEL // 4)
+                nc.sync.dma_start(out=x_sb[:, cols], in_=x_rows[:, cols])
+            for a in range(PASSES // PLANES):
+                for quad in range(4):
+                    nc.sync.dma_start(
+                        out=w_planes[32 * quad : 32 * quad + 16, a, :].bitcast(I32),
+                        in_=W_qkv_scales[PLANES * a : PLANES * (a + 1), 4 * quad : 4 * quad + 4, :].bitcast(I32),
+                    )
+            load_weights_up_to(W_BUFS)
+
+            gains_h = setup.tile([P, TOKENS * SCALES], BF16)
+            nc.gpsimd.memset(gains_h[:], 0.0)
+            nc.gpsimd.dma_start(out=gains_h[0:HEADS, :], in_=gains.rearrange("o h n j -> (o h) (n j)"))
+            bias_row = setup.tile([P, 3 * EMB], BF16)
+            nc.gpsimd.memset(bias_row[:], 0.0)
+            nc.gpsimd.dma_start(out=bias_row[0:1, :], in_=b_qkv.rearrange("(o n) -> o n", o=1))
+
+            token_of_row = setup.tile([P, GROUP], F32)
+            nc.vector.tensor_reduce(
+                out=token_of_row[:], in_=ident_f[:].rearrange("p (a s) -> p a s", s=SLOTS), op=ALU.add, axis=AXIS_X
+            )
+            slot_of_row = setup.tile([P, SLOTS], F32)
+            nc.vector.tensor_reduce(
+                out=slot_of_row[:], in_=ident_f[:].rearrange("p (a s) -> p s a", s=SLOTS), op=ALU.add, axis=AXIS_X
+            )
+            pb_first_step = [(1, 2), (2, 4)]
+            win_entries = []
+            for layer, taus in enumerate(LAYER_TAUS):
+                first, step = pb_first_step[layer]
+                win_entries.append([((TAPS * j + tau - first) // step, o, 1.0) for j, tau, o in taps_of(taus)])
+            for taus in LAYER_TAUS:
+                win_entries.append([(j, o, D4[tau]) for j, tau, o in taps_of(taus)])
+            win_t = setup.tile([P, 4, GROUP, SLOTS], F32)
+            nc.vector.memset(win_t[:], 0.0)
+            for i, entries in enumerate(win_entries):
+                for s, o, coef in entries:
+                    nc.vector.scalar_tensor_tensor(
+                        out=win_t[:, i, :, s],
+                        in0=ident_f[:, PAD - o : PAD - o + GROUP],
+                        scalar=coef,
+                        in1=win_t[:, i, :, s],
+                        op0=ALU.mult,
+                        op1=ALU.add,
+                    )
+            bias_win = setup.tile([P, 2, PAD + P], BF16)
+            gain_win = setup.tile([P, 2, PAD + P], F32)
+            nc.vector.memset(bias_win[:], 0.0)
+            nc.vector.memset(gain_win[:], 0.0)
+            gains_pad = setup.tile([P, 2, GROUP, SLOTS], BF16)
+            nc.vector.memset(gains_pad[:], 0.0)
+            nc.vector.tensor_copy(
+                out=gains_pad[:, :, :, 0:SCALES], in_=gains_hg[:].rearrange("p t (a j) -> p t a j", j=SCALES)
+            )
+
+            small_all = setup.tile([P, n_pb + HEADS], F32)
+            half = (n_pb + HEADS) // 2
+            for i in range(2):
+                ps = work.tile([P, half], F32, tag="work")
+                nc.tensor.matmul(out=ps[:], lhsT=ones_b[:], rhs=small_row[:, half * i : half * (i + 1)], start=True, stop=True)
+                nc.vector.tensor_copy(out=small_all[:, half * i : half * (i + 1)], in_=ps[:])
+            pb_all = small_all[:, 0:n_pb]
+            pb_by_tau = pb_all.rearrange("p (j t h) -> p t h j", t=TAPS, h=HEADS)
+            bypass_all = small_all[:, n_pb:]
+
+            x_words = x_sb[:].bitcast(F32)
+            grouped = setup.tile([P, PASSES, TOKENS, 4], BF16, align_bytes=64)
+            grouped_flat = grouped[:].rearrange("p g t e -> p (g t e)")
+            grouped_words = grouped_flat.bitcast(F32).rearrange("p (g t u) -> p g t u", g=PASSES, u=2)
+
+            def transpose_x(first_pair, last_pair):
+                for pair in range(first_pair, last_pair):
+                    xt = work.tile([P, 2, 2, TOKENS], F32, tag="work")
+                    for gi in range(2):
+                        g = 2 * pair + gi
+                        for u in range(2):
+                            nc.tensor.transpose(xt[:, gi, u, :], x_words[:, 256 * g + u : 256 * (g + 1) : 2], ident_f[:])
+                    nc.scalar.copy(
+                        out=grouped_words[:, 2 * pair : 2 * pair + 2, :, :], in_=xt[:].rearrange("p g u t -> p g t u")
+                    )
+
+            transpose_x(0, 2)
+            win_ps = work.tile([P, 4, P], F32, tag="work")
+            for i in range(4):
+                nc.tensor.transpose(win_ps[:, i, :], win_t[:, i, :, :].rearrange("p a s -> p (a s)"), ident_f[:])
+            nc.scalar.copy(out=bias_win[:, :, 0:P], in_=win_ps[:, 0:2, :])
+            nc.scalar.copy(out=gain_win[:, :, 0:P], in_=win_ps[:, 2:4, :])
+            gains_ps = work.tile([P, 2, P], BF16, tag="work")
+            for t in range(2):
+                nc.tensor.transpose(gains_ps[:, t, :], gains_pad[:, t, :, :].rearrange("p a s -> p (a s)"), ident_b[:])
+            transpose_x(2, PASSES // 2)
+
+            gains_rows = setup.tile([P, HEADS, GROUPS], F32)
+            nc.vector.tensor_copy(
+                out=gains_rows[:].rearrange("p h g -> p (h g)"), in_=gains_ps[:].rearrange("p t c -> p (t c)")
+            )
+            gain_moving = setup.tile([P, GROUPS, HEADS, GROUP], F32)
+            nc.vector.tensor_tensor(
+                out=gain_moving[:],
+                in0=gains_rows[:].rearrange("p h g -> p g h").unsqueeze(3).to_broadcast([P, GROUPS, HEADS, GROUP]),
+                in1=token_of_row[:].unsqueeze(1).unsqueeze(1).to_broadcast([P, GROUPS, HEADS, GROUP]),
+                op=ALU.mult,
+            )
+            bias_moving = setup.tile([P, 2, HEADS, GROUP], BF16)
+            for layer in range(2):
+                first, step = pb_first_step[layer]
+                n_slots = min(SLOTS, (SCALES * TAPS - first + step - 1) // step)
+                picked = setup.tile([P, HEADS, SLOTS], F32, tag="picked", bufs=2)
+                nc.vector.tensor_tensor(
+                    out=picked[:, :, 0:n_slots],
+                    in0=pb_all.rearrange("p (r h) -> p h r", h=HEADS)[:, :, first : first + step * (n_slots - 1) + 1 : step],
+                    in1=slot_of_row[:, 0:n_slots].unsqueeze(1).to_broadcast([P, HEADS, n_slots]),
+                    op=ALU.mult,
+                )
+                pb_rows = setup.tile([P, HEADS], F32, tag="pb_rows", bufs=2)
+                nc.vector.tensor_reduce(out=pb_rows[:], in_=picked[:, :, 0:n_slots], op=ALU.add, axis=AXIS_X)
+                nc.vector.tensor_tensor(
+                    out=bias_moving[:, layer, :, :],
+                    in0=pb_rows[:].unsqueeze(2).to_broadcast([P, HEADS, GROUP]),
+                    in1=token_of_row[:].unsqueeze(1).to_broadcast([P, HEADS, GROUP]),
+                    op=ALU.mult,
+                )
+
+            for quarter in range(4):
+                cols = slice(4 * TOKENS * quarter, 4 * TOKENS * (quarter + 1))
+                nc.vector.quantize_mx(
+                    out=x_codes[:, cols].bitcast(FP8X4),
+                    scales=x_scales[:, cols],
+                    in_=grouped_flat[:, 4 * K_PASS * quarter : 4 * K_PASS * (quarter + 1)],
+                )
+
+            def table_quarter(quarter):
+                cols = slice(4 * GROUP * quarter, 4 * GROUP * (quarter + 1))
+                for layer in range(2):
+                    bias_ps = work.tile([P, 4, HEADS, GROUP], F32, tag="work")
+                    gain_ps = work.tile([P, 4, HEADS, GROUP], F32, tag="work")
+                    for gl in range(4):
+                        grp = 4 * quarter + gl
+                        nc.tensor.matmul(
+                            out=bias_ps[:, gl, :, :],
+                            lhsT=bias_win[:, layer, PAD - GROUP * grp : PAD - GROUP * grp + P],
+                            rhs=bias_moving[:, layer, :, :],
+                            start=True,
+                            stop=True,
+                        )
+                    for gl in range(4):
+                        grp = 4 * quarter + gl
+                        nc.tensor.matmul(
+                            out=gain_ps[:, gl, :, :],
+                            lhsT=gain_win[:, layer, PAD - GROUP * grp : PAD - GROUP * grp + P],
+                            rhs=gain_moving[:, grp, :, :],
+                            start=True,
+                            stop=True,
+                        )
+                    nc.scalar.activation(
+                        out=bias_tab[layer][:, :, cols].rearrange("p h (g a) -> p h g a", a=GROUP),
+                        in_=bias_ps[:].rearrange("p g h a -> p h g a"),
+                        func=ACT.Identity,
+                        bias=ones_f[:, 0:1],
+                    )
+                    nc.vector.tensor_copy(
+                        out=gain_tab[layer][:, :, cols].rearrange("p h (g a) -> p h g a", a=GROUP),
+                        in_=gain_ps[:].rearrange("p g h a -> p h g a"),
+                    )
+
+            def spread_b_qkv():
+                for i in range(3 * EMB // BANK):
+                    ps = work.tile([P, BANK], F32, tag="work")
+                    nc.tensor.matmul(
+                        out=ps[:], lhsT=ones_b[:], rhs=bias_row[:, BANK * i : BANK * (i + 1)], start=True, stop=True
+                    )
+                    nc.scalar.copy(out=bias_all[:, BANK * i : BANK * (i + 1)], in_=ps[:])
+
+            gains_nt = setup.tile([P, HEADS, SCALES], F32)
+
+            def transpose_gains():
+                for j0 in range(0, SCALES, 8):
+                    n_j = min(8, SCALES - j0)
+                    ps = work.tile([P, 8, P], BF16, tag="work")
+                    for j in range(n_j):
+                        nc.tensor.transpose(ps[:, j, :], gains_h[:, j0 + j : TOKENS * SCALES : SCALES], ident_b[:])
+                    nc.vector.tensor_copy(
+                        out=gains_nt[:, :, j0 : j0 + n_j], in_=ps[:, 0:n_j, 0:HEADS].rearrange("p j h -> p h j")
+                    )
+
+            def small_tables():
+                nc.vector.memset(sign_tab[:], 1.0)
+                for j, tau, o in taps_of((3,)):
+                    nc.vector.scalar_tensor_tensor(
+                        out=sign_tab[:, o:],
+                        in0=ident_f[:, 0 : TOKENS - o],
+                        scalar=-2.0,
+                        in1=sign_tab[:, o:],
+                        op0=ALU.mult,
+                        op1=ALU.add,
+                    )
+                soft = setup.tile([P, HEADS], F32)
+                nc.scalar.activation(out=soft[:], in_=bypass_all, func=ACT.Abs)
+                nc.scalar.activation(out=soft[:], in_=soft[:], func=ACT.Exp, scale=-1.0)
+                nc.scalar.activation(out=soft[:], in_=soft[:], func=ACT.Ln, bias=ones_f[:, 0:1])
+                nc.vector.scalar_tensor_tensor(
+                    out=diag_gain[:, :, SCALES], in0=bypass_all, scalar=0.0, in1=soft[:], op0=ALU.max, op1=ALU.add
+                )
+                nc.vector.tensor_scalar_mul(out=diag_gain[:, :, 0:SCALES], in0=gains_nt[:], scalar1=D4[0])
+                nc.vector.memset(diag_bias[:, :, SCALES], 0.0)
+                nc.vector.tensor_copy(out=diag_bias[:, :, 0:SCALES], in_=pb_by_tau[:, 0, :, :])
+
+                f_of_bias = setup.tile([P, n_pb], F32)
+                f_tmp = setup.tile([P, n_pb], F32)
+                elu_plus_one(f_of_bias[:], pb_all, f_tmp[:])
+                f_by_tau = f_of_bias[:].rearrange("p (j t h) -> p t h j", t=TAPS, h=HEADS)
+                nc.vector.memset(z_fixed[:], EPS)
+                for tau in range(1, TAPS):
+                    taps = taps_of((tau,))
+                    n_j = len(taps)
+                    before = setup.tile([P, 8], F32, tag="before", bufs=2)
+                    for j, same_tau, o in taps:
+                        nc.vector.tensor_reduce(out=before[:, j : j + 1], in_=ident_f[:, 0:o], op=ALU.add, axis=AXIS_X)
+                    gf = setup.tile([P, HEADS, 8], F32, tag="gf", bufs=2)
+                    nc.vector.tensor_tensor(
+                        out=gf[:, :, 0:n_j], in0=gains_nt[:, :, 0:n_j], in1=f_by_tau[:, tau, :, 0:n_j], op=ALU.mult
+                    )
+                    nc.vector.tensor_tensor(
+                        out=gf[:, :, 0:n_j],
+                        in0=gf[:, :, 0:n_j],
+                        in1=before[:, 0:n_j].unsqueeze(1).to_broadcast([P, HEADS, n_j]),
+                        op=ALU.mult,
+                    )
+                    gf_sum = setup.tile([P, HEADS], F32, tag="gf_sum", bufs=2)
+                    nc.vector.tensor_reduce(out=gf_sum[:], in_=gf[:, :, 0:n_j], op=ALU.add, axis=AXIS_X)
+                    nc.vector.scalar_tensor_tensor(
+                        out=z_fixed[:], in0=gf_sum[:], scalar=abs(D4[tau]), in1=z_fixed[:], op0=ALU.mult, op1=ALU.add
+                    )
+
+            q0, q1, k0 = [accs.tile([P, BANK], F32, tag="acc", name="acc_%s" % n) for n in ("q0", "q1", "k0")]
+            table_quarter(0)
+            table_quarter(1)
+            transpose_gains()
+            mx_passes(0, 2, [q0, q1, k0])
+            small_tables()
+            table_quarter(2)
+            mx_passes(2, 3, [q0, q1, k0])
+            table_quarter(3)
+            mx_passes(3, 4, [q0, q1, k0])
+            spread_b_qkv()
+            mx_passes(4, 8, [q0, q1, k0])
+
+        with tc.tile_pool(name="dense", bufs=2) as dense:
+
+            def scores(half_i, q_bank, k_bank):
+                width = 4 * HEAD_DIM
+                toks, trs, k_ts, q_ts, sts = [], [], [], [], []
+                for i in range(2):
+                    b = 2 * half_i + i
+                    tok = dense.tile([P, 2, width], F32, tag="tok")
+                    for qk, bank in enumerate((q_bank, k_bank)):
+                        nc.vector.tensor_tensor(
+                            out=tok[:, qk, :],
+                            in0=bank[:, width * i : width * (i + 1)],
+                            in1=bias_all[:, EMB * qk + width * b : EMB * qk + width * (b + 1)],
+                            op=ALU.add,
+                        )
+                    toks.append(tok)
+                for i in range(2):
+                    tr = work.tile([P, 4, TOKENS], F32, tag="work")
+                    tok_flat = toks[i][:].rearrange("p qk c -> p (qk c)")
+                    for t in range(4):
+                        nc.tensor.transpose(tr[:, t, :], tok_flat[:, P * t : P * (t + 1)], ident_f[:])
+                    trs.append(tr)
+                for i in range(2):
+                    k_t = dense.tile([P, 2, TOKENS], F32, tag="k_t")
+                    nc.scalar.copy(out=k_t[:], in_=trs[i][:, 2:4, :])
+                    q_t = dense.tile([P, 2, 2, TOKENS], F32, tag="q_t")
+                    for hd in range(2):
+                        nc.scalar.activation(
+                            out=q_t[:, :, hd, :], in_=trs[i][:, 0:2, :], func=ACT.Copy, scale=half_mask[:, hd : hd + 1]
+                        )
+                    k_ts.append(k_t)
+                    q_ts.append(q_t)
+                for i in range(2):
+                    st = work.tile([P, 4, TOKENS], F32, tag="work")
+                    for pair in range(2):
+                        nc.tensor.matmul(
+                            out=st[:, 2 * pair : 2 * pair + 2, :],
+                            lhsT=k_ts[i][:, pair, :],
+                            rhs=q_ts[i][:, pair, :, :],
+                            start=True,
+                            stop=True,
+                        )
+                    sts.append(st)
+                for i in range(2):
+                    b = 2 * half_i + i
+                    prod = dense.tile([P, 4, HEAD_DIM], F32, tag="prod")
+                    nc.gpsimd.tensor_tensor(
+                        out=prod[:].rearrange("p h d -> p (h d)"), in0=toks[i][:, 0, :], in1=toks[i][:, 1, :], op=ALU.mult
+                    )
+                    nc.vector.tensor_reduce(out=qk_same[:, 4 * b : 4 * b + 4], in_=prod[:], op=ALU.add, axis=AXIS_X)
+                return sts
+
+            def attend(b, st, z_ps):
+                heads = slice(4 * b, 4 * b + 4)
+                us, fs = [], []
+                for layer in range(2):
+                    u = dense.tile([P, 4 * TOKENS], F32, tag="u", bufs=3)
+                    nc.vector.tensor_tensor(
+                        out=u[:],
+                        in0=st[:].rearrange("p h n -> p (h n)"),
+                        in1=bias_tab[layer][:, heads, :].rearrange("p h n -> p (h n)"),
+                        op=ALU.add,
+                    )
+                    f = dense.tile([P, 4 * TOKENS], F32, tag="f", bufs=3)
+                    nc.scalar.activation(out=f[:], in_=u[:], func=ACT.Exp, bias=minus_one[:])
+                    us.append(u)
+                    fs.append(f)
+                for layer in range(2):
+                    f = fs[layer]
+                    nc.vector.scalar_tensor_tensor(
+                        out=f[:], in0=us[layer][:], scalar=1.0, in1=f[:], op0=ALU.max, op1=ALU.min
+                    )
+                    nc.vector.tensor_tensor(
+                        out=f[:], in0=f[:], in1=gain_tab[layer][:, heads, :].rearrange("p h n -> p (h n)"), op=ALU.mult
+                    )
+                nc.vector.tensor_tensor(
+                    out=at_all[:, heads, :].rearrange("p h n -> p (h n)"), in0=fs[0][:], in1=fs[1][:], op=ALU.add
+                )
+                at_abs = dense.tile([P, 4, TOKENS], F32, tag="at_abs")
+                nc.gpsimd.tensor_tensor(
+                    out=at_abs[:],
+                    in0=at_all[:, heads, :],
+                    in1=sign_tab[:].unsqueeze(1).to_broadcast([P, 4, TOKENS]),
+                    op=ALU.mult,
+                )
+                for i in range(4):
+                    nc.tensor.matmul(
+                        out=z_ps[:, 4 * (b % 2) + i, :], lhsT=at_abs[:, i, :], rhs=ones_f[:], start=True, stop=True
+                    )
+
+            def same_token_terms(half_i):
+                heads = slice(8 * half_i, 8 * half_i + 8)
+                n_t = SCALES + 1
+                u = dense.tile([P, 8, n_t], F32, tag="u_diag")
+                nc.vector.tensor_tensor(
+                    out=u[:], in0=qk_same[:, heads].unsqueeze(2).to_broadcast([P, 8, n_t]), in1=diag_bias[:, heads, :], op=ALU.add
+                )
+                f = dense.tile([P, 8, n_t], F32, tag="f_diag")
+                elu_plus_one(f[:], u[:], u[:])
+                nc.vector.tensor_tensor(out=f[:], in0=f[:], in1=diag_gain[:, heads, :], op=ALU.mult)
+                nc.vector.tensor_reduce(out=w_diag[:, heads], in_=f[:], op=ALU.add, axis=AXIS_X)
+                nc.vector.tensor_tensor(out=z_all[:, heads], in0=w_diag[:, heads], in1=z_fixed[:, heads], op=ALU.add)
+
+            def normalise(half_i, z_ps):
+                heads = slice(8 * half_i, 8 * half_i + 8)
+                nc.vector.tensor_tensor(out=z_all[:, heads], in0=z_ps[:, :, 0], in1=z_all[:, heads], op=ALU.add)
+                nc.vector.reciprocal(out=z_inv[:, heads], in_=z_all[:, heads])
+                nc.vector.tensor_tensor(out=w_diag_n[:, heads], in0=w_diag[:, heads], in1=z_inv[:, heads], op=ALU.mult)
+
+            st0, st1 = scores(0, q0, k0)
+            same_token_terms(0)
+            k1 = accs.tile([P, BANK], F32, tag="acc")
+            mx_passes(8, first_v_load, [k1])
+            z_ps0 = work.tile([P, 8, 2], F32, tag="work")
+            attend(0, st0, z_ps0)
+            attend(1, st1, z_ps0)
+            st2, st3 = scores(1, q1, k1)
+            same_token_terms(1)
+            normalise(0, z_ps0)
+            v_banks = [accs.tile([P, BANK], F32, tag="acc", name="acc_v%d" % i) for i in range(2)]
+            mx_passes(first_v_load, first_v_load + 4, v_banks)
+            z_ps1 = work.tile([P, 8, 2], F32, tag="work")
+            attend(2, st2, z_ps1)
+            mx_passes(first_v_load + 4, len(w_loads) - 1, v_banks)
+            attend(3, st3, z_ps1)
+            mx_passes(len(w_loads) - 1, len(w_loads), v_banks)
+            normalise(1, z_ps1)
+
+            v_sb = dense.tile([P, HEADS, HEAD_DIM], F32, bufs=1)
+            v_diag = dense.tile([P, HEADS, HEAD_DIM], F32, bufs=1)
+            o_sb = dense.tile([P, HEADS, HEAD_DIM], F32, bufs=1)
+            out_rows = out.rearrange("o n e -> (o n) e")
+            for i, bank in enumerate(v_banks):
+                heads = slice(8 * i, 8 * i + 8)
+                nc.vector.tensor_tensor(
+                    out=v_sb[:, heads, :].rearrange("p h d -> p (h d)"),
+                    in0=bank[:],
+                    in1=bias_all[:, 2 * EMB + BANK * i : 2 * EMB + BANK * (i + 1)],
+                    op=ALU.add,
+                )
+                nc.gpsimd.tensor_tensor(
+                    out=v_diag[:, heads, :],
+                    in0=v_sb[:, heads, :],
+                    in1=w_diag_n[:, heads].unsqueeze(2).to_broadcast([P, 8, HEAD_DIM]),
+                    op=ALU.mult,
+                )
+            for b in range(4):
+                o_ps = work.tile([P, 4, HEAD_DIM], F32, tag="work")
+                for i in range(4):
+                    h = 4 * b + i
+                    nc.tensor.matmul(out=o_ps[:, i, :], lhsT=at_all[:, h, :], rhs=v_sb[:, h, :], start=True, stop=True)
+                for i in range(4):
+                    h = 4 * b + i
+                    nc.vector.scalar_tensor_tensor(
+                        out=o_sb[:, h, :],
+                        in0=o_ps[:, i, :],
+                        scalar=z_inv[:, h : h + 1],
+                        in1=v_diag[:, h, :],
+                        op0=ALU.mult,
+                        op1=ALU.add,
+                    )
+                if b % 2 == 1:
+                    cols = slice(BANK * (b // 2), BANK * (b // 2 + 1))
+                    nc.sync.dma_start(out=out_rows[:, cols], in_=o_sb[:].rearrange("p h d -> p (h d)")[:, cols])

@@ -68,19 +68,19 @@ def tile_dwarfattention_pa_k_kernel(
         x_codes = keep.tile([P, PASSES * TOKENS], U32, align_bytes=64)
         x_scales = keep.tile([P, PASSES * TOKENS], U8, align_bytes=64)
         w_planes = keep.tile([P, PASSES // PLANES, 3 * EMB], U8, align_bytes=64)
-        bias_all = keep.tile([P, 3 * EMB], BF16)
-        bias_tab = [keep.tile([P, HEADS, TOKENS], F32, name="bias_tab%d" % i) for i in range(2)]
-        gain_tab = [keep.tile([P, HEADS, TOKENS], F32, name="gain_tab%d" % i) for i in range(2)]
+        bias_v = keep.tile([P, EMB], BF16)
+        bias_cols = keep.tile([P, 2 * EMB // P], F32)
+        bias_q_half = keep.tile([P, EMB // P, 2], F32)
+        bias_tab = keep.tile([P, 2, HEADS, TOKENS], F32)
+        gain_tab = keep.tile([P, 2, HEADS, TOKENS], F32)
         sign_tab = keep.tile([P, TOKENS], F32)
         diag_bias = keep.tile([P, HEADS, SCALES + 1], F32)
         diag_gain = keep.tile([P, HEADS, SCALES + 1], F32)
         z_fixed = keep.tile([P, HEADS], F32)
         at_all = keep.tile([P, HEADS, TOKENS], F32)
-        qk_same = keep.tile([P, HEADS], F32)
         w_diag = keep.tile([P, HEADS], F32)
         z_all = keep.tile([P, HEADS], F32)
         z_inv = keep.tile([P, HEADS], F32)
-        w_diag_n = keep.tile([P, HEADS], F32)
 
         w_words = W_qkv_words.rearrange("g p n t -> p g (n t)").bitcast(I32)
         w_loads = [(g0, 2, 0, 3 * BANK) for g0 in range(0, PASSES, 2)]
@@ -159,9 +159,12 @@ def tile_dwarfattention_pa_k_kernel(
             gains_h = setup.tile([P, TOKENS * SCALES], BF16)
             nc.gpsimd.memset(gains_h[:], 0.0)
             nc.gpsimd.dma_start(out=gains_h[0:HEADS, :], in_=gains.rearrange("o h n j -> (o h) (n j)"))
-            bias_row = setup.tile([P, 3 * EMB], BF16)
+            bias_row = setup.tile([P, EMB], BF16)
             nc.gpsimd.memset(bias_row[:], 0.0)
-            nc.gpsimd.dma_start(out=bias_row[0:1, :], in_=b_qkv.rearrange("(o n) -> o n", o=1))
+            nc.gpsimd.dma_start(out=bias_row[0:1, :], in_=b_qkv[2 * EMB :].rearrange("(o n) -> o n", o=1))
+            bias_rows = setup.tile([P, P], BF16)
+            nc.gpsimd.memset(bias_rows[:], 0.0)
+            nc.gpsimd.dma_start(out=bias_rows[0 : 2 * EMB // P, :], in_=b_qkv[0 : 2 * EMB].rearrange("(r c) -> r c", c=P))
 
             token_of_row = setup.tile([P, GROUP], F32)
             nc.vector.tensor_reduce(
@@ -300,23 +303,32 @@ def tile_dwarfattention_pa_k_kernel(
                             stop=True,
                         )
                     nc.scalar.activation(
-                        out=bias_tab[layer][:, :, cols].rearrange("p h (g a) -> p h g a", a=GROUP),
+                        out=bias_tab[:, layer, :, cols].rearrange("p h (g a) -> p h g a", a=GROUP),
                         in_=bias_ps[:].rearrange("p g h a -> p h g a"),
                         func=ACT.Identity,
                         bias=ones_f[:, 0:1],
                     )
                     nc.vector.tensor_copy(
-                        out=gain_tab[layer][:, :, cols].rearrange("p h (g a) -> p h g a", a=GROUP),
+                        out=gain_tab[:, layer, :, cols].rearrange("p h (g a) -> p h g a", a=GROUP),
                         in_=gain_ps[:].rearrange("p g h a -> p h g a"),
                     )
 
             def spread_b_qkv():
-                for i in range(3 * EMB // BANK):
+                for i in range(EMB // BANK):
                     ps = work.tile([P, BANK], F32, tag="work")
                     nc.tensor.matmul(
                         out=ps[:], lhsT=ones_b[:], rhs=bias_row[:, BANK * i : BANK * (i + 1)], start=True, stop=True
                     )
-                    nc.scalar.copy(out=bias_all[:, BANK * i : BANK * (i + 1)], in_=ps[:])
+                    nc.scalar.copy(out=bias_v[:, BANK * i : BANK * (i + 1)], in_=ps[:])
+                ps = work.tile([P, P], BF16, tag="work")
+                nc.tensor.transpose(ps[:], bias_rows[:], ident_b[:])
+                nc.vector.tensor_copy(out=bias_cols[:], in_=ps[:, 0 : 2 * EMB // P])
+                nc.vector.tensor_tensor(
+                    out=bias_q_half[:],
+                    in0=bias_cols[:, 0 : EMB // P].unsqueeze(2).to_broadcast([P, EMB // P, 2]),
+                    in1=half_mask[:].unsqueeze(1).to_broadcast([P, EMB // P, 2]),
+                    op=ALU.mult,
+                )
 
             gains_nt = setup.tile([P, HEADS, SCALES], F32)
 
@@ -393,132 +405,190 @@ def tile_dwarfattention_pa_k_kernel(
             mx_passes(4, 8, [q0, q1, k0])
 
         with tc.tile_pool(name="dense", bufs=2) as dense:
+            width = 4 * HEAD_DIM
+            toks, trs, k_ts, q_ts, sts, us, fs, prods = {}, {}, {}, {}, {}, {}, {}, {}
 
-            def scores(half_i, q_bank, k_bank):
-                width = 4 * HEAD_DIM
-                toks, trs, k_ts, q_ts, sts = [], [], [], [], []
-                for i in range(2):
-                    b = 2 * half_i + i
-                    tok = dense.tile([P, 2, width], F32, tag="tok")
-                    for qk, bank in enumerate((q_bank, k_bank)):
-                        nc.vector.tensor_tensor(
-                            out=tok[:, qk, :],
-                            in0=bank[:, width * i : width * (i + 1)],
-                            in1=bias_all[:, EMB * qk + width * b : EMB * qk + width * (b + 1)],
-                            op=ALU.add,
-                        )
-                    toks.append(tok)
-                for i in range(2):
-                    tr = work.tile([P, 4, TOKENS], F32, tag="work")
-                    tok_flat = toks[i][:].rearrange("p qk c -> p (qk c)")
-                    for t in range(4):
-                        nc.tensor.transpose(tr[:, t, :], tok_flat[:, P * t : P * (t + 1)], ident_f[:])
-                    trs.append(tr)
-                for i in range(2):
-                    k_t = dense.tile([P, 2, TOKENS], F32, tag="k_t")
-                    nc.scalar.copy(out=k_t[:], in_=trs[i][:, 2:4, :])
-                    q_t = dense.tile([P, 2, 2, TOKENS], F32, tag="q_t")
+            def to_sbuf(b, q_bank, k_bank):
+                tok = dense.tile([P, 2, width], F32, tag="tok")
+                for qk, bank in enumerate((q_bank, k_bank)):
+                    nc.scalar.copy(out=tok[:, qk, :], in_=bank[:, width * (b % 2) : width * (b % 2 + 1)])
+                toks[b] = tok
+
+            def transposes(b):
+                tr = work.tile([P, 4, TOKENS], F32, tag="work")
+                tok_flat = toks[b][:].rearrange("p qk c -> p (qk c)")
+                for t in range(4):
+                    nc.tensor.transpose(tr[:, t, :], tok_flat[:, P * t : P * (t + 1)], ident_f[:])
+                trs[b] = tr
+
+            def add_bias(b):
+                k_t = dense.tile([P, 2, TOKENS], F32, tag="k_t")
+                q_t = dense.tile([P, 2, 2, TOKENS], F32, tag="q_t")
+                for pair in range(2):
+                    t = 2 * b + pair
+                    nc.scalar.activation(
+                        out=k_t[:, pair, :],
+                        in_=trs[b][:, 2 + pair, :],
+                        func=ACT.Identity,
+                        bias=bias_cols[:, EMB // P + t : EMB // P + t + 1],
+                    )
                     for hd in range(2):
                         nc.scalar.activation(
-                            out=q_t[:, :, hd, :], in_=trs[i][:, 0:2, :], func=ACT.Copy, scale=half_mask[:, hd : hd + 1]
+                            out=q_t[:, pair, hd, :],
+                            in_=trs[b][:, pair, :],
+                            func=ACT.Identity,
+                            scale=half_mask[:, hd : hd + 1],
+                            bias=bias_q_half[:, t, hd : hd + 1],
                         )
-                    k_ts.append(k_t)
-                    q_ts.append(q_t)
-                for i in range(2):
-                    st = work.tile([P, 4, TOKENS], F32, tag="work")
-                    for pair in range(2):
-                        nc.tensor.matmul(
-                            out=st[:, 2 * pair : 2 * pair + 2, :],
-                            lhsT=k_ts[i][:, pair, :],
-                            rhs=q_ts[i][:, pair, :, :],
-                            start=True,
-                            stop=True,
-                        )
-                    sts.append(st)
-                for i in range(2):
-                    b = 2 * half_i + i
-                    prod = dense.tile([P, 4, HEAD_DIM], F32, tag="prod")
-                    nc.gpsimd.tensor_tensor(
-                        out=prod[:].rearrange("p h d -> p (h d)"), in0=toks[i][:, 0, :], in1=toks[i][:, 1, :], op=ALU.mult
-                    )
-                    nc.vector.tensor_reduce(out=qk_same[:, 4 * b : 4 * b + 4], in_=prod[:], op=ALU.add, axis=AXIS_X)
-                return sts
+                k_ts[b] = k_t
+                q_ts[b] = q_t
 
-            def attend(b, st, z_ps):
-                heads = slice(4 * b, 4 * b + 4)
-                us, fs = [], []
-                for layer in range(2):
-                    u = dense.tile([P, 4 * TOKENS], F32, tag="u", bufs=3)
-                    nc.vector.tensor_tensor(
-                        out=u[:],
-                        in0=st[:].rearrange("p h n -> p (h n)"),
-                        in1=bias_tab[layer][:, heads, :].rearrange("p h n -> p (h n)"),
-                        op=ALU.add,
+            def scores(b):
+                st = work.tile([P, 4 * TOKENS], F32, tag="work")
+                for pair in range(2):
+                    nc.tensor.matmul(
+                        out=st[:, 2 * TOKENS * pair : 2 * TOKENS * (pair + 1)],
+                        lhsT=k_ts[b][:, pair, :],
+                        rhs=q_ts[b][:, pair, :, :],
+                        start=True,
+                        stop=True,
                     )
-                    f = dense.tile([P, 4 * TOKENS], F32, tag="f", bufs=3)
-                    nc.scalar.activation(out=f[:], in_=u[:], func=ACT.Exp, bias=minus_one[:])
-                    us.append(u)
-                    fs.append(f)
-                for layer in range(2):
-                    f = fs[layer]
-                    nc.vector.scalar_tensor_tensor(
-                        out=f[:], in0=us[layer][:], scalar=1.0, in1=f[:], op0=ALU.max, op1=ALU.min
+                sts[b] = st
+
+            def same_token_products(b):
+                prod = dense.tile([P, 2, 2, TOKENS], F32, tag="prod")
+                nc.gpsimd.tensor_tensor(
+                    out=prod[:],
+                    in0=q_ts[b][:],
+                    in1=k_ts[b][:].unsqueeze(2).to_broadcast([P, 2, 2, TOKENS]),
+                    op=ALU.mult,
+                )
+                prods[b] = prod
+
+            def same_token_dots(b, sums_ps):
+                for i in range(4):
+                    nc.tensor.matmul(
+                        out=sums_ps[:, 0, 4 * (b % 2) + i, :],
+                        lhsT=prods[b][:, i // 2, i % 2, :],
+                        rhs=ones_f[:],
+                        start=True,
+                        stop=True,
                     )
-                    nc.vector.tensor_tensor(
-                        out=f[:], in0=f[:], in1=gain_tab[layer][:, heads, :].rearrange("p h n -> p (h n)"), op=ALU.mult
-                    )
+
+            def exponentials(b):
+                u = dense.tile([P, 2, 4 * TOKENS], F32, tag="u", bufs=3)
                 nc.vector.tensor_tensor(
-                    out=at_all[:, heads, :].rearrange("p h n -> p (h n)"), in0=fs[0][:], in1=fs[1][:], op=ALU.add
+                    out=u[:],
+                    in0=sts[b][:].unsqueeze(1).to_broadcast([P, 2, 4 * TOKENS]),
+                    in1=bias_tab[:, :, 4 * b : 4 * b + 4, :].rearrange("p l h n -> p l (h n)"),
+                    op=ALU.add,
+                )
+                f = dense.tile([P, 2, 4 * TOKENS], F32, tag="f", bufs=3)
+                nc.scalar.activation(out=f[:], in_=u[:], func=ACT.Exp, bias=minus_one[:])
+                us[b] = u
+                fs[b] = f
+
+            def weigh(b, sign_engine):
+                heads = slice(4 * b, 4 * b + 4)
+                f = fs[b]
+                f_flat = f[:].rearrange("p l c -> p (l c)")
+                nc.vector.scalar_tensor_tensor(
+                    out=f_flat, in0=us[b][:].rearrange("p l c -> p (l c)"), scalar=1.0, in1=f_flat, op0=ALU.max, op1=ALU.min
+                )
+                nc.vector.tensor_tensor(
+                    out=f[:], in0=f[:], in1=gain_tab[:, :, heads, :].rearrange("p l h n -> p l (h n)"), op=ALU.mult
+                )
+                nc.vector.tensor_tensor(
+                    out=at_all[:, heads, :].rearrange("p h n -> p (h n)"), in0=f[:, 0, :], in1=f[:, 1, :], op=ALU.add
                 )
                 at_abs = dense.tile([P, 4, TOKENS], F32, tag="at_abs")
-                nc.gpsimd.tensor_tensor(
+                sign_engine.tensor_tensor(
                     out=at_abs[:],
                     in0=at_all[:, heads, :],
                     in1=sign_tab[:].unsqueeze(1).to_broadcast([P, 4, TOKENS]),
                     op=ALU.mult,
                 )
+                return at_abs
+
+            def column_sums(b, at_abs, sums_ps):
                 for i in range(4):
                     nc.tensor.matmul(
-                        out=z_ps[:, 4 * (b % 2) + i, :], lhsT=at_abs[:, i, :], rhs=ones_f[:], start=True, stop=True
+                        out=sums_ps[:, 1, 4 * (b % 2) + i, :], lhsT=at_abs[:, i, :], rhs=ones_f[:], start=True, stop=True
                     )
 
-            def same_token_terms(half_i):
+            def same_token_terms(half_i, sums_ps):
                 heads = slice(8 * half_i, 8 * half_i + 8)
                 n_t = SCALES + 1
                 u = dense.tile([P, 8, n_t], F32, tag="u_diag")
                 nc.vector.tensor_tensor(
-                    out=u[:], in0=qk_same[:, heads].unsqueeze(2).to_broadcast([P, 8, n_t]), in1=diag_bias[:, heads, :], op=ALU.add
+                    out=u[:], in0=sums_ps[:, 0, :, 0:1].to_broadcast([P, 8, n_t]), in1=diag_bias[:, heads, :], op=ALU.add
                 )
                 f = dense.tile([P, 8, n_t], F32, tag="f_diag")
-                elu_plus_one(f[:], u[:], u[:])
+                nc.scalar.activation(out=f[:], in_=u[:], func=ACT.Exp)
+                return u, f
+
+            def same_token_sum(half_i, u, f):
+                heads = slice(8 * half_i, 8 * half_i + 8)
+                nc.vector.tensor_scalar(out=u[:], in0=u[:], scalar1=0.0, scalar2=1.0, op0=ALU.max, op1=ALU.add)
+                nc.vector.tensor_tensor(out=f[:], in0=f[:], in1=u[:], op=ALU.min)
                 nc.vector.tensor_tensor(out=f[:], in0=f[:], in1=diag_gain[:, heads, :], op=ALU.mult)
                 nc.vector.tensor_reduce(out=w_diag[:, heads], in_=f[:], op=ALU.add, axis=AXIS_X)
                 nc.vector.tensor_tensor(out=z_all[:, heads], in0=w_diag[:, heads], in1=z_fixed[:, heads], op=ALU.add)
 
-            def normalise(half_i, z_ps):
+            def normalise(half_i, sums_ps):
                 heads = slice(8 * half_i, 8 * half_i + 8)
-                nc.vector.tensor_tensor(out=z_all[:, heads], in0=z_ps[:, :, 0], in1=z_all[:, heads], op=ALU.add)
+                nc.vector.tensor_tensor(out=z_all[:, heads], in0=sums_ps[:, 1, :, 0], in1=z_all[:, heads], op=ALU.add)
                 nc.vector.reciprocal(out=z_inv[:, heads], in_=z_all[:, heads])
-                nc.vector.tensor_tensor(out=w_diag_n[:, heads], in0=w_diag[:, heads], in1=z_inv[:, heads], op=ALU.mult)
 
-            st0, st1 = scores(0, q0, k0)
-            same_token_terms(0)
+            def score_half(half_i, q_bank, k_bank):
+                banks = (2 * half_i, 2 * half_i + 1)
+                for b in banks:
+                    to_sbuf(b, q_bank, k_bank)
+                for b in banks:
+                    transposes(b)
+                for b in banks:
+                    add_bias(b)
+
             k1 = accs.tile([P, BANK], F32, tag="acc")
-            mx_passes(8, first_v_load, [k1])
-            z_ps0 = work.tile([P, 8, 2], F32, tag="work")
-            attend(0, st0, z_ps0)
-            attend(1, st1, z_ps0)
-            st2, st3 = scores(1, q1, k1)
-            same_token_terms(1)
-            normalise(0, z_ps0)
             v_banks = [accs.tile([P, BANK], F32, tag="acc", name="acc_v%d" % i) for i in range(2)]
+
+            score_half(0, q0, k0)
+            mx_passes(8, 10, [k1])
+            scores(0)
+            scores(1)
+            mx_passes(10, first_v_load, [k1])
+            same_token_products(0)
+            same_token_products(1)
+            exponentials(0)
+            exponentials(1)
+            score_half(1, q1, k1)
+            sums_ps0 = work.tile([P, 2, 8, 2], F32, tag="work")
+            same_token_dots(0, sums_ps0)
+            same_token_dots(1, sums_ps0)
+            at_abs0 = weigh(0, nc.gpsimd)
+            scores(2)
+            scores(3)
             mx_passes(first_v_load, first_v_load + 4, v_banks)
-            z_ps1 = work.tile([P, 8, 2], F32, tag="work")
-            attend(2, st2, z_ps1)
-            mx_passes(first_v_load + 4, len(w_loads) - 1, v_banks)
-            attend(3, st3, z_ps1)
-            mx_passes(len(w_loads) - 1, len(w_loads), v_banks)
-            normalise(1, z_ps1)
+            same_token_products(2)
+            same_token_products(3)
+            at_abs1 = weigh(1, nc.gpsimd)
+            u_diag0, f_diag0 = same_token_terms(0, sums_ps0)
+            exponentials(2)
+            exponentials(3)
+            sums_ps1 = work.tile([P, 2, 8, 2], F32, tag="work")
+            same_token_dots(2, sums_ps1)
+            same_token_dots(3, sums_ps1)
+            column_sums(0, at_abs0, sums_ps0)
+            column_sums(1, at_abs1, sums_ps0)
+            same_token_sum(0, u_diag0, f_diag0)
+            at_abs2 = weigh(2, nc.gpsimd)
+            u_diag1, f_diag1 = same_token_terms(1, sums_ps1)
+            at_abs3 = weigh(3, nc.vector)
+            same_token_sum(1, u_diag1, f_diag1)
+            normalise(0, sums_ps0)
+            mx_passes(first_v_load + 4, len(w_loads), v_banks)
+            column_sums(2, at_abs2, sums_ps1)
+            column_sums(3, at_abs3, sums_ps1)
 
             v_sb = dense.tile([P, HEADS, HEAD_DIM], F32, bufs=1)
             v_diag = dense.tile([P, HEADS, HEAD_DIM], F32, bufs=1)
@@ -529,30 +599,34 @@ def tile_dwarfattention_pa_k_kernel(
                 nc.vector.tensor_tensor(
                     out=v_sb[:, heads, :].rearrange("p h d -> p (h d)"),
                     in0=bank[:],
-                    in1=bias_all[:, 2 * EMB + BANK * i : 2 * EMB + BANK * (i + 1)],
+                    in1=bias_v[:, BANK * i : BANK * (i + 1)],
                     op=ALU.add,
                 )
-                nc.gpsimd.tensor_tensor(
+            for i in range(2):
+                heads = slice(8 * i, 8 * i + 8)
+                nc.vector.tensor_tensor(
                     out=v_diag[:, heads, :],
                     in0=v_sb[:, heads, :],
-                    in1=w_diag_n[:, heads].unsqueeze(2).to_broadcast([P, 8, HEAD_DIM]),
+                    in1=w_diag[:, heads].unsqueeze(2).to_broadcast([P, 8, HEAD_DIM]),
                     op=ALU.mult,
                 )
+            o_pss = []
             for b in range(4):
                 o_ps = work.tile([P, 4, HEAD_DIM], F32, tag="work")
                 for i in range(4):
                     h = 4 * b + i
                     nc.tensor.matmul(out=o_ps[:, i, :], lhsT=at_all[:, h, :], rhs=v_sb[:, h, :], start=True, stop=True)
-                for i in range(4):
-                    h = 4 * b + i
-                    nc.vector.scalar_tensor_tensor(
-                        out=o_sb[:, h, :],
-                        in0=o_ps[:, i, :],
-                        scalar=z_inv[:, h : h + 1],
-                        in1=v_diag[:, h, :],
-                        op0=ALU.mult,
-                        op1=ALU.add,
-                    )
+                o_pss.append(o_ps)
+            normalise(1, sums_ps1)
+            for b in range(4):
+                heads = slice(4 * b, 4 * b + 4)
+                nc.vector.tensor_tensor(out=o_sb[:, heads, :], in0=o_pss[b][:], in1=v_diag[:, heads, :], op=ALU.add)
+                nc.vector.tensor_tensor(
+                    out=o_sb[:, heads, :],
+                    in0=o_sb[:, heads, :],
+                    in1=z_inv[:, heads].unsqueeze(2).to_broadcast([P, 4, HEAD_DIM]),
+                    op=ALU.mult,
+                )
                 if b % 2 == 1:
                     cols = slice(BANK * (b // 2), BANK * (b // 2 + 1))
                     nc.sync.dma_start(out=out_rows[:, cols], in_=o_sb[:].rearrange("p h d -> p (h d)")[:, cols])

@@ -73,7 +73,8 @@ def tile_dwarfattention_pa_k_kernel(
         bias_q_half = keep.tile([P, EMB // P, 2], F32)
         bias_tab = keep.tile([P, 2, HEADS, TOKENS], F32)
         gain_tab = keep.tile([P, 2, HEADS, TOKENS], F32)
-        sign_tab = keep.tile([P, TOKENS], F32)
+        class3 = keep.tile([P, 4], F32)
+        sign3 = keep.tile([P, 4], F32)
         diag_bias = keep.tile([P, HEADS, SCALES + 1], F32)
         diag_gain = keep.tile([P, HEADS, SCALES + 1], F32)
         z_fixed = keep.tile([P, HEADS], F32)
@@ -343,16 +344,10 @@ def tile_dwarfattention_pa_k_kernel(
                     )
 
             def small_tables():
-                nc.vector.memset(sign_tab[:], 1.0)
-                for j, tau, o in taps_of((3,)):
-                    nc.vector.scalar_tensor_tensor(
-                        out=sign_tab[:, o:],
-                        in0=ident_f[:, 0 : TOKENS - o],
-                        scalar=-2.0,
-                        in1=sign_tab[:, o:],
-                        op0=ALU.mult,
-                        op1=ALU.add,
-                    )
+                nc.vector.memset(class3[:], 0.0)
+                for c in range(3):
+                    nc.vector.tensor_reduce(out=class3[:, c : c + 1], in_=ident_f[:, c:TOKENS:3], op=ALU.add, axis=AXIS_X)
+                nc.vector.tensor_scalar(out=sign3[:], in0=class3[:], scalar1=-2.0, scalar2=1.0, op0=ALU.mult, op1=ALU.add)
                 soft = setup.tile([P, HEADS], F32)
                 nc.scalar.activation(out=soft[:], in_=bypass_all, func=ACT.Abs)
                 nc.scalar.activation(out=soft[:], in_=soft[:], func=ACT.Exp, scale=-1.0)
@@ -406,7 +401,7 @@ def tile_dwarfattention_pa_k_kernel(
 
         with tc.tile_pool(name="dense", bufs=2) as dense:
             width = 4 * HEAD_DIM
-            toks, trs, k_ts, q_ts, sts, us, fs, prods = {}, {}, {}, {}, {}, {}, {}, {}
+            toks, trs, k_ts, q_ts, q_ps, sts, us, fs, prods = {}, {}, {}, {}, {}, {}, {}, {}, {}
 
             def to_sbuf(b, q_bank, k_bank):
                 tok = dense.tile([P, 2, width], F32, tag="tok")
@@ -455,24 +450,25 @@ def tile_dwarfattention_pa_k_kernel(
                     )
                 sts[b] = st
 
+            def plain_q(b):
+                q_p = dense.tile([P, 2, TOKENS], F32, tag="q_p")
+                for pair in range(2):
+                    t = 2 * b + pair
+                    nc.scalar.activation(
+                        out=q_p[:, pair, :], in_=trs[b][:, pair, :], func=ACT.Identity, bias=bias_cols[:, t : t + 1]
+                    )
+                q_ps[b] = q_p
+
             def same_token_products(b):
-                prod = dense.tile([P, 2, 2, TOKENS], F32, tag="prod")
-                nc.gpsimd.tensor_tensor(
-                    out=prod[:],
-                    in0=q_ts[b][:],
-                    in1=k_ts[b][:].unsqueeze(2).to_broadcast([P, 2, 2, TOKENS]),
-                    op=ALU.mult,
-                )
+                prod = dense.tile([P, 2, TOKENS], F32, tag="prod")
+                nc.vector.tensor_tensor(out=prod[:], in0=q_ps[b][:], in1=k_ts[b][:], op=ALU.mult)
                 prods[b] = prod
 
             def same_token_dots(b, sums_ps):
-                for i in range(4):
+                for pair in range(2):
+                    h = 4 * (b % 2) + 2 * pair
                     nc.tensor.matmul(
-                        out=sums_ps[:, 0, 4 * (b % 2) + i, :],
-                        lhsT=prods[b][:, i // 2, i % 2, :],
-                        rhs=ones_f[:],
-                        start=True,
-                        stop=True,
+                        out=sums_ps[:, h : h + 2], lhsT=prods[b][:, pair, :], rhs=half_mask[:], start=True, stop=True
                     )
 
             def exponentials(b):
@@ -488,32 +484,32 @@ def tile_dwarfattention_pa_k_kernel(
                 us[b] = u
                 fs[b] = f
 
-            def weigh(b, sign_engine):
-                heads = slice(4 * b, 4 * b + 4)
-                f = fs[b]
-                f_flat = f[:].rearrange("p l c -> p (l c)")
-                nc.vector.scalar_tensor_tensor(
-                    out=f_flat, in0=us[b][:].rearrange("p l c -> p (l c)"), scalar=1.0, in1=f_flat, op0=ALU.max, op1=ALU.min
-                )
-                nc.vector.tensor_tensor(
-                    out=f[:], in0=f[:], in1=gain_tab[:, :, heads, :].rearrange("p l h n -> p l (h n)"), op=ALU.mult
-                )
-                nc.vector.tensor_tensor(
-                    out=at_all[:, heads, :].rearrange("p h n -> p (h n)"), in0=f[:, 0, :], in1=f[:, 1, :], op=ALU.add
-                )
-                at_abs = dense.tile([P, 4, TOKENS], F32, tag="at_abs")
-                sign_engine.tensor_tensor(
-                    out=at_abs[:],
-                    in0=at_all[:, heads, :],
-                    in1=sign_tab[:].unsqueeze(1).to_broadcast([P, 4, TOKENS]),
-                    op=ALU.mult,
-                )
-                return at_abs
+            def weigh(half_i):
+                banks = (2 * half_i, 2 * half_i + 1)
+                for b in banks:
+                    f_flat = fs[b][:].rearrange("p l c -> p (l c)")
+                    nc.vector.scalar_tensor_tensor(
+                        out=f_flat, in0=us[b][:].rearrange("p l c -> p (l c)"), scalar=1.0, in1=f_flat, op0=ALU.max, op1=ALU.min
+                    )
+                for b in banks:
+                    nc.vector.tensor_tensor(
+                        out=fs[b][:],
+                        in0=fs[b][:],
+                        in1=gain_tab[:, :, 4 * b : 4 * b + 4, :].rearrange("p l h n -> p l (h n)"),
+                        op=ALU.mult,
+                    )
+                for b in banks:
+                    nc.vector.tensor_tensor(
+                        out=at_all[:, 4 * b : 4 * b + 4, :].rearrange("p h n -> p (h n)"),
+                        in0=fs[b][:, 0, :],
+                        in1=fs[b][:, 1, :],
+                        op=ALU.add,
+                    )
 
-            def column_sums(b, at_abs, sums_ps):
-                for i in range(4):
+            def column_sums(half_i, sums_ps):
+                for i in range(8):
                     nc.tensor.matmul(
-                        out=sums_ps[:, 1, 4 * (b % 2) + i, :], lhsT=at_abs[:, i, :], rhs=ones_f[:], start=True, stop=True
+                        out=sums_ps[:, 8 + 4 * i : 12 + 4 * i], lhsT=at_all[:, 8 * half_i + i, :], rhs=class3[:], start=True, stop=True
                     )
 
             def same_token_terms(half_i, sums_ps):
@@ -521,7 +517,7 @@ def tile_dwarfattention_pa_k_kernel(
                 n_t = SCALES + 1
                 u = dense.tile([P, 8, n_t], F32, tag="u_diag")
                 nc.vector.tensor_tensor(
-                    out=u[:], in0=sums_ps[:, 0, :, 0:1].to_broadcast([P, 8, n_t]), in1=diag_bias[:, heads, :], op=ALU.add
+                    out=u[:], in0=sums_ps[:, 0:8].unsqueeze(2).to_broadcast([P, 8, n_t]), in1=diag_bias[:, heads, :], op=ALU.add
                 )
                 f = dense.tile([P, 8, n_t], F32, tag="f_diag")
                 nc.scalar.activation(out=f[:], in_=u[:], func=ACT.Exp)
@@ -537,7 +533,16 @@ def tile_dwarfattention_pa_k_kernel(
 
             def normalise(half_i, sums_ps):
                 heads = slice(8 * half_i, 8 * half_i + 8)
-                nc.vector.tensor_tensor(out=z_all[:, heads], in0=sums_ps[:, 1, :, 0], in1=z_all[:, heads], op=ALU.add)
+                signed = dense.tile([P, 8, 4], F32, tag="signed")
+                nc.vector.tensor_tensor(
+                    out=signed[:],
+                    in0=sums_ps[:, 8:40].rearrange("p (h c) -> p h c", c=4),
+                    in1=sign3[:].unsqueeze(1).to_broadcast([P, 8, 4]),
+                    op=ALU.mult,
+                )
+                z_taps = dense.tile([P, 8], F32, tag="z_taps")
+                nc.vector.tensor_reduce(out=z_taps[:], in_=signed[:], op=ALU.add, axis=AXIS_X)
+                nc.vector.tensor_tensor(out=z_all[:, heads], in0=z_taps[:], in1=z_all[:, heads], op=ALU.add)
                 nc.vector.reciprocal(out=z_inv[:, heads], in_=z_all[:, heads])
 
             def score_half(half_i, q_bank, k_bank):
@@ -548,6 +553,8 @@ def tile_dwarfattention_pa_k_kernel(
                     transposes(b)
                 for b in banks:
                     add_bias(b)
+                for b in banks:
+                    plain_q(b)
 
             k1 = accs.tile([P, BANK], F32, tag="acc")
             v_banks = [accs.tile([P, BANK], F32, tag="acc", name="acc_v%d" % i) for i in range(2)]
@@ -557,58 +564,45 @@ def tile_dwarfattention_pa_k_kernel(
             scores(0)
             scores(1)
             mx_passes(10, first_v_load, [k1])
-            same_token_products(0)
-            same_token_products(1)
             exponentials(0)
             exponentials(1)
+            same_token_products(0)
+            same_token_products(1)
             score_half(1, q1, k1)
-            sums_ps0 = work.tile([P, 2, 8, 2], F32, tag="work")
+            sums_ps0 = accs.tile([P, 40], F32, tag="acc")
             same_token_dots(0, sums_ps0)
             same_token_dots(1, sums_ps0)
-            at_abs0 = weigh(0, nc.gpsimd)
+            weigh(0)
             scores(2)
             scores(3)
             mx_passes(first_v_load, first_v_load + 4, v_banks)
-            same_token_products(2)
-            same_token_products(3)
-            at_abs1 = weigh(1, nc.gpsimd)
             u_diag0, f_diag0 = same_token_terms(0, sums_ps0)
             exponentials(2)
             exponentials(3)
-            sums_ps1 = work.tile([P, 2, 8, 2], F32, tag="work")
+            same_token_products(2)
+            same_token_products(3)
+            column_sums(0, sums_ps0)
+            sums_ps1 = accs.tile([P, 40], F32, tag="acc")
             same_token_dots(2, sums_ps1)
             same_token_dots(3, sums_ps1)
-            column_sums(0, at_abs0, sums_ps0)
-            column_sums(1, at_abs1, sums_ps0)
             same_token_sum(0, u_diag0, f_diag0)
-            at_abs2 = weigh(2, nc.gpsimd)
+            weigh(1)
             u_diag1, f_diag1 = same_token_terms(1, sums_ps1)
-            at_abs3 = weigh(3, nc.vector)
-            same_token_sum(1, u_diag1, f_diag1)
             normalise(0, sums_ps0)
             mx_passes(first_v_load + 4, len(w_loads), v_banks)
-            column_sums(2, at_abs2, sums_ps1)
-            column_sums(3, at_abs3, sums_ps1)
+            column_sums(1, sums_ps1)
 
+            same_token_sum(1, u_diag1, f_diag1)
             v_sb = dense.tile([P, HEADS, HEAD_DIM], F32, bufs=1)
             v_diag = dense.tile([P, HEADS, HEAD_DIM], F32, bufs=1)
             o_sb = dense.tile([P, HEADS, HEAD_DIM], F32, bufs=1)
             out_rows = out.rearrange("o n e -> (o n) e")
             for i, bank in enumerate(v_banks):
-                heads = slice(8 * i, 8 * i + 8)
                 nc.vector.tensor_tensor(
-                    out=v_sb[:, heads, :].rearrange("p h d -> p (h d)"),
+                    out=v_sb[:, 8 * i : 8 * i + 8, :].rearrange("p h d -> p (h d)"),
                     in0=bank[:],
                     in1=bias_v[:, BANK * i : BANK * (i + 1)],
                     op=ALU.add,
-                )
-            for i in range(2):
-                heads = slice(8 * i, 8 * i + 8)
-                nc.vector.tensor_tensor(
-                    out=v_diag[:, heads, :],
-                    in0=v_sb[:, heads, :],
-                    in1=w_diag[:, heads].unsqueeze(2).to_broadcast([P, 8, HEAD_DIM]),
-                    op=ALU.mult,
                 )
             o_pss = []
             for b in range(4):
@@ -618,15 +612,21 @@ def tile_dwarfattention_pa_k_kernel(
                     nc.tensor.matmul(out=o_ps[:, i, :], lhsT=at_all[:, h, :], rhs=v_sb[:, h, :], start=True, stop=True)
                 o_pss.append(o_ps)
             normalise(1, sums_ps1)
+            nc.vector.tensor_tensor(out=w_diag[:], in0=w_diag[:], in1=z_inv[:], op=ALU.mult)
+            nc.vector.tensor_tensor(
+                out=v_diag[:], in0=v_sb[:], in1=w_diag[:].unsqueeze(2).to_broadcast([P, HEADS, HEAD_DIM]), op=ALU.mult
+            )
             for b in range(4):
-                heads = slice(4 * b, 4 * b + 4)
-                nc.vector.tensor_tensor(out=o_sb[:, heads, :], in0=o_pss[b][:], in1=v_diag[:, heads, :], op=ALU.add)
-                nc.vector.tensor_tensor(
-                    out=o_sb[:, heads, :],
-                    in0=o_sb[:, heads, :],
-                    in1=z_inv[:, heads].unsqueeze(2).to_broadcast([P, 4, HEAD_DIM]),
-                    op=ALU.mult,
-                )
+                for i in range(4):
+                    h = 4 * b + i
+                    nc.vector.scalar_tensor_tensor(
+                        out=o_sb[:, h, :],
+                        in0=o_pss[b][:, i, :],
+                        scalar=z_inv[:, h : h + 1],
+                        in1=v_diag[:, h, :],
+                        op0=ALU.mult,
+                        op1=ALU.add,
+                    )
                 if b % 2 == 1:
                     cols = slice(BANK * (b // 2), BANK * (b // 2 + 1))
                     nc.sync.dma_start(out=out_rows[:, cols], in_=o_sb[:].rearrange("p h d -> p (h d)")[:, cols])

@@ -73,6 +73,7 @@ def tile_dwarfattention_pa_k_kernel(
         bias_q_half = keep.tile([P, EMB // P, 2], F32)
         bias_tab = keep.tile([P, 2, HEADS, TOKENS], F32)
         gain_tab = keep.tile([P, 2, HEADS, TOKENS], F32)
+        tap_coef = keep.tile([P, TOKENS], F32)
         class3 = keep.tile([P, 4], F32)
         sign3 = keep.tile([P, 4], F32)
         diag_bias = keep.tile([P, HEADS, SCALES + 1], F32)
@@ -157,6 +158,10 @@ def tile_dwarfattention_pa_k_kernel(
                     )
             load_weights_up_to(W_BUFS)
 
+            before = setup.tile([P, TAPS - 1, 8], F32)
+            nc.gpsimd.memset(before[:], 0.0)
+            for j, tau, o in taps_of((1, 2, 3)):
+                nc.gpsimd.memset(before[0:o, tau - 1, j : j + 1], 1.0)
             gains_h = setup.tile([P, TOKENS * SCALES], BF16)
             nc.gpsimd.memset(gains_h[:], 0.0)
             nc.gpsimd.dma_start(out=gains_h[0:HEADS, :], in_=gains.rearrange("o h n j -> (o h) (n j)"))
@@ -175,41 +180,36 @@ def tile_dwarfattention_pa_k_kernel(
             nc.vector.tensor_reduce(
                 out=slot_of_row[:], in_=ident_f[:].rearrange("p (a s) -> p s a", s=SLOTS), op=ALU.add, axis=AXIS_X
             )
-            pb_first_step = [(1, 2), (2, 4)]
-            win_entries = []
-            for layer, taus in enumerate(LAYER_TAUS):
-                first, step = pb_first_step[layer]
-                win_entries.append([((TAPS * j + tau - first) // step, o, 1.0) for j, tau, o in taps_of(taus)])
-            for taus in LAYER_TAUS:
-                win_entries.append([(j, o, D4[tau]) for j, tau, o in taps_of(taus)])
-            win_t = setup.tile([P, 4, GROUP, SLOTS], F32)
+            win_t = setup.tile([P, 2, GROUP, SLOTS], F32)
             nc.vector.memset(win_t[:], 0.0)
-            for i, entries in enumerate(win_entries):
-                for s, o, coef in entries:
-                    nc.vector.scalar_tensor_tensor(
-                        out=win_t[:, i, :, s],
-                        in0=ident_f[:, PAD - o : PAD - o + GROUP],
-                        scalar=coef,
-                        in1=win_t[:, i, :, s],
-                        op0=ALU.mult,
-                        op1=ALU.add,
+            for layer, taus in enumerate(LAYER_TAUS):
+                for j, tau, o in taps_of(taus):
+                    nc.vector.tensor_copy(
+                        out=win_t[:, layer, :, (TAPS * j + tau - layer - 1) // 2], in_=ident_f[:, PAD - o : PAD - o + GROUP]
                     )
-            bias_win = setup.tile([P, 2, PAD + P], BF16)
-            gain_win = setup.tile([P, 2, PAD + P], F32)
-            nc.vector.memset(bias_win[:], 0.0)
-            nc.vector.memset(gain_win[:], 0.0)
+            win = setup.tile([P, 2, PAD + P], BF16)
+            nc.vector.memset(win[:], 0.0)
             gains_pad = setup.tile([P, 2, GROUP, SLOTS], BF16)
-            nc.vector.memset(gains_pad[:], 0.0)
-            nc.vector.tensor_copy(
-                out=gains_pad[:, :, :, 0:SCALES], in_=gains_hg[:].rearrange("p t (a j) -> p t a j", j=SCALES)
-            )
+            gains_by_j = gains_hg[:].rearrange("p t (a j) -> p t a j", j=SCALES)
+            for twin in range(2):
+                nc.vector.tensor_copy(out=gains_pad[:, :, :, twin:SLOTS:2], in_=gains_by_j[:, :, :, 0 : SLOTS // 2])
+
+            nc.vector.memset(class3[:], 0.0)
+            for c in range(3):
+                nc.vector.tensor_reduce(out=class3[:, c : c + 1], in_=ident_f[:, c:TOKENS:3], op=ALU.add, axis=AXIS_X)
+            nc.vector.tensor_scalar(out=sign3[:], in0=class3[:], scalar1=-2.0, scalar2=1.0, op0=ALU.mult, op1=ALU.add)
+            for c in range(3):
+                n_c = len(range(c, TOKENS, 3))
+                nc.vector.tensor_scalar(
+                    out=tap_coef[:, c:TOKENS:3],
+                    in0=class3[:, c : c + 1].to_broadcast([P, n_c]),
+                    scalar1=D4[3] - D4[1],
+                    scalar2=D4[1],
+                    op0=ALU.mult,
+                    op1=ALU.add,
+                )
 
             small_all = setup.tile([P, n_pb + HEADS], F32)
-            half = (n_pb + HEADS) // 2
-            for i in range(2):
-                ps = work.tile([P, half], F32, tag="work")
-                nc.tensor.matmul(out=ps[:], lhsT=ones_b[:], rhs=small_row[:, half * i : half * (i + 1)], start=True, stop=True)
-                nc.vector.tensor_copy(out=small_all[:, half * i : half * (i + 1)], in_=ps[:])
             pb_all = small_all[:, 0:n_pb]
             pb_by_tau = pb_all.rearrange("p (j t h) -> p t h j", t=TAPS, h=HEADS)
             bypass_all = small_all[:, n_pb:]
@@ -230,48 +230,7 @@ def tile_dwarfattention_pa_k_kernel(
                         out=grouped_words[:, 2 * pair : 2 * pair + 2, :, :], in_=xt[:].rearrange("p g u t -> p g t u")
                     )
 
-            transpose_x(0, 2)
-            win_ps = work.tile([P, 4, P], F32, tag="work")
-            for i in range(4):
-                nc.tensor.transpose(win_ps[:, i, :], win_t[:, i, :, :].rearrange("p a s -> p (a s)"), ident_f[:])
-            nc.scalar.copy(out=bias_win[:, :, 0:P], in_=win_ps[:, 0:2, :])
-            nc.scalar.copy(out=gain_win[:, :, 0:P], in_=win_ps[:, 2:4, :])
-            gains_ps = work.tile([P, 2, P], BF16, tag="work")
-            for t in range(2):
-                nc.tensor.transpose(gains_ps[:, t, :], gains_pad[:, t, :, :].rearrange("p a s -> p (a s)"), ident_b[:])
-            transpose_x(2, PASSES // 2)
-
-            gains_rows = setup.tile([P, HEADS, GROUPS], F32)
-            nc.vector.tensor_copy(
-                out=gains_rows[:].rearrange("p h g -> p (h g)"), in_=gains_ps[:].rearrange("p t c -> p (t c)")
-            )
-            gain_moving = setup.tile([P, GROUPS, HEADS, GROUP], F32)
-            nc.vector.tensor_tensor(
-                out=gain_moving[:],
-                in0=gains_rows[:].rearrange("p h g -> p g h").unsqueeze(3).to_broadcast([P, GROUPS, HEADS, GROUP]),
-                in1=token_of_row[:].unsqueeze(1).unsqueeze(1).to_broadcast([P, GROUPS, HEADS, GROUP]),
-                op=ALU.mult,
-            )
-            bias_moving = setup.tile([P, 2, HEADS, GROUP], BF16)
-            for layer in range(2):
-                first, step = pb_first_step[layer]
-                n_slots = min(SLOTS, (SCALES * TAPS - first + step - 1) // step)
-                picked = setup.tile([P, HEADS, SLOTS], F32, tag="picked", bufs=2)
-                nc.vector.tensor_tensor(
-                    out=picked[:, :, 0:n_slots],
-                    in0=pb_all.rearrange("p (r h) -> p h r", h=HEADS)[:, :, first : first + step * (n_slots - 1) + 1 : step],
-                    in1=slot_of_row[:, 0:n_slots].unsqueeze(1).to_broadcast([P, HEADS, n_slots]),
-                    op=ALU.mult,
-                )
-                pb_rows = setup.tile([P, HEADS], F32, tag="pb_rows", bufs=2)
-                nc.vector.tensor_reduce(out=pb_rows[:], in_=picked[:, :, 0:n_slots], op=ALU.add, axis=AXIS_X)
-                nc.vector.tensor_tensor(
-                    out=bias_moving[:, layer, :, :],
-                    in0=pb_rows[:].unsqueeze(2).to_broadcast([P, HEADS, GROUP]),
-                    in1=token_of_row[:].unsqueeze(1).to_broadcast([P, HEADS, GROUP]),
-                    op=ALU.mult,
-                )
-
+            transpose_x(0, PASSES // 2)
             for quarter in range(4):
                 cols = slice(4 * TOKENS * quarter, 4 * TOKENS * (quarter + 1))
                 nc.vector.quantize_mx(
@@ -279,40 +238,71 @@ def tile_dwarfattention_pa_k_kernel(
                     scales=x_scales[:, cols],
                     in_=grouped_flat[:, 4 * K_PASS * quarter : 4 * K_PASS * (quarter + 1)],
                 )
+            half = (n_pb + HEADS) // 2
+            for i in range(2):
+                ps = work.tile([P, half], F32, tag="work")
+                nc.tensor.matmul(out=ps[:], lhsT=ones_b[:], rhs=small_row[:, half * i : half * (i + 1)], start=True, stop=True)
+                nc.vector.tensor_copy(out=small_all[:, half * i : half * (i + 1)], in_=ps[:])
+            win_ps = work.tile([P, 2, P], F32, tag="work")
+            for layer in range(2):
+                nc.tensor.transpose(win_ps[:, layer, :], win_t[:, layer, :, :].rearrange("p a s -> p (a s)"), ident_f[:])
+            nc.scalar.copy(out=win[:, :, 0:P], in_=win_ps[:])
+            gains_ps = work.tile([P, 2, P], BF16, tag="work")
+            for t in range(2):
+                nc.tensor.transpose(gains_ps[:, t, :], gains_pad[:, t, :, :].rearrange("p a s -> p (a s)"), ident_b[:])
+
+            bias_moving = setup.tile([P, 2, GROUP, HEADS], BF16)
+            for layer in range(2):
+                picked = setup.tile([P, HEADS, SLOTS], F32, tag="picked", bufs=2)
+                nc.vector.tensor_tensor(
+                    out=picked[:],
+                    in0=pb_all.rearrange("p (r h) -> p h r", h=HEADS)[:, :, layer + 1 : layer + 2 * SLOTS : 2],
+                    in1=slot_of_row[:].unsqueeze(1).to_broadcast([P, HEADS, SLOTS]),
+                    op=ALU.mult,
+                )
+                pb_rows = setup.tile([P, HEADS], F32, tag="pb_rows", bufs=2)
+                nc.vector.tensor_reduce(out=pb_rows[:], in_=picked[:], op=ALU.add, axis=AXIS_X)
+                nc.vector.tensor_tensor(
+                    out=bias_moving[:, layer, :, :],
+                    in0=pb_rows[:].unsqueeze(1).to_broadcast([P, GROUP, HEADS]),
+                    in1=token_of_row[:].unsqueeze(2).to_broadcast([P, GROUP, HEADS]),
+                    op=ALU.mult,
+                )
+            gains_rows = setup.tile([P, GROUPS, HEADS], BF16)
+            nc.vector.tensor_copy(
+                out=gains_rows[:], in_=gains_ps[:].rearrange("p t c -> p (t c)").rearrange("p (h g) -> p g h", h=HEADS)
+            )
+            gain_moving = setup.tile([P, GROUPS, GROUP, HEADS], BF16)
+            for a in range(GROUP):
+                nc.vector.tensor_scalar_mul(out=gain_moving[:, :, a, :], in0=gains_rows[:], scalar1=token_of_row[:, a : a + 1])
 
             def table_quarter(quarter):
                 cols = slice(4 * GROUP * quarter, 4 * GROUP * (quarter + 1))
                 for layer in range(2):
-                    bias_ps = work.tile([P, 4, HEADS, GROUP], F32, tag="work")
-                    gain_ps = work.tile([P, 4, HEADS, GROUP], F32, tag="work")
+                    bias_ps = work.tile([P, 4 * GROUP, HEADS], F32, tag="work")
+                    gain_ps = work.tile([P, 4 * GROUP, HEADS], F32, tag="work")
                     for gl in range(4):
                         grp = 4 * quarter + gl
-                        nc.tensor.matmul(
-                            out=bias_ps[:, gl, :, :],
-                            lhsT=bias_win[:, layer, PAD - GROUP * grp : PAD - GROUP * grp + P],
-                            rhs=bias_moving[:, layer, :, :],
-                            start=True,
-                            stop=True,
-                        )
-                    for gl in range(4):
-                        grp = 4 * quarter + gl
-                        nc.tensor.matmul(
-                            out=gain_ps[:, gl, :, :],
-                            lhsT=gain_win[:, layer, PAD - GROUP * grp : PAD - GROUP * grp + P],
-                            rhs=gain_moving[:, grp, :, :],
-                            start=True,
-                            stop=True,
-                        )
+                        for ps, moving in ((bias_ps, bias_moving[:, layer, :, :]), (gain_ps, gain_moving[:, grp, :, :])):
+                            nc.tensor.matmul(
+                                out=ps[:, GROUP * gl : GROUP * (gl + 1), :],
+                                lhsT=win[:, layer, PAD - GROUP * grp : PAD - GROUP * grp + P],
+                                rhs=moving,
+                                start=True,
+                                stop=True,
+                            )
                     nc.scalar.activation(
-                        out=bias_tab[:, layer, :, cols].rearrange("p h (g a) -> p h g a", a=GROUP),
-                        in_=bias_ps[:].rearrange("p g h a -> p h g a"),
+                        out=bias_tab[:, layer, :, cols],
+                        in_=bias_ps[:].rearrange("p n h -> p h n"),
                         func=ACT.Identity,
                         bias=ones_f[:, 0:1],
                     )
-                    nc.vector.tensor_copy(
-                        out=gain_tab[:, layer, :, cols].rearrange("p h (g a) -> p h g a", a=GROUP),
-                        in_=gain_ps[:].rearrange("p g h a -> p h g a"),
-                    )
+                    gain_in = gain_ps[:].rearrange("p n h -> p h n")
+                    if layer == 0:
+                        coef = tap_coef[:, cols].unsqueeze(1).to_broadcast([P, HEADS, 4 * GROUP])
+                        nc.vector.tensor_tensor(out=gain_tab[:, layer, :, cols], in0=gain_in, in1=coef, op=ALU.mult)
+                    else:
+                        nc.vector.tensor_scalar_mul(out=gain_tab[:, layer, :, cols], in0=gain_in, scalar1=D4[2])
 
             def spread_b_qkv():
                 for i in range(EMB // BANK):
@@ -344,10 +334,6 @@ def tile_dwarfattention_pa_k_kernel(
                     )
 
             def small_tables():
-                nc.vector.memset(class3[:], 0.0)
-                for c in range(3):
-                    nc.vector.tensor_reduce(out=class3[:, c : c + 1], in_=ident_f[:, c:TOKENS:3], op=ALU.add, axis=AXIS_X)
-                nc.vector.tensor_scalar(out=sign3[:], in0=class3[:], scalar1=-2.0, scalar2=1.0, op0=ALU.mult, op1=ALU.add)
                 soft = setup.tile([P, HEADS], F32)
                 nc.scalar.activation(out=soft[:], in_=bypass_all, func=ACT.Abs)
                 nc.scalar.activation(out=soft[:], in_=soft[:], func=ACT.Exp, scale=-1.0)
@@ -359,45 +345,36 @@ def tile_dwarfattention_pa_k_kernel(
                 nc.vector.memset(diag_bias[:, :, SCALES], 0.0)
                 nc.vector.tensor_copy(out=diag_bias[:, :, 0:SCALES], in_=pb_by_tau[:, 0, :, :])
 
-                f_of_bias = setup.tile([P, n_pb], F32)
-                f_tmp = setup.tile([P, n_pb], F32)
-                elu_plus_one(f_of_bias[:], pb_all, f_tmp[:])
-                f_by_tau = f_of_bias[:].rearrange("p (j t h) -> p t h j", t=TAPS, h=HEADS)
-                nc.vector.memset(z_fixed[:], EPS)
+                n_f = TAPS * 8 * HEADS
+                f_of_bias = setup.tile([P, n_f], F32)
+                f_tmp = setup.tile([P, n_f], F32)
+                elu_plus_one(f_of_bias[:], pb_all[:, 0:n_f], f_tmp[:])
                 for tau in range(1, TAPS):
-                    taps = taps_of((tau,))
-                    n_j = len(taps)
-                    before = setup.tile([P, 8], F32, tag="before", bufs=2)
-                    for j, same_tau, o in taps:
-                        nc.vector.tensor_reduce(out=before[:, j : j + 1], in_=ident_f[:, 0:o], op=ALU.add, axis=AXIS_X)
-                    gf = setup.tile([P, HEADS, 8], F32, tag="gf", bufs=2)
-                    nc.vector.tensor_tensor(
-                        out=gf[:, :, 0:n_j], in0=gains_nt[:, :, 0:n_j], in1=f_by_tau[:, tau, :, 0:n_j], op=ALU.mult
-                    )
-                    nc.vector.tensor_tensor(
-                        out=gf[:, :, 0:n_j],
-                        in0=gf[:, :, 0:n_j],
-                        in1=before[:, 0:n_j].unsqueeze(1).to_broadcast([P, HEADS, n_j]),
-                        op=ALU.mult,
-                    )
-                    gf_sum = setup.tile([P, HEADS], F32, tag="gf_sum", bufs=2)
-                    nc.vector.tensor_reduce(out=gf_sum[:], in_=gf[:, :, 0:n_j], op=ALU.add, axis=AXIS_X)
-                    nc.vector.scalar_tensor_tensor(
-                        out=z_fixed[:], in0=gf_sum[:], scalar=abs(D4[tau]), in1=z_fixed[:], op0=ALU.mult, op1=ALU.add
-                    )
+                    nc.vector.tensor_scalar_mul(out=before[:, tau - 1, :], in0=before[:, tau - 1, :], scalar1=abs(D4[tau]))
+                gf = setup.tile([P, HEADS, TAPS - 1, 8], F32)
+                nc.vector.tensor_tensor(
+                    out=gf[:],
+                    in0=f_of_bias[:].rearrange("p (j t h) -> p h t j", t=TAPS, h=HEADS)[:, :, 1:TAPS, :],
+                    in1=gains_nt[:, :, 0:8].unsqueeze(2).to_broadcast([P, HEADS, TAPS - 1, 8]),
+                    op=ALU.mult,
+                )
+                nc.vector.tensor_tensor(
+                    out=gf[:], in0=gf[:], in1=before[:].unsqueeze(1).to_broadcast([P, HEADS, TAPS - 1, 8]), op=ALU.mult
+                )
+                gf_sum = setup.tile([P, HEADS], F32)
+                nc.vector.tensor_reduce(out=gf_sum[:], in_=gf[:].rearrange("p h t j -> p h (t j)"), op=ALU.add, axis=AXIS_X)
+                nc.vector.tensor_scalar_add(out=z_fixed[:], in0=gf_sum[:], scalar1=EPS)
 
             q0, q1, k0 = [accs.tile([P, BANK], F32, tag="acc", name="acc_%s" % n) for n in ("q0", "q1", "k0")]
-            table_quarter(0)
-            table_quarter(1)
+            for t in range(4):
+                mx_passes(t, t + 1, [q0, q1, k0])
+                table_quarter(t)
+            mx_passes(4, 5, [q0, q1, k0])
             transpose_gains()
-            mx_passes(0, 2, [q0, q1, k0])
             small_tables()
-            table_quarter(2)
-            mx_passes(2, 3, [q0, q1, k0])
-            table_quarter(3)
-            mx_passes(3, 4, [q0, q1, k0])
+            mx_passes(5, 6, [q0, q1, k0])
             spread_b_qkv()
-            mx_passes(4, 8, [q0, q1, k0])
+            mx_passes(6, 8, [q0, q1, k0])
 
         with tc.tile_pool(name="dense", bufs=2) as dense:
             width = 4 * HEAD_DIM

@@ -64,14 +64,14 @@ def tile_dwarfattention_pa_k_kernel(
         ones_b = keep.tile([P, P], BF16)
         ones_f = keep.tile([P, 2], F32)
         minus_one = keep.tile([P, 1], F32)
-        half_mask = keep.tile([P, 2], F32)
         x_codes = keep.tile([P, PASSES * TOKENS], U32, align_bytes=64)
         x_scales = keep.tile([P, PASSES * TOKENS], U8, align_bytes=64)
         w_planes = keep.tile([P, PASSES // PLANES, 3 * EMB], U8, align_bytes=64)
-        bias_v = keep.tile([P, EMB], BF16)
-        bias_cols = keep.tile([P, 2 * EMB // P], F32)
-        bias_q_half = keep.tile([P, EMB // P, 2], F32)
-        bias_tab = keep.tile([P, 2, HEADS, TOKENS], F32)
+        bias_all = keep.tile([P, 3 * EMB], BF16)
+        q_split = [keep.tile([P, 4, 2, TOKENS], F32, name="q_split%d" % i) for i in range(2)]
+        base_tab = keep.tile([P, HEADS, TOKENS], BF16)
+        step_tab = keep.tile([P, HEADS, TOKENS], F32)
+        add_base = keep.tile([P, P], BF16)
         gain_tab = keep.tile([P, 2, HEADS, TOKENS], F32)
         tap_coef = keep.tile([P, TOKENS], F32)
         class3 = keep.tile([P, 4], F32)
@@ -80,19 +80,29 @@ def tile_dwarfattention_pa_k_kernel(
         diag_gain = keep.tile([P, HEADS, SCALES + 1], F32)
         z_fixed = keep.tile([P, HEADS], F32)
         at_all = keep.tile([P, HEADS, TOKENS], F32)
+        v_sb = keep.tile([P, HEADS, HEAD_DIM + 4], F32)
         w_diag = keep.tile([P, HEADS], F32)
-        z_all = keep.tile([P, HEADS], F32)
+        z_parts = keep.tile([P, HEADS, 4], F32)
         z_inv = keep.tile([P, HEADS], F32)
 
         w_words = W_qkv_words.rearrange("g p n t -> p g (n t)").bitcast(I32)
-        w_loads = [(g0, 2, 0, 3 * BANK) for g0 in range(0, PASSES, 2)]
-        w_loads += [(g0, 4, 3 * BANK, BANK) for g0 in range(0, PASSES, 4)]
-        first_v_load = len(w_loads)
-        g0 = 0
-        while g0 < PASSES:
-            n_g = min(2, max(1, (PASSES - g0) // 2))
-            w_loads.append((g0, n_g, 2 * EMB, 2 * BANK))
-            g0 += n_g
+        wide, head = 4, PASSES - 4
+        w_loads = [(g0, 1, 0, 4 * BANK) for g0 in range(wide)]
+        qk_load = len(w_loads)
+        w_loads += [(g0, 2, 0, 3 * BANK) for g0 in range(wide, head, 2)]
+        q0_load = len(w_loads)
+        w_loads += [(head, 4, col0, BANK) for col0 in (0, EMB, BANK)]
+        k1_load = len(w_loads)
+        w_loads += [(g0, 4, 3 * BANK, BANK) for g0 in range(wide, head, 4)]
+        w_loads += [(g0, 2, 3 * BANK, BANK) for g0 in range(head, PASSES, 2)]
+        v_load = len(w_loads)
+        half_v = PASSES - 8
+        w_loads += [(g0, 2, 2 * EMB, 2 * BANK) for g0 in range(0, half_v, 2)]
+        v0_load = len(w_loads)
+        w_loads += [(g0, 4, 2 * EMB, BANK) for g0 in range(half_v, PASSES, 4)]
+        v1_load = len(w_loads)
+        w_loads += [(half_v, 4, 2 * EMB + BANK, BANK)]
+        w_loads += [(g0, 2, 2 * EMB + BANK, BANK) for g0 in range(half_v + 4, PASSES, 2)]
         w_tiles = []
 
         def load_weights_up_to(n):
@@ -141,9 +151,6 @@ def tile_dwarfattention_pa_k_kernel(
             nc.gpsimd.memset(ones_b[:], 1.0)
             nc.gpsimd.memset(ones_f[:], 1.0)
             nc.gpsimd.memset(minus_one[:], -1.0)
-            nc.gpsimd.memset(half_mask[:], 0.0)
-            nc.gpsimd.memset(half_mask[0:HEAD_DIM, 0:1], 1.0)
-            nc.gpsimd.memset(half_mask[HEAD_DIM:P, 1:2], 1.0)
 
             x_sb = setup.tile([P, D_MODEL], BF16)
             x_rows = x.rearrange("o n k -> (o n) k")
@@ -158,19 +165,18 @@ def tile_dwarfattention_pa_k_kernel(
                     )
             load_weights_up_to(W_BUFS)
 
+            gains_h = setup.tile([P, TOKENS * SCALES], BF16)
+            nc.gpsimd.memset(gains_h[:], 0.0)
+            nc.gpsimd.dma_start(out=gains_h[0:HEADS, :], in_=gains.rearrange("o h n j -> (o h) (n j)"))
+            bias_row = setup.tile([P, 3 * EMB], BF16)
+            nc.gpsimd.memset(bias_row[:], 0.0)
+            nc.gpsimd.dma_start(out=bias_row[0:1, :], in_=b_qkv.rearrange("(o n) -> o n", o=1))
             before = setup.tile([P, TAPS - 1, 8], F32)
             nc.gpsimd.memset(before[:], 0.0)
             for j, tau, o in taps_of((1, 2, 3)):
                 nc.gpsimd.memset(before[0:o, tau - 1, j : j + 1], 1.0)
-            gains_h = setup.tile([P, TOKENS * SCALES], BF16)
-            nc.gpsimd.memset(gains_h[:], 0.0)
-            nc.gpsimd.dma_start(out=gains_h[0:HEADS, :], in_=gains.rearrange("o h n j -> (o h) (n j)"))
-            bias_row = setup.tile([P, EMB], BF16)
-            nc.gpsimd.memset(bias_row[:], 0.0)
-            nc.gpsimd.dma_start(out=bias_row[0:1, :], in_=b_qkv[2 * EMB :].rearrange("(o n) -> o n", o=1))
-            bias_rows = setup.tile([P, P], BF16)
-            nc.gpsimd.memset(bias_rows[:], 0.0)
-            nc.gpsimd.dma_start(out=bias_rows[0 : 2 * EMB // P, :], in_=b_qkv[0 : 2 * EMB].rearrange("(r c) -> r c", c=P))
+            for tile in q_split:
+                nc.gpsimd.memset(tile[:], 0.0)
 
             token_of_row = setup.tile([P, GROUP], F32)
             nc.vector.tensor_reduce(
@@ -179,6 +185,9 @@ def tile_dwarfattention_pa_k_kernel(
             slot_of_row = setup.tile([P, SLOTS], F32)
             nc.vector.tensor_reduce(
                 out=slot_of_row[:], in_=ident_f[:].rearrange("p (a s) -> p s a", s=SLOTS), op=ALU.add, axis=AXIS_X
+            )
+            nc.vector.tensor_tensor(
+                out=add_base[:], in0=ident_b[:], in1=ident_b[:, P - 1 : P].to_broadcast([P, P]), op=ALU.max
             )
             win_t = setup.tile([P, 2, GROUP, SLOTS], F32)
             nc.vector.memset(win_t[:], 0.0)
@@ -197,6 +206,7 @@ def tile_dwarfattention_pa_k_kernel(
             nc.vector.memset(class3[:], 0.0)
             for c in range(3):
                 nc.vector.tensor_reduce(out=class3[:, c : c + 1], in_=ident_f[:, c:TOKENS:3], op=ALU.add, axis=AXIS_X)
+            nc.vector.tensor_copy(out=v_sb[:, :, HEAD_DIM:], in_=class3[:].unsqueeze(1).to_broadcast([P, HEADS, 4]))
             nc.vector.tensor_scalar(out=sign3[:], in0=class3[:], scalar1=-2.0, scalar2=1.0, op0=ALU.mult, op1=ALU.add)
             for c in range(3):
                 n_c = len(range(c, TOKENS, 3))
@@ -251,7 +261,7 @@ def tile_dwarfattention_pa_k_kernel(
             for t in range(2):
                 nc.tensor.transpose(gains_ps[:, t, :], gains_pad[:, t, :, :].rearrange("p a s -> p (a s)"), ident_b[:])
 
-            bias_moving = setup.tile([P, 2, GROUP, HEADS], BF16)
+            bias_moving = setup.tile([P, 3, GROUP, HEADS], BF16)
             for layer in range(2):
                 picked = setup.tile([P, HEADS, SLOTS], F32, tag="picked", bufs=2)
                 nc.vector.tensor_tensor(
@@ -268,6 +278,7 @@ def tile_dwarfattention_pa_k_kernel(
                     in1=token_of_row[:].unsqueeze(2).to_broadcast([P, GROUP, HEADS]),
                     op=ALU.mult,
                 )
+            nc.vector.tensor_scalar_mul(out=bias_moving[:, 2, :, :], in0=bias_moving[:, 0, :, :], scalar1=-1.0)
             gains_rows = setup.tile([P, GROUPS, HEADS], BF16)
             nc.vector.tensor_copy(
                 out=gains_rows[:], in_=gains_ps[:].rearrange("p t c -> p (t c)").rearrange("p (h g) -> p g h", h=HEADS)
@@ -283,20 +294,25 @@ def tile_dwarfattention_pa_k_kernel(
                     gain_ps = work.tile([P, 4 * GROUP, HEADS], F32, tag="work")
                     for gl in range(4):
                         grp = 4 * quarter + gl
-                        for ps, moving in ((bias_ps, bias_moving[:, layer, :, :]), (gain_ps, gain_moving[:, grp, :, :])):
+                        rows = slice(GROUP * gl, GROUP * (gl + 1))
+                        wins = [win[:, i, PAD - GROUP * grp : PAD - GROUP * grp + P] for i in range(2)]
+                        nc.tensor.matmul(
+                            out=bias_ps[:, rows, :], lhsT=wins[layer], rhs=bias_moving[:, layer, :, :], start=True, stop=(layer == 0)
+                        )
+                        if layer == 1:
                             nc.tensor.matmul(
-                                out=ps[:, GROUP * gl : GROUP * (gl + 1), :],
-                                lhsT=win[:, layer, PAD - GROUP * grp : PAD - GROUP * grp + P],
-                                rhs=moving,
-                                start=True,
-                                stop=True,
+                                out=bias_ps[:, rows, :], lhsT=wins[0], rhs=bias_moving[:, 2, :, :], start=False, stop=True
                             )
-                    nc.scalar.activation(
-                        out=bias_tab[:, layer, :, cols],
-                        in_=bias_ps[:].rearrange("p n h -> p h n"),
-                        func=ACT.Identity,
-                        bias=ones_f[:, 0:1],
-                    )
+                        nc.tensor.matmul(
+                            out=gain_ps[:, rows, :], lhsT=wins[layer], rhs=gain_moving[:, grp, :, :], start=True, stop=True
+                        )
+                    bias_in = bias_ps[:].rearrange("p n h -> p h n")
+                    if layer == 0:
+                        nc.scalar.activation(
+                            out=base_tab[:, :, cols], in_=bias_in, func=ACT.Identity, bias=ident_f[:, P - 1 : P]
+                        )
+                    else:
+                        nc.scalar.copy(out=step_tab[:, :, cols], in_=bias_in)
                     gain_in = gain_ps[:].rearrange("p n h -> p h n")
                     if layer == 0:
                         coef = tap_coef[:, cols].unsqueeze(1).to_broadcast([P, HEADS, 4 * GROUP])
@@ -304,22 +320,13 @@ def tile_dwarfattention_pa_k_kernel(
                     else:
                         nc.vector.tensor_scalar_mul(out=gain_tab[:, layer, :, cols], in0=gain_in, scalar1=D4[2])
 
-            def spread_b_qkv():
-                for i in range(EMB // BANK):
+            def spread_b_qkv(first, last):
+                for i in range(first, last):
                     ps = work.tile([P, BANK], F32, tag="work")
                     nc.tensor.matmul(
                         out=ps[:], lhsT=ones_b[:], rhs=bias_row[:, BANK * i : BANK * (i + 1)], start=True, stop=True
                     )
-                    nc.scalar.copy(out=bias_v[:, BANK * i : BANK * (i + 1)], in_=ps[:])
-                ps = work.tile([P, P], BF16, tag="work")
-                nc.tensor.transpose(ps[:], bias_rows[:], ident_b[:])
-                nc.vector.tensor_copy(out=bias_cols[:], in_=ps[:, 0 : 2 * EMB // P])
-                nc.vector.tensor_tensor(
-                    out=bias_q_half[:],
-                    in0=bias_cols[:, 0 : EMB // P].unsqueeze(2).to_broadcast([P, EMB // P, 2]),
-                    in1=half_mask[:].unsqueeze(1).to_broadcast([P, EMB // P, 2]),
-                    op=ALU.mult,
-                )
+                    nc.scalar.copy(out=bias_all[:, BANK * i : BANK * (i + 1)], in_=ps[:])
 
             gains_nt = setup.tile([P, HEADS, SCALES], F32)
 
@@ -342,8 +349,8 @@ def tile_dwarfattention_pa_k_kernel(
                     out=diag_gain[:, :, SCALES], in0=bypass_all, scalar=0.0, in1=soft[:], op0=ALU.max, op1=ALU.add
                 )
                 nc.vector.tensor_scalar_mul(out=diag_gain[:, :, 0:SCALES], in0=gains_nt[:], scalar1=D4[0])
-                nc.vector.memset(diag_bias[:, :, SCALES], 0.0)
-                nc.vector.tensor_copy(out=diag_bias[:, :, 0:SCALES], in_=pb_by_tau[:, 0, :, :])
+                nc.vector.memset(diag_bias[:, :, SCALES], 1.0)
+                nc.vector.tensor_scalar_add(out=diag_bias[:, :, 0:SCALES], in0=pb_by_tau[:, 0, :, :], scalar1=1.0)
 
                 n_f = TAPS * 8 * HEADS
                 f_of_bias = setup.tile([P, n_f], F32)
@@ -365,245 +372,281 @@ def tile_dwarfattention_pa_k_kernel(
                 nc.vector.tensor_reduce(out=gf_sum[:], in_=gf[:].rearrange("p h t j -> p h (t j)"), op=ALU.add, axis=AXIS_X)
                 nc.vector.tensor_scalar_add(out=z_fixed[:], in0=gf_sum[:], scalar1=EPS)
 
-            q0, q1, k0 = [accs.tile([P, BANK], F32, tag="acc", name="acc_%s" % n) for n in ("q0", "q1", "k0")]
+            q0, q1, k0, k1 = [accs.tile([P, BANK], F32, tag="acc", name="acc_%s" % n) for n in ("q0", "q1", "k0", "k1")]
             for t in range(4):
-                mx_passes(t, t + 1, [q0, q1, k0])
+                mx_passes(t, t + 1, [q0, q1, k0, k1])
                 table_quarter(t)
-            mx_passes(4, 5, [q0, q1, k0])
+            mx_passes(qk_load, qk_load + 1, [q0, q1, k0])
             transpose_gains()
             small_tables()
-            mx_passes(5, 6, [q0, q1, k0])
-            spread_b_qkv()
-            mx_passes(6, 8, [q0, q1, k0])
-
+            mx_passes(qk_load + 1, qk_load + 2, [q0, q1, k0])
+            spread_b_qkv(0, 6)
+            mx_passes(qk_load + 2, q0_load, [q0, q1, k0])
         with tc.tile_pool(name="dense", bufs=2) as dense:
-            width = 4 * HEAD_DIM
-            toks, trs, k_ts, q_ts, q_ps, sts, us, fs, prods = {}, {}, {}, {}, {}, {}, {}, {}, {}
+            pairs = range(4)
+            toks, trs, k_ts, prods = {}, {}, {}, {}
+            sts, us, fs = {}, {}, {}
 
-            def to_sbuf(b, q_bank, k_bank):
-                tok = dense.tile([P, 2, width], F32, tag="tok")
-                for qk, bank in enumerate((q_bank, k_bank)):
-                    nc.scalar.copy(out=tok[:, qk, :], in_=bank[:, width * (b % 2) : width * (b % 2 + 1)])
-                toks[b] = tok
+            def to_sbuf(key, bank, col0):
+                tok = dense.tile([P, BANK], F32, tag="tok", bufs=4)
+                nc.vector.tensor_tensor(out=tok[:], in0=bank[:], in1=bias_all[:, col0 : col0 + BANK], op=ALU.add)
+                toks[key] = tok
 
-            def transposes(b):
+            def transposes(key):
                 tr = work.tile([P, 4, TOKENS], F32, tag="work")
-                tok_flat = toks[b][:].rearrange("p qk c -> p (qk c)")
-                for t in range(4):
-                    nc.tensor.transpose(tr[:, t, :], tok_flat[:, P * t : P * (t + 1)], ident_f[:])
-                trs[b] = tr
+                for pair in pairs:
+                    nc.tensor.transpose(tr[:, pair, :], toks[key][:, P * pair : P * (pair + 1)], ident_f[:])
+                trs[key] = tr
 
-            def add_bias(b):
-                k_t = dense.tile([P, 2, TOKENS], F32, tag="k_t")
-                q_t = dense.tile([P, 2, 2, TOKENS], F32, tag="q_t")
-                for pair in range(2):
-                    t = 2 * b + pair
-                    nc.scalar.activation(
-                        out=k_t[:, pair, :],
-                        in_=trs[b][:, 2 + pair, :],
-                        func=ACT.Identity,
-                        bias=bias_cols[:, EMB // P + t : EMB // P + t + 1],
-                    )
-                    for hd in range(2):
-                        nc.scalar.activation(
-                            out=q_t[:, pair, hd, :],
-                            in_=trs[b][:, pair, :],
-                            func=ACT.Identity,
-                            scale=half_mask[:, hd : hd + 1],
-                            bias=bias_q_half[:, t, hd : hd + 1],
-                        )
-                k_ts[b] = k_t
-                q_ts[b] = q_t
+            def plain_k(half_i, copy):
+                k_t = dense.tile([P, 4, TOKENS], F32, tag="k_t")
+                for two in (slice(0, 2), slice(2, 4)):
+                    copy(out=k_t[:, two, :], in_=trs["k", half_i][:, two, :])
+                k_ts[half_i] = k_t
+
+            def split_q(b):
+                two = slice(2 * (b % 2), 2 * (b % 2) + 2)
+                for hd in range(2):
+                    rows = slice(HEAD_DIM * hd, HEAD_DIM * (hd + 1))
+                    nc.scalar.copy(out=q_split[b // 2][rows, two, hd, :], in_=trs["q", b // 2][rows, two, :])
 
             def scores(b):
-                st = work.tile([P, 4 * TOKENS], F32, tag="work")
-                for pair in range(2):
+                st = work.tile([P, 4, TOKENS], F32, tag="work")
+                for i in range(2):
+                    pair = 2 * (b % 2) + i
+                    out_i = st[:, 2 * i : 2 * i + 2, :]
                     nc.tensor.matmul(
-                        out=st[:, 2 * TOKENS * pair : 2 * TOKENS * (pair + 1)],
-                        lhsT=k_ts[b][:, pair, :],
-                        rhs=q_ts[b][:, pair, :, :],
+                        out=out_i,
+                        lhsT=add_base[:],
+                        rhs=base_tab[:, 4 * b + 2 * i : 4 * b + 2 * i + 2, :],
                         start=True,
-                        stop=True,
+                        stop=False,
+                    )
+                    nc.tensor.matmul(
+                        out=out_i, lhsT=k_ts[b // 2][:, pair, :], rhs=q_split[b // 2][:, pair, :, :], start=False, stop=True
                     )
                 sts[b] = st
 
-            def plain_q(b):
-                q_p = dense.tile([P, 2, TOKENS], F32, tag="q_p")
-                for pair in range(2):
-                    t = 2 * b + pair
+            dots = dense.tile([P, HEADS], F32, bufs=1)
+
+            def same_token_products(half_i):
+                prod = dense.tile([P, BANK], F32, tag="prod")
+                nc.vector.tensor_tensor(out=prod[:], in0=toks["q", half_i][:], in1=toks["k", half_i][:], op=ALU.mult)
+                prods[half_i] = prod
+
+            def same_token_dots(half_i):
+                for i in range(8):
+                    cols = slice(HEAD_DIM * i, HEAD_DIM * (i + 1))
                     nc.scalar.activation(
-                        out=q_p[:, pair, :], in_=trs[b][:, pair, :], func=ACT.Identity, bias=bias_cols[:, t : t + 1]
-                    )
-                q_ps[b] = q_p
-
-            def same_token_products(b):
-                prod = dense.tile([P, 2, TOKENS], F32, tag="prod")
-                nc.vector.tensor_tensor(out=prod[:], in0=q_ps[b][:], in1=k_ts[b][:], op=ALU.mult)
-                prods[b] = prod
-
-            def same_token_dots(b, sums_ps):
-                for pair in range(2):
-                    h = 4 * (b % 2) + 2 * pair
-                    nc.tensor.matmul(
-                        out=sums_ps[:, h : h + 2], lhsT=prods[b][:, pair, :], rhs=half_mask[:], start=True, stop=True
+                        out=prods[half_i][:, cols],
+                        in_=prods[half_i][:, cols],
+                        func=ACT.Identity,
+                        accum_out=dots[:, 8 * half_i + i : 8 * half_i + i + 1],
                     )
 
             def exponentials(b):
-                u = dense.tile([P, 2, 4 * TOKENS], F32, tag="u", bufs=3)
-                nc.vector.tensor_tensor(
-                    out=u[:],
-                    in0=sts[b][:].unsqueeze(1).to_broadcast([P, 2, 4 * TOKENS]),
-                    in1=bias_tab[:, :, 4 * b : 4 * b + 4, :].rearrange("p l h n -> p l (h n)"),
-                    op=ALU.add,
-                )
-                f = dense.tile([P, 2, 4 * TOKENS], F32, tag="f", bufs=3)
-                nc.scalar.activation(out=f[:], in_=u[:], func=ACT.Exp, bias=minus_one[:])
-                us[b] = u
+                u = dense.tile([P, 4, TOKENS], F32, tag="u", bufs=3)
+                nc.vector.tensor_tensor(out=u[:], in0=sts[b][:], in1=step_tab[:, 4 * b : 4 * b + 4, :], op=ALU.add)
+                f = dense.tile([P, 2, 4, TOKENS], F32, tag="f", bufs=3)
+                us[b] = (sts[b], u)
+                for layer in range(2):
+                    nc.scalar.activation(out=f[:, layer, :, :], in_=us[b][layer][:], func=ACT.Exp, bias=minus_one[:])
                 fs[b] = f
 
-            def weigh(half_i):
-                banks = (2 * half_i, 2 * half_i + 1)
-                for b in banks:
-                    f_flat = fs[b][:].rearrange("p l c -> p (l c)")
-                    nc.vector.scalar_tensor_tensor(
-                        out=f_flat, in0=us[b][:].rearrange("p l c -> p (l c)"), scalar=1.0, in1=f_flat, op0=ALU.max, op1=ALU.min
-                    )
-                for b in banks:
-                    nc.vector.tensor_tensor(
-                        out=fs[b][:],
-                        in0=fs[b][:],
-                        in1=gain_tab[:, :, 4 * b : 4 * b + 4, :].rearrange("p l h n -> p l (h n)"),
-                        op=ALU.mult,
-                    )
-                for b in banks:
-                    nc.vector.tensor_tensor(
-                        out=at_all[:, 4 * b : 4 * b + 4, :].rearrange("p h n -> p (h n)"),
-                        in0=fs[b][:, 0, :],
-                        in1=fs[b][:, 1, :],
-                        op=ALU.add,
-                    )
+            def clip(b):
+                for layer in range(2):
+                    f = fs[b][:, layer, :, :]
+                    nc.vector.scalar_tensor_tensor(out=f, in0=us[b][layer][:], scalar=1.0, in1=f, op0=ALU.max, op1=ALU.min)
 
-            def column_sums(half_i, sums_ps):
-                for i in range(8):
-                    nc.tensor.matmul(
-                        out=sums_ps[:, 8 + 4 * i : 12 + 4 * i], lhsT=at_all[:, 8 * half_i + i, :], rhs=class3[:], start=True, stop=True
-                    )
-
-            def same_token_terms(half_i, sums_ps):
-                heads = slice(8 * half_i, 8 * half_i + 8)
-                n_t = SCALES + 1
-                u = dense.tile([P, 8, n_t], F32, tag="u_diag")
+            def weigh(b):
                 nc.vector.tensor_tensor(
-                    out=u[:], in0=sums_ps[:, 0:8].unsqueeze(2).to_broadcast([P, 8, n_t]), in1=diag_bias[:, heads, :], op=ALU.add
-                )
-                f = dense.tile([P, 8, n_t], F32, tag="f_diag")
-                nc.scalar.activation(out=f[:], in_=u[:], func=ACT.Exp)
-                return u, f
-
-            def same_token_sum(half_i, u, f):
-                heads = slice(8 * half_i, 8 * half_i + 8)
-                nc.vector.tensor_scalar(out=u[:], in0=u[:], scalar1=0.0, scalar2=1.0, op0=ALU.max, op1=ALU.add)
-                nc.vector.tensor_tensor(out=f[:], in0=f[:], in1=u[:], op=ALU.min)
-                nc.vector.tensor_tensor(out=f[:], in0=f[:], in1=diag_gain[:, heads, :], op=ALU.mult)
-                nc.vector.tensor_reduce(out=w_diag[:, heads], in_=f[:], op=ALU.add, axis=AXIS_X)
-                nc.vector.tensor_tensor(out=z_all[:, heads], in0=w_diag[:, heads], in1=z_fixed[:, heads], op=ALU.add)
-
-            def normalise(half_i, sums_ps):
-                heads = slice(8 * half_i, 8 * half_i + 8)
-                signed = dense.tile([P, 8, 4], F32, tag="signed")
-                nc.vector.tensor_tensor(
-                    out=signed[:],
-                    in0=sums_ps[:, 8:40].rearrange("p (h c) -> p h c", c=4),
-                    in1=sign3[:].unsqueeze(1).to_broadcast([P, 8, 4]),
+                    out=fs[b][:].rearrange("p l h n -> p l (h n)"),
+                    in0=fs[b][:].rearrange("p l h n -> p l (h n)"),
+                    in1=gain_tab[:, :, 4 * b : 4 * b + 4, :].rearrange("p l h n -> p l (h n)"),
                     op=ALU.mult,
                 )
-                z_taps = dense.tile([P, 8], F32, tag="z_taps")
-                nc.vector.tensor_reduce(out=z_taps[:], in_=signed[:], op=ALU.add, axis=AXIS_X)
-                nc.vector.tensor_tensor(out=z_all[:, heads], in0=z_taps[:], in1=z_all[:, heads], op=ALU.add)
-                nc.vector.reciprocal(out=z_inv[:, heads], in_=z_all[:, heads])
 
-            def score_half(half_i, q_bank, k_bank):
-                banks = (2 * half_i, 2 * half_i + 1)
-                for b in banks:
-                    to_sbuf(b, q_bank, k_bank)
-                for b in banks:
-                    transposes(b)
-                for b in banks:
-                    add_bias(b)
-                for b in banks:
-                    plain_q(b)
+            def add_layers(b):
+                nc.vector.tensor_tensor(
+                    out=at_all[:, 4 * b : 4 * b + 4, :], in0=fs[b][:, 0, :, :], in1=fs[b][:, 1, :, :], op=ALU.add
+                )
 
-            k1 = accs.tile([P, BANK], F32, tag="acc")
-            v_banks = [accs.tile([P, BANK], F32, tag="acc", name="acc_v%d" % i) for i in range(2)]
+            n_t = SCALES + 1
+            u_diag = dense.tile([P, HEADS, n_t], F32, bufs=1)
+            f_diag = dense.tile([P, HEADS, n_t], F32, bufs=1)
 
-            score_half(0, q0, k0)
-            mx_passes(8, 10, [k1])
-            scores(0)
-            scores(1)
-            mx_passes(10, first_v_load, [k1])
-            exponentials(0)
-            exponentials(1)
-            same_token_products(0)
-            same_token_products(1)
-            score_half(1, q1, k1)
-            sums_ps0 = accs.tile([P, 40], F32, tag="acc")
-            same_token_dots(0, sums_ps0)
-            same_token_dots(1, sums_ps0)
-            weigh(0)
-            scores(2)
-            scores(3)
-            mx_passes(first_v_load, first_v_load + 4, v_banks)
-            u_diag0, f_diag0 = same_token_terms(0, sums_ps0)
-            exponentials(2)
-            exponentials(3)
-            same_token_products(2)
-            same_token_products(3)
-            column_sums(0, sums_ps0)
-            sums_ps1 = accs.tile([P, 40], F32, tag="acc")
-            same_token_dots(2, sums_ps1)
-            same_token_dots(3, sums_ps1)
-            same_token_sum(0, u_diag0, f_diag0)
-            weigh(1)
-            u_diag1, f_diag1 = same_token_terms(1, sums_ps1)
-            normalise(0, sums_ps0)
-            mx_passes(first_v_load + 4, len(w_loads), v_banks)
-            column_sums(1, sums_ps1)
+            def same_token_exp():
+                nc.vector.tensor_tensor(
+                    out=u_diag[:], in0=dots[:].unsqueeze(2).to_broadcast([P, HEADS, n_t]), in1=diag_bias[:], op=ALU.add
+                )
+                nc.scalar.activation(out=f_diag[:], in_=u_diag[:], func=ACT.Exp, bias=minus_one[:])
 
-            same_token_sum(1, u_diag1, f_diag1)
-            v_sb = dense.tile([P, HEADS, HEAD_DIM], F32, bufs=1)
+            def same_token_clip():
+                nc.vector.scalar_tensor_tensor(
+                    out=f_diag[:], in0=u_diag[:], scalar=1.0, in1=f_diag[:], op0=ALU.max, op1=ALU.min
+                )
+
+            def same_token_weigh():
+                nc.vector.tensor_tensor(out=f_diag[:], in0=f_diag[:], in1=diag_gain[:], op=ALU.mult)
+
+            def same_token_sum():
+                nc.vector.tensor_reduce(out=w_diag[:], in_=f_diag[:], op=ALU.add, axis=AXIS_X)
+
+            def same_token_z():
+                nc.vector.tensor_tensor(out=z_parts[:, :, 3], in0=w_diag[:], in1=z_fixed[:], op=ALU.add)
+
             v_diag = dense.tile([P, HEADS, HEAD_DIM], F32, bufs=1)
             o_sb = dense.tile([P, HEADS, HEAD_DIM], F32, bufs=1)
+            z_sum = dense.tile([P, HEADS], F32, bufs=1)
             out_rows = out.rearrange("o n e -> (o n) e")
-            for i, bank in enumerate(v_banks):
+            o_pss = {}
+
+            def of_bank(b):
+                return slice(4 * b, 4 * b + 4)
+
+            def biased_v(b, v_bank):
+                cols = slice(4 * HEAD_DIM * (b % 2), 4 * HEAD_DIM * (b % 2 + 1))
                 nc.vector.tensor_tensor(
-                    out=v_sb[:, 8 * i : 8 * i + 8, :].rearrange("p h d -> p (h d)"),
-                    in0=bank[:],
-                    in1=bias_v[:, BANK * i : BANK * (i + 1)],
+                    out=v_sb[:, of_bank(b), 0:HEAD_DIM],
+                    in0=v_bank[:, cols].rearrange("p (h d) -> p h d", d=HEAD_DIM),
+                    in1=bias_all[:, 2 * EMB :].rearrange("p (h d) -> p h d", d=HEAD_DIM)[:, of_bank(b), :],
                     op=ALU.add,
                 )
-            o_pss = []
-            for b in range(4):
-                o_ps = work.tile([P, 4, HEAD_DIM], F32, tag="work")
+
+            def weighted_sums(b):
+                o_ps = work.tile([P, 4, HEAD_DIM + 4], F32, tag="work")
                 for i in range(4):
                     h = 4 * b + i
                     nc.tensor.matmul(out=o_ps[:, i, :], lhsT=at_all[:, h, :], rhs=v_sb[:, h, :], start=True, stop=True)
-                o_pss.append(o_ps)
-            normalise(1, sums_ps1)
-            nc.vector.tensor_tensor(out=w_diag[:], in0=w_diag[:], in1=z_inv[:], op=ALU.mult)
-            nc.vector.tensor_tensor(
-                out=v_diag[:], in0=v_sb[:], in1=w_diag[:].unsqueeze(2).to_broadcast([P, HEADS, HEAD_DIM]), op=ALU.mult
-            )
-            for b in range(4):
-                for i in range(4):
-                    h = 4 * b + i
-                    nc.vector.scalar_tensor_tensor(
-                        out=o_sb[:, h, :],
-                        in0=o_pss[b][:, i, :],
-                        scalar=z_inv[:, h : h + 1],
-                        in1=v_diag[:, h, :],
-                        op0=ALU.mult,
-                        op1=ALU.add,
-                    )
-                if b % 2 == 1:
-                    cols = slice(BANK * (b // 2), BANK * (b // 2 + 1))
-                    nc.sync.dma_start(out=out_rows[:, cols], in_=o_sb[:].rearrange("p h d -> p (h d)")[:, cols])
+                o_pss[b] = o_ps
+
+            def same_token_v(b):
+                nc.vector.tensor_tensor(
+                    out=v_diag[:, of_bank(b), :],
+                    in0=v_sb[:, of_bank(b), 0:HEAD_DIM],
+                    in1=w_diag[:, of_bank(b)].unsqueeze(2).to_broadcast([P, 4, HEAD_DIM]),
+                    op=ALU.mult,
+                )
+
+            def signed_sums(b):
+                nc.vector.tensor_tensor(
+                    out=z_parts[:, of_bank(b), 0:3],
+                    in0=o_pss[b][:, :, HEAD_DIM : HEAD_DIM + 3],
+                    in1=sign3[:, 0:3].unsqueeze(1).to_broadcast([P, 4, 3]),
+                    op=ALU.mult,
+                )
+
+            def numerator(b):
+                nc.vector.tensor_tensor(
+                    out=v_diag[:, of_bank(b), :], in0=o_pss[b][:, :, 0:HEAD_DIM], in1=v_diag[:, of_bank(b), :], op=ALU.add
+                )
+
+            def sum_z(b):
+                nc.vector.tensor_reduce(out=z_sum[:, of_bank(b)], in_=z_parts[:, of_bank(b), :], op=ALU.add, axis=AXIS_X)
+
+            def invert_z(b):
+                nc.vector.reciprocal(out=z_inv[:, of_bank(b)], in_=z_sum[:, of_bank(b)])
+
+            def quotient(b):
+                nc.vector.tensor_tensor(
+                    out=o_sb[:, of_bank(b), :],
+                    in0=v_diag[:, of_bank(b), :],
+                    in1=z_inv[:, of_bank(b)].unsqueeze(2).to_broadcast([P, 4, HEAD_DIM]),
+                    op=ALU.mult,
+                )
+
+            def store(half_i):
+                cols = slice(BANK * half_i, BANK * (half_i + 1))
+                nc.sync.dma_start(out=out_rows[:, cols], in_=o_sb[:].rearrange("p h d -> p (h d)")[:, cols])
+
+            v0 = accs.tile([P, BANK], F32, tag="acc")
+            v1 = accs.tile([P, BANK], F32, tag="acc")
+            v_banks = [v0, v1]
+
+            mx_passes(q0_load, q0_load + 1, [q0])
+            to_sbuf(("q", 0), q0, 0)
+            transposes(("q", 0))
+            split_q(0)
+            split_q(1)
+            mx_passes(q0_load + 1, q0_load + 2, [k0])
+            to_sbuf(("k", 0), k0, EMB)
+            transposes(("k", 0))
+            plain_k(0, nc.vector.tensor_copy)
+            same_token_products(0)
+            scores(0)
+            scores(1)
+            mx_passes(q0_load + 2, k1_load, [q1])
+            exponentials(0)
+            exponentials(1)
+            to_sbuf(("q", 1), q1, BANK)
+            mx_passes(k1_load, v_load - 2, [k1])
+            transposes(("q", 1))
+            split_q(2)
+            split_q(3)
+            same_token_dots(0)
+            mx_passes(v_load - 2, v_load, [k1])
+            clip(0)
+            clip(1)
+            weigh(0)
+            to_sbuf(("k", 1), k1, EMB + BANK)
+            weigh(1)
+            transposes(("k", 1))
+            plain_k(1, nc.scalar.copy)
+            add_layers(0)
+            add_layers(1)
+            same_token_products(1)
+            scores(2)
+            scores(3)
+            mx_passes(v_load, v_load + 2, v_banks)
+            exponentials(2)
+            exponentials(3)
+            same_token_dots(1)
+            mx_passes(v_load + 2, v0_load, v_banks)
+            clip(2)
+            clip(3)
+            same_token_exp()
+            weigh(2)
+            weigh(3)
+            same_token_clip()
+            add_layers(2)
+            same_token_weigh()
+            add_layers(3)
+            same_token_sum()
+            mx_passes(v0_load, v1_load, [v0])
+            biased_v(0, v0)
+            same_token_z()
+            biased_v(1, v0)
+            weighted_sums(0)
+            weighted_sums(1)
+            same_token_v(0)
+            same_token_v(1)
+            mx_passes(v1_load, v1_load + 2, [v1])
+            signed_sums(0)
+            numerator(0)
+            signed_sums(1)
+            sum_z(0)
+            numerator(1)
+            invert_z(0)
+            sum_z(1)
+            quotient(0)
+            invert_z(1)
+            quotient(1)
+            store(0)
+            mx_passes(v1_load + 2, v1_load + 3, [v1])
+            biased_v(2, v1)
+            biased_v(3, v1)
+            weighted_sums(2)
+            weighted_sums(3)
+            same_token_v(2)
+            same_token_v(3)
+            signed_sums(2)
+            numerator(2)
+            sum_z(2)
+            signed_sums(3)
+            invert_z(2)
+            numerator(3)
+            sum_z(3)
+            quotient(2)
+            invert_z(3)
+            quotient(3)
+            store(1)

@@ -96,13 +96,14 @@ def tile_dwarfattention_pa_k_kernel(
         w_loads += [(g0, 4, 3 * BANK, BANK) for g0 in range(wide, head, 4)]
         w_loads += [(g0, 2, 3 * BANK, BANK) for g0 in range(head, PASSES, 2)]
         v_load = len(w_loads)
-        half_v = PASSES - 8
+        half_v = 8
         w_loads += [(g0, 2, 2 * EMB, 2 * BANK) for g0 in range(0, half_v, 2)]
         v0_load = len(w_loads)
-        w_loads += [(g0, 4, 2 * EMB, BANK) for g0 in range(half_v, PASSES, 4)]
+        w_loads += [(g0, min(4, PASSES - g0), 2 * EMB, BANK) for g0 in range(half_v, PASSES, 4)]
         v1_load = len(w_loads)
-        w_loads += [(half_v, 4, 2 * EMB + BANK, BANK)]
-        w_loads += [(g0, 2, 2 * EMB + BANK, BANK) for g0 in range(half_v + 4, PASSES, 2)]
+        w_loads += [(g0, 2, 2 * EMB + BANK, BANK) for g0 in range(half_v, PASSES - 2, 2)]
+        v2_load = len(w_loads)
+        w_loads += [(PASSES - 2, 2, 2 * EMB + BANK + i * BANK // 2, BANK // 2) for i in (1, 0)]
         w_tiles = []
 
         def load_weights_up_to(n):
@@ -116,18 +117,19 @@ def tile_dwarfattention_pa_k_kernel(
                 g0, n_g, col0, n_cols = w_loads[t]
                 for gi in range(n_g):
                     g = g0 + gi
-                    for i, bank in enumerate(banks):
+                    col = 0
+                    for bank in banks:
+                        cols = slice(col, col + bank.shape[1])
                         nc.tensor.matmul_mx(
                             out=bank[:],
                             lhsT=x_codes[:, TOKENS * g : TOKENS * (g + 1)].bitcast(FP8X4),
                             lhsT_scale=x_scales[:, TOKENS * g : TOKENS * (g + 1)],
-                            rhs=w_tiles[t][:, gi, BANK * i : BANK * (i + 1)].bitcast(FP8X4),
-                            rhs_scale=w_planes[
-                                4 * (g % PLANES) : P, g // PLANES, col0 + BANK * i : col0 + BANK * (i + 1)
-                            ],
+                            rhs=w_tiles[t][:, gi, cols].bitcast(FP8X4),
+                            rhs_scale=w_planes[4 * (g % PLANES) : P, g // PLANES, col0 + cols.start : col0 + cols.stop],
                             start=(g == 0),
                             stop=(g == PASSES - 1),
                         )
+                        col = cols.stop
                 load_weights_up_to(t + 1 + W_BUFS)
 
         def elu_plus_one(dst, u, tmp):
@@ -373,15 +375,19 @@ def tile_dwarfattention_pa_k_kernel(
                 nc.vector.tensor_scalar_add(out=z_fixed[:], in0=gf_sum[:], scalar1=EPS)
 
             q0, q1, k0, k1 = [accs.tile([P, BANK], F32, tag="acc", name="acc_%s" % n) for n in ("q0", "q1", "k0", "k1")]
+            def qk_passes(first, last):
+                mx_passes(first, min(last, qk_load), [q0, q1, k0, k1])
+                mx_passes(max(first, qk_load), last, [q0, q1, k0])
+
             for t in range(4):
-                mx_passes(t, t + 1, [q0, q1, k0, k1])
+                qk_passes(t, t + 1)
                 table_quarter(t)
-            mx_passes(qk_load, qk_load + 1, [q0, q1, k0])
+            qk_passes(4, 5)
             transpose_gains()
             small_tables()
-            mx_passes(qk_load + 1, qk_load + 2, [q0, q1, k0])
+            qk_passes(5, 6)
             spread_b_qkv(0, 6)
-            mx_passes(qk_load + 2, q0_load, [q0, q1, k0])
+            qk_passes(6, q0_load)
         with tc.tile_pool(name="dense", bufs=2) as dense:
             pairs = range(4)
             toks, trs, k_ts, prods = {}, {}, {}, {}
@@ -474,26 +480,36 @@ def tile_dwarfattention_pa_k_kernel(
             n_t = SCALES + 1
             u_diag = dense.tile([P, HEADS, n_t], F32, bufs=1)
             f_diag = dense.tile([P, HEADS, n_t], F32, bufs=1)
+            halves = [slice(0, 8), slice(8, 16)]
 
-            def same_token_exp():
+            def same_token_exp(half_i):
+                heads = halves[half_i]
                 nc.vector.tensor_tensor(
-                    out=u_diag[:], in0=dots[:].unsqueeze(2).to_broadcast([P, HEADS, n_t]), in1=diag_bias[:], op=ALU.add
+                    out=u_diag[:, heads, :],
+                    in0=dots[:, heads].unsqueeze(2).to_broadcast([P, 8, n_t]),
+                    in1=diag_bias[:, heads, :],
+                    op=ALU.add,
                 )
-                nc.scalar.activation(out=f_diag[:], in_=u_diag[:], func=ACT.Exp, bias=minus_one[:])
+                nc.scalar.activation(out=f_diag[:, heads, :], in_=u_diag[:, heads, :], func=ACT.Exp, bias=minus_one[:])
 
-            def same_token_clip():
+            def same_token_clip(half_i):
+                f = f_diag[:, halves[half_i], :]
                 nc.vector.scalar_tensor_tensor(
-                    out=f_diag[:], in0=u_diag[:], scalar=1.0, in1=f_diag[:], op0=ALU.max, op1=ALU.min
+                    out=f, in0=u_diag[:, halves[half_i], :], scalar=1.0, in1=f, op0=ALU.max, op1=ALU.min
                 )
 
-            def same_token_weigh():
-                nc.vector.tensor_tensor(out=f_diag[:], in0=f_diag[:], in1=diag_gain[:], op=ALU.mult)
+            def same_token_weigh(half_i):
+                f = f_diag[:, halves[half_i], :]
+                nc.vector.tensor_tensor(out=f, in0=f, in1=diag_gain[:, halves[half_i], :], op=ALU.mult)
 
-            def same_token_sum():
-                nc.vector.tensor_reduce(out=w_diag[:], in_=f_diag[:], op=ALU.add, axis=AXIS_X)
+            def same_token_sum(half_i):
+                nc.vector.tensor_reduce(
+                    out=w_diag[:, halves[half_i]], in_=f_diag[:, halves[half_i], :], op=ALU.add, axis=AXIS_X
+                )
 
-            def same_token_z():
-                nc.vector.tensor_tensor(out=z_parts[:, :, 3], in0=w_diag[:], in1=z_fixed[:], op=ALU.add)
+            def same_token_z(half_i):
+                heads = halves[half_i]
+                nc.vector.tensor_tensor(out=z_parts[:, heads, 3], in0=w_diag[:, heads], in1=z_fixed[:, heads], op=ALU.add)
 
             v_diag = dense.tile([P, HEADS, HEAD_DIM], F32, bufs=1)
             o_sb = dense.tile([P, HEADS, HEAD_DIM], F32, bufs=1)
@@ -504,11 +520,10 @@ def tile_dwarfattention_pa_k_kernel(
             def of_bank(b):
                 return slice(4 * b, 4 * b + 4)
 
-            def biased_v(b, v_bank):
-                cols = slice(4 * HEAD_DIM * (b % 2), 4 * HEAD_DIM * (b % 2 + 1))
+            def biased_v(b):
                 nc.vector.tensor_tensor(
                     out=v_sb[:, of_bank(b), 0:HEAD_DIM],
-                    in0=v_bank[:, cols].rearrange("p (h d) -> p h d", d=HEAD_DIM),
+                    in0=v_of_bank[b].rearrange("p (h d) -> p h d", d=HEAD_DIM),
                     in1=bias_all[:, 2 * EMB :].rearrange("p (h d) -> p h d", d=HEAD_DIM)[:, of_bank(b), :],
                     op=ALU.add,
                 )
@@ -528,13 +543,20 @@ def tile_dwarfattention_pa_k_kernel(
                     op=ALU.mult,
                 )
 
-            def signed_sums(b):
+            def signed_sums(b, sums):
                 nc.vector.tensor_tensor(
                     out=z_parts[:, of_bank(b), 0:3],
-                    in0=o_pss[b][:, :, HEAD_DIM : HEAD_DIM + 3],
+                    in0=sums,
                     in1=sign3[:, 0:3].unsqueeze(1).to_broadcast([P, 4, 3]),
                     op=ALU.mult,
                 )
+
+            def class_sums(b):
+                signed_sums(b, o_pss[b][:, :, HEAD_DIM : HEAD_DIM + 3])
+
+            def column_sums():
+                for i in range(4):
+                    nc.tensor.matmul(out=sums_ps[:, i, :], lhsT=at_all[:, 8 + i, :], rhs=class3[:], start=True, stop=True)
 
             def numerator(b):
                 nc.vector.tensor_tensor(
@@ -555,13 +577,30 @@ def tile_dwarfattention_pa_k_kernel(
                     op=ALU.mult,
                 )
 
-            def store(half_i):
-                cols = slice(BANK * half_i, BANK * (half_i + 1))
+            def scale_w(b):
+                nc.vector.tensor_tensor(out=w_diag[:, of_bank(b)], in0=w_diag[:, of_bank(b)], in1=z_inv[:, of_bank(b)], op=ALU.mult)
+
+            def finish(b, first, last):
+                for i in range(first, last):
+                    h = 4 * b + i
+                    nc.vector.scalar_tensor_tensor(
+                        out=o_sb[:, h, :],
+                        in0=o_pss[b][:, i, 0:HEAD_DIM],
+                        scalar=z_inv[:, h : h + 1],
+                        in1=v_diag[:, h, :],
+                        op0=ALU.mult,
+                        op1=ALU.add,
+                    )
+
+            def store(first, last):
+                cols = slice(4 * HEAD_DIM * first, 4 * HEAD_DIM * (last + 1))
                 nc.sync.dma_start(out=out_rows[:, cols], in_=o_sb[:].rearrange("p h d -> p (h d)")[:, cols])
 
             v0 = accs.tile([P, BANK], F32, tag="acc")
-            v1 = accs.tile([P, BANK], F32, tag="acc")
-            v_banks = [v0, v1]
+            v2, v3 = [accs.tile([P, BANK // 2], F32, tag="acc", name="acc_v%d" % b) for b in (2, 3)]
+            sums_ps = accs.tile([P, 4, 4], F32, tag="acc")
+            v_banks = [v0, v2, v3]
+            v_of_bank = [v0[:, 0 : BANK // 2], v0[:, BANK // 2 :], v2[:], v3[:]]
 
             mx_passes(q0_load, q0_load + 1, [q0])
             to_sbuf(("q", 0), q0, 0)
@@ -571,82 +610,93 @@ def tile_dwarfattention_pa_k_kernel(
             mx_passes(q0_load + 1, q0_load + 2, [k0])
             to_sbuf(("k", 0), k0, EMB)
             transposes(("k", 0))
-            plain_k(0, nc.vector.tensor_copy)
+            plain_k(0, nc.scalar.copy)
             same_token_products(0)
+            mx_passes(q0_load + 2, k1_load, [q1])
             scores(0)
             scores(1)
-            mx_passes(q0_load + 2, k1_load, [q1])
-            exponentials(0)
-            exponentials(1)
             to_sbuf(("q", 1), q1, BANK)
+            same_token_dots(0)
+            exponentials(0)
+            same_token_exp(0)
+            exponentials(1)
             mx_passes(k1_load, v_load - 2, [k1])
             transposes(("q", 1))
             split_q(2)
             split_q(3)
-            same_token_dots(0)
             mx_passes(v_load - 2, v_load, [k1])
             clip(0)
+            same_token_clip(0)
             clip(1)
+            same_token_weigh(0)
             weigh(0)
             to_sbuf(("k", 1), k1, EMB + BANK)
             weigh(1)
+            same_token_sum(0)
+            same_token_products(1)
             transposes(("k", 1))
             plain_k(1, nc.scalar.copy)
             add_layers(0)
+            same_token_z(0)
             add_layers(1)
-            same_token_products(1)
             scores(2)
             scores(3)
             mx_passes(v_load, v_load + 2, v_banks)
+            same_token_dots(1)
             exponentials(2)
             exponentials(3)
-            same_token_dots(1)
+            same_token_exp(1)
             mx_passes(v_load + 2, v0_load, v_banks)
             clip(2)
+            same_token_clip(1)
             clip(3)
-            same_token_exp()
             weigh(2)
-            weigh(3)
-            same_token_clip()
+            same_token_weigh(1)
             add_layers(2)
-            same_token_weigh()
+            mx_passes(v0_load, v1_load - 1, [v0])
+            column_sums()
+            same_token_sum(1)
+            weigh(3)
+            signed_sums(2, sums_ps[:, :, 0:3])
+            same_token_z(1)
             add_layers(3)
-            same_token_sum()
-            mx_passes(v0_load, v1_load, [v0])
-            biased_v(0, v0)
-            same_token_z()
-            biased_v(1, v0)
+            sum_z(2)
+            mx_passes(v1_load - 1, v1_load, [v0])
+            invert_z(2)
+            biased_v(0)
+            scale_w(2)
+            biased_v(1)
+            mx_passes(v1_load, v1_load + 1, [v2, v3])
             weighted_sums(0)
-            weighted_sums(1)
             same_token_v(0)
             same_token_v(1)
-            mx_passes(v1_load, v1_load + 2, [v1])
-            signed_sums(0)
+            mx_passes(v1_load + 1, v1_load + 2, [v2, v3])
+            weighted_sums(1)
+            class_sums(0)
             numerator(0)
-            signed_sums(1)
             sum_z(0)
-            numerator(1)
             invert_z(0)
+            mx_passes(v1_load + 2, v2_load, [v2, v3])
+            mx_passes(v2_load, v2_load + 1, [v3])
+            mx_passes(v2_load + 1, v2_load + 2, [v2])
+            class_sums(1)
+            numerator(1)
             sum_z(1)
-            quotient(0)
-            invert_z(1)
-            quotient(1)
-            store(0)
-            mx_passes(v1_load + 2, v1_load + 3, [v1])
-            biased_v(2, v1)
-            biased_v(3, v1)
-            weighted_sums(2)
+            biased_v(3)
+            biased_v(2)
             weighted_sums(3)
-            same_token_v(2)
+            weighted_sums(2)
+            invert_z(1)
+            quotient(0)
+            quotient(1)
+            store(0, 1)
             same_token_v(3)
-            signed_sums(2)
-            numerator(2)
-            sum_z(2)
-            signed_sums(3)
-            invert_z(2)
+            same_token_v(2)
+            class_sums(3)
             numerator(3)
             sum_z(3)
-            quotient(2)
+            finish(2, 0, 2)
             invert_z(3)
+            finish(2, 2, 4)
             quotient(3)
-            store(1)
+            store(2, 3)

@@ -71,6 +71,7 @@ def tile_dwarfattention_pa_k_kernel(
         q_split = [keep.tile([P, 4, 2, TOKENS], F32, name="q_split%d" % i) for i in range(2)]
         base_tab = keep.tile([P, HEADS, TOKENS], BF16)
         step_tab = keep.tile([P, HEADS, TOKENS], F32)
+        k_bias = keep.tile([P, 2], F32)
         add_base = keep.tile([P, P], BF16)
         gain_tab = keep.tile([P, 2, HEADS, TOKENS], F32)
         tap_coef = keep.tile([P, TOKENS], F32)
@@ -86,17 +87,19 @@ def tile_dwarfattention_pa_k_kernel(
         z_inv = keep.tile([P, HEADS], F32)
 
         w_words = W_qkv_words.rearrange("g p n t -> p g (n t)").bitcast(I32)
-        wide, head = 4, PASSES - 4
-        w_loads = [(g0, 1, 0, 4 * BANK) for g0 in range(wide)]
-        qk_load = len(w_loads)
-        w_loads += [(g0, 2, 0, 3 * BANK) for g0 in range(wide, head, 2)]
+        head = PASSES - 4
+        w_loads = [(g0, 2, 0, 3 * BANK) for g0 in range(0, head, 2)]
         q0_load = len(w_loads)
-        w_loads += [(head, 4, col0, BANK) for col0 in (0, EMB, BANK)]
+        w_loads += [(g0, 4, 0, BANK) for g0 in range(head, PASSES, 4)]
+        k0_load = len(w_loads)
+        w_loads += [(g0, 4, EMB, BANK) for g0 in range(head, PASSES, 4)]
+        q1_load = len(w_loads)
+        w_loads += [(g0, 4, BANK, BANK) for g0 in range(head, PASSES, 4)]
         k1_load = len(w_loads)
-        w_loads += [(g0, 4, 3 * BANK, BANK) for g0 in range(wide, head, 4)]
-        w_loads += [(g0, 2, 3 * BANK, BANK) for g0 in range(head, PASSES, 2)]
+        w_loads += [(g0, 4, 3 * BANK, BANK) for g0 in range(0, PASSES - 4, 4)]
+        w_loads += [(g0, 2, 3 * BANK, BANK) for g0 in range(PASSES - 4, PASSES, 2)]
         v_load = len(w_loads)
-        half_v = 8
+        half_v = 6
         w_loads += [(g0, 2, 2 * EMB, 2 * BANK) for g0 in range(0, half_v, 2)]
         v0_load = len(w_loads)
         w_loads += [(g0, min(4, PASSES - g0), 2 * EMB, BANK) for g0 in range(half_v, PASSES, 4)]
@@ -130,6 +133,29 @@ def tile_dwarfattention_pa_k_kernel(
                             stop=(g == PASSES - 1),
                         )
                         col = cols.stop
+                load_weights_up_to(t + 1 + W_BUFS)
+
+        def k1_passes(first, last):
+            for t in range(first, last):
+                g0, n_g, col0, n_cols = w_loads[t]
+                for gi in range(n_g):
+                    g = g0 + gi
+                    x_g = slice(TOKENS * g, TOKENS * (g + 1))
+                    planes = w_planes[4 * (g % PLANES) : P, g // PLANES, col0 : col0 + BANK]
+                    for i, acc in enumerate(k1_pairs + [k1_rest]):
+                        x_side = (x_codes[:, x_g].bitcast(FP8X4), x_scales[:, x_g])
+                        cols = slice(P * i, P * i + acc.shape[1])
+                        w_side = (w_tiles[t][:, gi, cols].bitcast(FP8X4), planes[:, cols])
+                        stationary, moving = (x_side, w_side) if acc is k1_rest else (w_side, x_side)
+                        nc.tensor.matmul_mx(
+                            out=acc[:],
+                            lhsT=stationary[0],
+                            lhsT_scale=stationary[1],
+                            rhs=moving[0],
+                            rhs_scale=moving[1],
+                            start=(g == 0),
+                            stop=(g == PASSES - 1),
+                        )
                 load_weights_up_to(t + 1 + W_BUFS)
 
         def elu_plus_one(dst, u, tmp):
@@ -353,6 +379,8 @@ def tile_dwarfattention_pa_k_kernel(
                 nc.vector.tensor_scalar_mul(out=diag_gain[:, :, 0:SCALES], in0=gains_nt[:], scalar1=D4[0])
                 nc.vector.memset(diag_bias[:, :, SCALES], 1.0)
                 nc.vector.tensor_scalar_add(out=diag_bias[:, :, 0:SCALES], in0=pb_by_tau[:, 0, :, :], scalar1=1.0)
+                nc.vector.memset(diag_bias[:, 8:12, SCALES], 0.0)
+                nc.vector.tensor_copy(out=diag_bias[:, 8:12, 0:SCALES], in_=pb_by_tau[:, 0, 8:12, :])
 
                 n_f = TAPS * 8 * HEADS
                 f_of_bias = setup.tile([P, n_f], F32)
@@ -374,41 +402,51 @@ def tile_dwarfattention_pa_k_kernel(
                 nc.vector.tensor_reduce(out=gf_sum[:], in_=gf[:].rearrange("p h t j -> p h (t j)"), op=ALU.add, axis=AXIS_X)
                 nc.vector.tensor_scalar_add(out=z_fixed[:], in0=gf_sum[:], scalar1=EPS)
 
-            q0, q1, k0, k1 = [accs.tile([P, BANK], F32, tag="acc", name="acc_%s" % n) for n in ("q0", "q1", "k0", "k1")]
-            def qk_passes(first, last):
-                mx_passes(first, min(last, qk_load), [q0, q1, k0, k1])
-                mx_passes(max(first, qk_load), last, [q0, q1, k0])
-
+            q0, k0, q1 = [accs.tile([P, BANK], F32, tag="acc", name="acc_%s" % n) for n in ("q0", "k0", "q1")]
             for t in range(4):
-                qk_passes(t, t + 1)
+                mx_passes(t, t + 1, [q0, q1, k0])
                 table_quarter(t)
-            qk_passes(4, 5)
             transpose_gains()
             small_tables()
-            qk_passes(5, 6)
+            mx_passes(4, 5, [q0, q1, k0])
             spread_b_qkv(0, 6)
-            qk_passes(6, q0_load)
+            ps = work.tile([P, 2, 2], F32, tag="work")
+            for pair in range(2):
+                cols = slice(EMB + BANK + P * pair, EMB + BANK + P * (pair + 1))
+                nc.tensor.matmul(out=ps[:, pair, :], lhsT=bias_all[:, cols], rhs=ident_b[:, 0:2], start=True, stop=True)
+            nc.vector.tensor_copy(out=k_bias[:], in_=ps[:, :, 0])
+            mx_passes(5, q0_load, [q0, q1, k0])
         with tc.tile_pool(name="dense", bufs=2) as dense:
-            pairs = range(4)
             toks, trs, k_ts, prods = {}, {}, {}, {}
             sts, us, fs = {}, {}, {}
 
             def to_sbuf(key, bank, col0):
-                tok = dense.tile([P, BANK], F32, tag="tok", bufs=4)
-                nc.vector.tensor_tensor(out=tok[:], in0=bank[:], in1=bias_all[:, col0 : col0 + BANK], op=ALU.add)
+                width = bank.shape[1]
+                tok = dense.tile([P, width], F32, tag="tok", bufs=4)
+                nc.vector.tensor_tensor(out=tok[:], in0=bank[:], in1=bias_all[:, col0 : col0 + width], op=ALU.add)
                 toks[key] = tok
 
             def transposes(key):
-                tr = work.tile([P, 4, TOKENS], F32, tag="work")
-                for pair in pairs:
+                n_pairs = toks[key].shape[1] // P
+                tr = work.tile([P, n_pairs, TOKENS], F32, tag="work")
+                for pair in range(n_pairs):
                     nc.tensor.transpose(tr[:, pair, :], toks[key][:, P * pair : P * (pair + 1)], ident_f[:])
                 trs[key] = tr
 
-            def plain_k(half_i, copy):
+            for half_i in range(2):
                 k_t = dense.tile([P, 4, TOKENS], F32, tag="k_t")
-                for two in (slice(0, 2), slice(2, 4)):
-                    copy(out=k_t[:, two, :], in_=trs["k", half_i][:, two, :])
                 k_ts[half_i] = k_t
+
+            def plain_k(half_i, first):
+                tr = trs["k", half_i]
+                for i in range(0, tr.shape[1], 2):
+                    nc.scalar.copy(out=k_ts[half_i][:, first + i : first + i + 2, :], in_=tr[:, i : i + 2, :])
+
+            def biased_k():
+                for pair in range(2):
+                    nc.scalar.activation(
+                        out=k_ts[1][:, pair, :], in_=k1_pairs[pair][:], func=ACT.Identity, bias=k_bias[:, pair : pair + 1]
+                    )
 
             def split_q(b):
                 two = slice(2 * (b % 2), 2 * (b % 2) + 2)
@@ -435,19 +473,27 @@ def tile_dwarfattention_pa_k_kernel(
 
             dots = dense.tile([P, HEADS], F32, bufs=1)
 
-            def same_token_products(half_i):
-                prod = dense.tile([P, BANK], F32, tag="prod")
-                nc.vector.tensor_tensor(out=prod[:], in0=toks["q", half_i][:], in1=toks["k", half_i][:], op=ALU.mult)
-                prods[half_i] = prod
+            def same_token_products(key, first):
+                k_tok = toks["k", key]
+                width = k_tok.shape[1]
+                prod = dense.tile([P, width], F32, tag="prod")
+                nc.vector.tensor_tensor(out=prod[:], in0=toks["q", key][:, BANK - width :], in1=k_tok[:], op=ALU.mult)
+                prods[first] = prod[:].rearrange("p (h d) -> p h d", d=HEAD_DIM)
 
-            def same_token_dots(half_i):
-                for i in range(8):
-                    cols = slice(HEAD_DIM * i, HEAD_DIM * (i + 1))
+            def same_token_diagonal(b):
+                prod = dense.tile([P, 4, TOKENS], F32, tag="diagonal")
+                nc.vector.tensor_tensor(
+                    out=prod[:], in0=sts[b][:], in1=ident_f[:].unsqueeze(1).to_broadcast([P, 4, TOKENS]), op=ALU.mult
+                )
+                prods[4 * b] = prod
+
+            def same_token_dots(first):
+                for i in range(prods[first].shape[1]):
                     nc.scalar.activation(
-                        out=prods[half_i][:, cols],
-                        in_=prods[half_i][:, cols],
+                        out=prods[first][:, i, :],
+                        in_=prods[first][:, i, :],
                         func=ACT.Identity,
-                        accum_out=dots[:, 8 * half_i + i : 8 * half_i + i + 1],
+                        accum_out=dots[:, first + i : first + i + 1],
                     )
 
             def exponentials(b):
@@ -543,31 +589,31 @@ def tile_dwarfattention_pa_k_kernel(
                     op=ALU.mult,
                 )
 
-            def signed_sums(b, sums):
+            def signed_sums(heads, sums):
                 nc.vector.tensor_tensor(
-                    out=z_parts[:, of_bank(b), 0:3],
+                    out=z_parts[:, heads, 0:3],
                     in0=sums,
-                    in1=sign3[:, 0:3].unsqueeze(1).to_broadcast([P, 4, 3]),
+                    in1=sign3[:, 0:3].unsqueeze(1).to_broadcast([P, heads.stop - heads.start, 3]),
                     op=ALU.mult,
                 )
 
             def class_sums(b):
-                signed_sums(b, o_pss[b][:, :, HEAD_DIM : HEAD_DIM + 3])
+                signed_sums(of_bank(b), o_pss[b][:, :, HEAD_DIM : HEAD_DIM + 3])
 
-            def column_sums():
-                for i in range(4):
-                    nc.tensor.matmul(out=sums_ps[:, i, :], lhsT=at_all[:, 8 + i, :], rhs=class3[:], start=True, stop=True)
+            def column_sums(b):
+                for h in range(4 * b, 4 * b + 4):
+                    nc.tensor.matmul(out=sums_ps[:, h - 8, :], lhsT=at_all[:, h, :], rhs=class3[:], start=True, stop=True)
 
             def numerator(b):
                 nc.vector.tensor_tensor(
                     out=v_diag[:, of_bank(b), :], in0=o_pss[b][:, :, 0:HEAD_DIM], in1=v_diag[:, of_bank(b), :], op=ALU.add
                 )
 
-            def sum_z(b):
-                nc.vector.tensor_reduce(out=z_sum[:, of_bank(b)], in_=z_parts[:, of_bank(b), :], op=ALU.add, axis=AXIS_X)
+            def sum_z(heads):
+                nc.vector.tensor_reduce(out=z_sum[:, heads], in_=z_parts[:, heads, :], op=ALU.add, axis=AXIS_X)
 
-            def invert_z(b):
-                nc.vector.reciprocal(out=z_inv[:, of_bank(b)], in_=z_sum[:, of_bank(b)])
+            def invert_z(heads):
+                nc.vector.reciprocal(out=z_inv[:, heads], in_=z_sum[:, heads])
 
             def quotient(b):
                 nc.vector.tensor_tensor(
@@ -577,11 +623,11 @@ def tile_dwarfattention_pa_k_kernel(
                     op=ALU.mult,
                 )
 
-            def scale_w(b):
-                nc.vector.tensor_tensor(out=w_diag[:, of_bank(b)], in0=w_diag[:, of_bank(b)], in1=z_inv[:, of_bank(b)], op=ALU.mult)
+            def scale_w(heads):
+                nc.vector.tensor_tensor(out=w_diag[:, heads], in0=w_diag[:, heads], in1=z_inv[:, heads], op=ALU.mult)
 
-            def finish(b, first, last):
-                for i in range(first, last):
+            def finish(b):
+                for i in range(4):
                     h = 4 * b + i
                     nc.vector.scalar_tensor_tensor(
                         out=o_sb[:, h, :],
@@ -596,23 +642,25 @@ def tile_dwarfattention_pa_k_kernel(
                 cols = slice(4 * HEAD_DIM * first, 4 * HEAD_DIM * (last + 1))
                 nc.sync.dma_start(out=out_rows[:, cols], in_=o_sb[:].rearrange("p h d -> p (h d)")[:, cols])
 
+            k1_pairs = [accs.tile([P, TOKENS], F32, tag="acc", name="acc_k1_%d" % i) for i in range(2)]
+            k1_rest = accs.tile([P, BANK // 2], F32, tag="acc")
             v0 = accs.tile([P, BANK], F32, tag="acc")
             v2, v3 = [accs.tile([P, BANK // 2], F32, tag="acc", name="acc_v%d" % b) for b in (2, 3)]
-            sums_ps = accs.tile([P, 4, 4], F32, tag="acc")
+            sums_ps = accs.tile([P, 8, 4], F32, tag="acc")
             v_banks = [v0, v2, v3]
             v_of_bank = [v0[:, 0 : BANK // 2], v0[:, BANK // 2 :], v2[:], v3[:]]
 
-            mx_passes(q0_load, q0_load + 1, [q0])
+            mx_passes(q0_load, k0_load, [q0])
             to_sbuf(("q", 0), q0, 0)
             transposes(("q", 0))
             split_q(0)
             split_q(1)
-            mx_passes(q0_load + 1, q0_load + 2, [k0])
+            mx_passes(k0_load, q1_load, [k0])
             to_sbuf(("k", 0), k0, EMB)
             transposes(("k", 0))
-            plain_k(0, nc.scalar.copy)
-            same_token_products(0)
-            mx_passes(q0_load + 2, k1_load, [q1])
+            plain_k(0, 0)
+            same_token_products(0, 0)
+            mx_passes(q1_load, k1_load, [q1])
             scores(0)
             scores(1)
             to_sbuf(("q", 1), q1, BANK)
@@ -620,83 +668,81 @@ def tile_dwarfattention_pa_k_kernel(
             exponentials(0)
             same_token_exp(0)
             exponentials(1)
-            mx_passes(k1_load, v_load - 2, [k1])
+            k1_passes(k1_load, v_load - 3)
             transposes(("q", 1))
             split_q(2)
             split_q(3)
-            mx_passes(v_load - 2, v_load, [k1])
+            k1_passes(v_load - 3, v_load)
+            biased_k()
             clip(0)
             same_token_clip(0)
             clip(1)
             same_token_weigh(0)
             weigh(0)
-            to_sbuf(("k", 1), k1, EMB + BANK)
+            to_sbuf(("k", 1), k1_rest, EMB + BANK + BANK // 2)
+            scores(2)
+            transposes(("k", 1))
+            plain_k(1, 2)
             weigh(1)
             same_token_sum(0)
-            same_token_products(1)
-            transposes(("k", 1))
-            plain_k(1, nc.scalar.copy)
+            same_token_products(1, 12)
             add_layers(0)
             same_token_z(0)
             add_layers(1)
-            scores(2)
             scores(3)
-            mx_passes(v_load, v_load + 2, v_banks)
-            same_token_dots(1)
             exponentials(2)
+            same_token_diagonal(2)
             exponentials(3)
-            same_token_exp(1)
-            mx_passes(v_load + 2, v0_load, v_banks)
+            same_token_dots(12)
+            same_token_dots(8)
+            mx_passes(v_load, v0_load, v_banks)
             clip(2)
-            same_token_clip(1)
+            same_token_exp(1)
             clip(3)
+            same_token_clip(1)
             weigh(2)
             same_token_weigh(1)
             add_layers(2)
-            mx_passes(v0_load, v1_load - 1, [v0])
-            column_sums()
+            mx_passes(v0_load, v0_load + 1, [v0])
+            column_sums(2)
+            mx_passes(v0_load + 1, v1_load, [v0])
             same_token_sum(1)
             weigh(3)
-            signed_sums(2, sums_ps[:, :, 0:3])
             same_token_z(1)
             add_layers(3)
-            sum_z(2)
-            mx_passes(v1_load - 1, v1_load, [v0])
-            invert_z(2)
+            column_sums(3)
             biased_v(0)
-            scale_w(2)
             biased_v(1)
-            mx_passes(v1_load, v1_load + 1, [v2, v3])
             weighted_sums(0)
+            signed_sums(halves[1], sums_ps[:, :, 0:3])
             same_token_v(0)
-            same_token_v(1)
-            mx_passes(v1_load + 1, v1_load + 2, [v2, v3])
+            sum_z(halves[1])
+            mx_passes(v1_load, v1_load + 1, [v2, v3])
             weighted_sums(1)
+            same_token_v(1)
+            invert_z(halves[1])
             class_sums(0)
             numerator(0)
-            sum_z(0)
-            invert_z(0)
-            mx_passes(v1_load + 2, v2_load, [v2, v3])
-            mx_passes(v2_load, v2_load + 1, [v3])
-            mx_passes(v2_load + 1, v2_load + 2, [v2])
+            scale_w(halves[1])
+            sum_z(of_bank(0))
+            mx_passes(v1_load + 1, v2_load, [v2, v3])
             class_sums(1)
+            invert_z(of_bank(0))
             numerator(1)
-            sum_z(1)
-            biased_v(3)
-            biased_v(2)
-            weighted_sums(3)
-            weighted_sums(2)
-            invert_z(1)
+            sum_z(of_bank(1))
             quotient(0)
+            invert_z(of_bank(1))
+            mx_passes(v2_load, v2_load + 1, [v3])
+            biased_v(3)
+            mx_passes(v2_load + 1, v2_load + 2, [v2])
             quotient(1)
             store(0, 1)
+            weighted_sums(3)
+            biased_v(2)
             same_token_v(3)
+            weighted_sums(2)
             same_token_v(2)
-            class_sums(3)
-            numerator(3)
-            sum_z(3)
-            finish(2, 0, 2)
-            invert_z(3)
-            finish(2, 2, 4)
-            quotient(3)
-            store(2, 3)
+            finish(3)
+            store(3, 3)
+            finish(2)
+            store(2, 2)

@@ -44,7 +44,7 @@ def taps_of(taus):
 LAYER_TAUS = [(1, 3), (2,)]
 
 
-W_BUFS = 7
+W_BUFS = 11
 
 
 def tile_dwarfattention_pa_k_kernel(
@@ -71,7 +71,6 @@ def tile_dwarfattention_pa_k_kernel(
         q_split = [keep.tile([P, 4, 2, TOKENS], F32, name="q_split%d" % i) for i in range(2)]
         base_tab = keep.tile([P, HEADS, TOKENS], BF16)
         step_tab = keep.tile([P, HEADS, TOKENS], F32)
-        k_bias = keep.tile([P, 2], F32)
         add_base = keep.tile([P, P], BF16)
         gain_tab = keep.tile([P, 2, HEADS, TOKENS], F32)
         tap_coef = keep.tile([P, TOKENS], F32)
@@ -87,8 +86,10 @@ def tile_dwarfattention_pa_k_kernel(
         z_inv = keep.tile([P, HEADS], F32)
 
         w_words = W_qkv_words.rearrange("g p n t -> p g (n t)").bitcast(I32)
-        head = PASSES - 4
-        w_loads = [(g0, 2, 0, 3 * BANK) for g0 in range(0, head, 2)]
+        wide, head = 8, 12
+        w_loads = [(g0, 1, 0, 4 * BANK) for g0 in range(wide)]
+        qk_load = len(w_loads)
+        w_loads += [(g0, 1, 0, 3 * BANK) for g0 in range(wide, head)]
         q0_load = len(w_loads)
         w_loads += [(g0, 4, 0, BANK) for g0 in range(head, PASSES, 4)]
         k0_load = len(w_loads)
@@ -96,8 +97,7 @@ def tile_dwarfattention_pa_k_kernel(
         q1_load = len(w_loads)
         w_loads += [(g0, 4, BANK, BANK) for g0 in range(head, PASSES, 4)]
         k1_load = len(w_loads)
-        w_loads += [(g0, 4, 3 * BANK, BANK) for g0 in range(0, PASSES - 4, 4)]
-        w_loads += [(g0, 2, 3 * BANK, BANK) for g0 in range(PASSES - 4, PASSES, 2)]
+        w_loads += [(g0, min(4, PASSES - g0), 3 * BANK, BANK) for g0 in range(wide, PASSES, 4)]
         v_load = len(w_loads)
         half_v = 6
         w_loads += [(g0, 2, 2 * EMB, 2 * BANK) for g0 in range(0, half_v, 2)]
@@ -135,34 +135,6 @@ def tile_dwarfattention_pa_k_kernel(
                         col = cols.stop
                 load_weights_up_to(t + 1 + W_BUFS)
 
-        def k1_passes(first, last):
-            for t in range(first, last):
-                g0, n_g, col0, n_cols = w_loads[t]
-                for gi in range(n_g):
-                    g = g0 + gi
-                    x_g = slice(TOKENS * g, TOKENS * (g + 1))
-                    planes = w_planes[4 * (g % PLANES) : P, g // PLANES, col0 : col0 + BANK]
-                    for i, acc in enumerate(k1_pairs + [k1_rest]):
-                        x_side = (x_codes[:, x_g].bitcast(FP8X4), x_scales[:, x_g])
-                        cols = slice(P * i, P * i + acc.shape[1])
-                        w_side = (w_tiles[t][:, gi, cols].bitcast(FP8X4), planes[:, cols])
-                        stationary, moving = (x_side, w_side) if acc is k1_rest else (w_side, x_side)
-                        nc.tensor.matmul_mx(
-                            out=acc[:],
-                            lhsT=stationary[0],
-                            lhsT_scale=stationary[1],
-                            rhs=moving[0],
-                            rhs_scale=moving[1],
-                            start=(g == 0),
-                            stop=(g == PASSES - 1),
-                        )
-                load_weights_up_to(t + 1 + W_BUFS)
-
-        def elu_plus_one(dst, u, tmp):
-            nc.scalar.activation(out=dst, in_=u, func=ACT.Exp)
-            nc.vector.tensor_scalar(out=tmp, in0=u, scalar1=0.0, scalar2=1.0, op0=ALU.max, op1=ALU.add)
-            nc.vector.tensor_tensor(out=dst, in0=dst, in1=tmp, op=ALU.min)
-
         with tc.tile_pool(name="setup", bufs=1) as setup:
             small_row = setup.tile([P, n_pb + HEADS], BF16)
             nc.vector.memset(small_row[:], 0.0)
@@ -193,12 +165,12 @@ def tile_dwarfattention_pa_k_kernel(
                     )
             load_weights_up_to(W_BUFS)
 
+            bias_rows = setup.tile([P, P], BF16)
+            nc.gpsimd.memset(bias_rows[:], 0.0)
+            nc.gpsimd.dma_start(out=bias_rows[0 : 3 * EMB // P, :], in_=b_qkv.rearrange("(r c) -> r c", c=P))
             gains_h = setup.tile([P, TOKENS * SCALES], BF16)
             nc.gpsimd.memset(gains_h[:], 0.0)
             nc.gpsimd.dma_start(out=gains_h[0:HEADS, :], in_=gains.rearrange("o h n j -> (o h) (n j)"))
-            bias_row = setup.tile([P, 3 * EMB], BF16)
-            nc.gpsimd.memset(bias_row[:], 0.0)
-            nc.gpsimd.dma_start(out=bias_row[0:1, :], in_=b_qkv.rearrange("(o n) -> o n", o=1))
             before = setup.tile([P, TAPS - 1, 8], F32)
             nc.gpsimd.memset(before[:], 0.0)
             for j, tau, o in taps_of((1, 2, 3)):
@@ -350,11 +322,17 @@ def tile_dwarfattention_pa_k_kernel(
 
             def spread_b_qkv(first, last):
                 for i in range(first, last):
-                    ps = work.tile([P, BANK], F32, tag="work")
-                    nc.tensor.matmul(
-                        out=ps[:], lhsT=ones_b[:], rhs=bias_row[:, BANK * i : BANK * (i + 1)], start=True, stop=True
-                    )
-                    nc.scalar.copy(out=bias_all[:, BANK * i : BANK * (i + 1)], in_=ps[:])
+                    ps = work.tile([P, 4, P], F32, tag="work")
+                    for j in range(4):
+                        row = 4 * i + j
+                        nc.tensor.matmul(
+                            out=ps[:, j, :],
+                            lhsT=ident_b[:, row : row + 1].to_broadcast([P, P]),
+                            rhs=bias_rows[:],
+                            start=True,
+                            stop=True,
+                        )
+                    nc.scalar.copy(out=bias_all[:, BANK * i : BANK * (i + 1)], in_=ps[:].rearrange("p j c -> p (j c)"))
 
             gains_nt = setup.tile([P, HEADS, SCALES], F32)
 
@@ -368,24 +346,27 @@ def tile_dwarfattention_pa_k_kernel(
                         out=gains_nt[:, :, j0 : j0 + n_j], in_=ps[:, 0:n_j, 0:HEADS].rearrange("p j h -> p h j")
                     )
 
-            def small_tables():
-                soft = setup.tile([P, HEADS], F32)
+            soft = setup.tile([P, HEADS], F32)
+            n_f = TAPS * 8 * HEADS
+            f_of_bias = setup.tile([P, n_f], F32)
+            f_tmp = setup.tile([P, n_f], F32)
+
+            def bias_functions():
                 nc.scalar.activation(out=soft[:], in_=bypass_all, func=ACT.Abs)
                 nc.scalar.activation(out=soft[:], in_=soft[:], func=ACT.Exp, scale=-1.0)
                 nc.scalar.activation(out=soft[:], in_=soft[:], func=ACT.Ln, bias=ones_f[:, 0:1])
+                nc.scalar.activation(out=f_of_bias[:], in_=pb_all[:, 0:n_f], func=ACT.Exp)
+
+            def small_tables():
                 nc.vector.scalar_tensor_tensor(
                     out=diag_gain[:, :, SCALES], in0=bypass_all, scalar=0.0, in1=soft[:], op0=ALU.max, op1=ALU.add
                 )
                 nc.vector.tensor_scalar_mul(out=diag_gain[:, :, 0:SCALES], in0=gains_nt[:], scalar1=D4[0])
                 nc.vector.memset(diag_bias[:, :, SCALES], 1.0)
                 nc.vector.tensor_scalar_add(out=diag_bias[:, :, 0:SCALES], in0=pb_by_tau[:, 0, :, :], scalar1=1.0)
-                nc.vector.memset(diag_bias[:, 8:12, SCALES], 0.0)
-                nc.vector.tensor_copy(out=diag_bias[:, 8:12, 0:SCALES], in_=pb_by_tau[:, 0, 8:12, :])
 
-                n_f = TAPS * 8 * HEADS
-                f_of_bias = setup.tile([P, n_f], F32)
-                f_tmp = setup.tile([P, n_f], F32)
-                elu_plus_one(f_of_bias[:], pb_all[:, 0:n_f], f_tmp[:])
+                nc.vector.tensor_scalar(out=f_tmp[:], in0=pb_all[:, 0:n_f], scalar1=0.0, scalar2=1.0, op0=ALU.max, op1=ALU.add)
+                nc.vector.tensor_tensor(out=f_of_bias[:], in0=f_of_bias[:], in1=f_tmp[:], op=ALU.min)
                 for tau in range(1, TAPS):
                     nc.vector.tensor_scalar_mul(out=before[:, tau - 1, :], in0=before[:, tau - 1, :], scalar1=abs(D4[tau]))
                 gf = setup.tile([P, HEADS, TAPS - 1, 8], F32)
@@ -402,20 +383,21 @@ def tile_dwarfattention_pa_k_kernel(
                 nc.vector.tensor_reduce(out=gf_sum[:], in_=gf[:].rearrange("p h t j -> p h (t j)"), op=ALU.add, axis=AXIS_X)
                 nc.vector.tensor_scalar_add(out=z_fixed[:], in0=gf_sum[:], scalar1=EPS)
 
-            q0, k0, q1 = [accs.tile([P, BANK], F32, tag="acc", name="acc_%s" % n) for n in ("q0", "k0", "q1")]
-            for t in range(4):
-                mx_passes(t, t + 1, [q0, q1, k0])
-                table_quarter(t)
+            q0, k0, q1, k1 = [accs.tile([P, BANK], F32, tag="acc", name="acc_%s" % n) for n in ("q0", "k0", "q1", "k1")]
+
+            def qk_passes(first, last):
+                mx_passes(first, min(last, qk_load), [q0, q1, k0, k1])
+                mx_passes(max(first, qk_load), last, [q0, q1, k0])
+
+            bias_functions()
+            for quarter in range(4):
+                qk_passes(2 * quarter, 2 * quarter + 2)
+                table_quarter(quarter)
             transpose_gains()
             small_tables()
-            mx_passes(4, 5, [q0, q1, k0])
             spread_b_qkv(0, 6)
-            ps = work.tile([P, 2, 2], F32, tag="work")
-            for pair in range(2):
-                cols = slice(EMB + BANK + P * pair, EMB + BANK + P * (pair + 1))
-                nc.tensor.matmul(out=ps[:, pair, :], lhsT=bias_all[:, cols], rhs=ident_b[:, 0:2], start=True, stop=True)
-            nc.vector.tensor_copy(out=k_bias[:], in_=ps[:, :, 0])
-            mx_passes(5, q0_load, [q0, q1, k0])
+            qk_passes(8, q0_load)
+
         with tc.tile_pool(name="dense", bufs=2) as dense:
             toks, trs, k_ts, prods = {}, {}, {}, {}
             sts, us, fs = {}, {}, {}
@@ -437,16 +419,9 @@ def tile_dwarfattention_pa_k_kernel(
                 k_t = dense.tile([P, 4, TOKENS], F32, tag="k_t")
                 k_ts[half_i] = k_t
 
-            def plain_k(half_i, first):
-                tr = trs["k", half_i]
-                for i in range(0, tr.shape[1], 2):
-                    nc.scalar.copy(out=k_ts[half_i][:, first + i : first + i + 2, :], in_=tr[:, i : i + 2, :])
-
-            def biased_k():
-                for pair in range(2):
-                    nc.scalar.activation(
-                        out=k_ts[1][:, pair, :], in_=k1_pairs[pair][:], func=ACT.Identity, bias=k_bias[:, pair : pair + 1]
-                    )
+            def plain_k(half_i):
+                for two in (slice(0, 2), slice(2, 4)):
+                    nc.scalar.copy(out=k_ts[half_i][:, two, :], in_=trs["k", half_i][:, two, :])
 
             def split_q(b):
                 two = slice(2 * (b % 2), 2 * (b % 2) + 2)
@@ -473,27 +448,19 @@ def tile_dwarfattention_pa_k_kernel(
 
             dots = dense.tile([P, HEADS], F32, bufs=1)
 
-            def same_token_products(key, first):
-                k_tok = toks["k", key]
-                width = k_tok.shape[1]
-                prod = dense.tile([P, width], F32, tag="prod")
-                nc.vector.tensor_tensor(out=prod[:], in0=toks["q", key][:, BANK - width :], in1=k_tok[:], op=ALU.mult)
-                prods[first] = prod[:].rearrange("p (h d) -> p h d", d=HEAD_DIM)
+            def same_token_products(half_i):
+                prod = dense.tile([P, BANK], F32, tag="prod")
+                nc.vector.tensor_tensor(out=prod[:], in0=toks["q", half_i][:], in1=toks["k", half_i][:], op=ALU.mult)
+                prods[half_i] = prod
 
-            def same_token_diagonal(b):
-                prod = dense.tile([P, 4, TOKENS], F32, tag="diagonal")
-                nc.vector.tensor_tensor(
-                    out=prod[:], in0=sts[b][:], in1=ident_f[:].unsqueeze(1).to_broadcast([P, 4, TOKENS]), op=ALU.mult
-                )
-                prods[4 * b] = prod
-
-            def same_token_dots(first):
-                for i in range(prods[first].shape[1]):
+            def same_token_dots(half_i):
+                for i in range(8):
+                    cols = slice(HEAD_DIM * i, HEAD_DIM * (i + 1))
                     nc.scalar.activation(
-                        out=prods[first][:, i, :],
-                        in_=prods[first][:, i, :],
+                        out=prods[half_i][:, cols],
+                        in_=prods[half_i][:, cols],
                         func=ACT.Identity,
-                        accum_out=dots[:, first + i : first + i + 1],
+                        accum_out=dots[:, 8 * half_i + i : 8 * half_i + i + 1],
                     )
 
             def exponentials(b):
@@ -642,8 +609,6 @@ def tile_dwarfattention_pa_k_kernel(
                 cols = slice(4 * HEAD_DIM * first, 4 * HEAD_DIM * (last + 1))
                 nc.sync.dma_start(out=out_rows[:, cols], in_=o_sb[:].rearrange("p h d -> p (h d)")[:, cols])
 
-            k1_pairs = [accs.tile([P, TOKENS], F32, tag="acc", name="acc_k1_%d" % i) for i in range(2)]
-            k1_rest = accs.tile([P, BANK // 2], F32, tag="acc")
             v0 = accs.tile([P, BANK], F32, tag="acc")
             v2, v3 = [accs.tile([P, BANK // 2], F32, tag="acc", name="acc_v%d" % b) for b in (2, 3)]
             sums_ps = accs.tile([P, 8, 4], F32, tag="acc")
@@ -658,8 +623,8 @@ def tile_dwarfattention_pa_k_kernel(
             mx_passes(k0_load, q1_load, [k0])
             to_sbuf(("k", 0), k0, EMB)
             transposes(("k", 0))
-            plain_k(0, 0)
-            same_token_products(0, 0)
+            plain_k(0)
+            same_token_products(0)
             mx_passes(q1_load, k1_load, [q1])
             scores(0)
             scores(1)
@@ -668,44 +633,41 @@ def tile_dwarfattention_pa_k_kernel(
             exponentials(0)
             same_token_exp(0)
             exponentials(1)
-            k1_passes(k1_load, v_load - 3)
             transposes(("q", 1))
             split_q(2)
             split_q(3)
-            k1_passes(v_load - 3, v_load)
-            biased_k()
+            mx_passes(k1_load, v_load, [k1])
             clip(0)
             same_token_clip(0)
             clip(1)
             same_token_weigh(0)
+            to_sbuf(("k", 1), k1, EMB + BANK)
             weigh(0)
-            to_sbuf(("k", 1), k1_rest, EMB + BANK + BANK // 2)
-            scores(2)
-            transposes(("k", 1))
-            plain_k(1, 2)
             weigh(1)
             same_token_sum(0)
-            same_token_products(1, 12)
+            same_token_products(1)
+            transposes(("k", 1))
+            plain_k(1)
             add_layers(0)
             same_token_z(0)
             add_layers(1)
+            scores(2)
             scores(3)
+            mx_passes(v_load, v_load + 1, v_banks)
+            same_token_dots(1)
             exponentials(2)
-            same_token_diagonal(2)
             exponentials(3)
-            same_token_dots(12)
-            same_token_dots(8)
-            mx_passes(v_load, v0_load, v_banks)
-            clip(2)
             same_token_exp(1)
-            clip(3)
+            mx_passes(v_load + 1, v0_load, v_banks)
+            clip(2)
             same_token_clip(1)
+            clip(3)
             weigh(2)
             same_token_weigh(1)
             add_layers(2)
-            mx_passes(v0_load, v0_load + 1, [v0])
+            mx_passes(v0_load, v1_load - 1, [v0])
             column_sums(2)
-            mx_passes(v0_load + 1, v1_load, [v0])
+            mx_passes(v1_load - 1, v1_load, [v0])
             same_token_sum(1)
             weigh(3)
             same_token_z(1)

@@ -44,6 +44,7 @@ def taps_of(taus):
 LAYER_TAUS = [(1, 3), (2,)]
 
 
+CLASS_WIDTH = 48
 W_BUFS = 11
 
 
@@ -74,7 +75,8 @@ def tile_dwarfattention_pa_k_kernel(
         add_base = keep.tile([P, P], BF16)
         gain_tab = keep.tile([P, 2, HEADS, TOKENS], F32)
         tap_coef = keep.tile([P, TOKENS], F32)
-        class3 = keep.tile([P, 4], F32)
+        class_wide = keep.tile([P, CLASS_WIDTH], F32)
+        class3 = class_wide[:, 0:4]
         sign3 = keep.tile([P, 4], F32)
         diag_bias = keep.tile([P, HEADS, SCALES + 1], F32)
         diag_gain = keep.tile([P, HEADS, SCALES + 1], F32)
@@ -86,7 +88,7 @@ def tile_dwarfattention_pa_k_kernel(
         z_inv = keep.tile([P, HEADS], F32)
 
         w_words = W_qkv_words.rearrange("g p n t -> p g (n t)").bitcast(I32)
-        wide, head = 8, 12
+        wide, head = 4, 12
         w_loads = [(g0, 1, 0, 4 * BANK) for g0 in range(wide)]
         qk_load = len(w_loads)
         w_loads += [(g0, 1, 0, 3 * BANK) for g0 in range(wide, head)]
@@ -154,8 +156,8 @@ def tile_dwarfattention_pa_k_kernel(
 
             x_sb = setup.tile([P, D_MODEL], BF16)
             x_rows = x.rearrange("o n k -> (o n) k")
-            for c in range(4):
-                cols = slice(c * D_MODEL // 4, (c + 1) * D_MODEL // 4)
+            for c in range(2):
+                cols = slice(c * D_MODEL // 2, (c + 1) * D_MODEL // 2)
                 nc.sync.dma_start(out=x_sb[:, cols], in_=x_rows[:, cols])
             for a in range(PASSES // PLANES):
                 for quad in range(4):
@@ -203,11 +205,11 @@ def tile_dwarfattention_pa_k_kernel(
             for twin in range(2):
                 nc.vector.tensor_copy(out=gains_pad[:, :, :, twin:SLOTS:2], in_=gains_by_j[:, :, :, 0 : SLOTS // 2])
 
-            nc.vector.memset(class3[:], 0.0)
+            nc.vector.memset(class_wide[:], 0.0)
             for c in range(3):
                 nc.vector.tensor_reduce(out=class3[:, c : c + 1], in_=ident_f[:, c:TOKENS:3], op=ALU.add, axis=AXIS_X)
-            nc.vector.tensor_copy(out=v_sb[:, :, HEAD_DIM:], in_=class3[:].unsqueeze(1).to_broadcast([P, HEADS, 4]))
-            nc.vector.tensor_scalar(out=sign3[:], in0=class3[:], scalar1=-2.0, scalar2=1.0, op0=ALU.mult, op1=ALU.add)
+            nc.vector.tensor_copy(out=v_sb[:, :, HEAD_DIM:], in_=class3.unsqueeze(1).to_broadcast([P, HEADS, 4]))
+            nc.vector.tensor_scalar(out=sign3[:], in0=class3, scalar1=-2.0, scalar2=1.0, op0=ALU.mult, op1=ALU.add)
             for c in range(3):
                 n_c = len(range(c, TOKENS, 3))
                 nc.vector.tensor_scalar(
@@ -528,7 +530,7 @@ def tile_dwarfattention_pa_k_kernel(
             o_sb = dense.tile([P, HEADS, HEAD_DIM], F32, bufs=1)
             z_sum = dense.tile([P, HEADS], F32, bufs=1)
             out_rows = out.rearrange("o n e -> (o n) e")
-            o_pss = {}
+            o_pss, sums_pss = {}, {}
 
             def of_bank(b):
                 return slice(4 * b, 4 * b + 4)
@@ -568,8 +570,10 @@ def tile_dwarfattention_pa_k_kernel(
                 signed_sums(of_bank(b), o_pss[b][:, :, HEAD_DIM : HEAD_DIM + 3])
 
             def column_sums(b):
-                for h in range(4 * b, 4 * b + 4):
-                    nc.tensor.matmul(out=sums_ps[:, h - 8, :], lhsT=at_all[:, h, :], rhs=class3[:], start=True, stop=True)
+                sums_ps = work.tile([P, 4, CLASS_WIDTH], F32, tag="work")
+                for i in range(4):
+                    nc.tensor.matmul(out=sums_ps[:, i, :], lhsT=at_all[:, 4 * b + i, :], rhs=class_wide[:], start=True, stop=True)
+                sums_pss[b] = sums_ps
 
             def numerator(b):
                 nc.vector.tensor_tensor(
@@ -611,7 +615,6 @@ def tile_dwarfattention_pa_k_kernel(
 
             v0 = accs.tile([P, BANK], F32, tag="acc")
             v2, v3 = [accs.tile([P, BANK // 2], F32, tag="acc", name="acc_v%d" % b) for b in (2, 3)]
-            sums_ps = accs.tile([P, 8, 4], F32, tag="acc")
             v_banks = [v0, v2, v3]
             v_of_bank = [v0[:, 0 : BANK // 2], v0[:, BANK // 2 :], v2[:], v3[:]]
 
@@ -676,7 +679,8 @@ def tile_dwarfattention_pa_k_kernel(
             biased_v(0)
             biased_v(1)
             weighted_sums(0)
-            signed_sums(halves[1], sums_ps[:, :, 0:3])
+            signed_sums(of_bank(2), sums_pss[2][:, :, 0:3])
+            signed_sums(of_bank(3), sums_pss[3][:, :, 0:3])
             same_token_v(0)
             sum_z(halves[1])
             mx_passes(v1_load, v1_load + 1, [v2, v3])

@@ -45,7 +45,7 @@ LAYER_TAUS = [(1, 3), (2,)]
 
 
 CLASS_WIDTH = 48
-W_BUFS = 11
+W_BUFS = 7
 
 
 def tile_dwarfattention_pa_k_kernel(
@@ -88,10 +88,10 @@ def tile_dwarfattention_pa_k_kernel(
         z_inv = keep.tile([P, HEADS], F32)
 
         w_words = W_qkv_words.rearrange("g p n t -> p g (n t)").bitcast(I32)
-        wide, head = 4, 12
+        wide, head = 4, PASSES - 4
         w_loads = [(g0, 1, 0, 4 * BANK) for g0 in range(wide)]
         qk_load = len(w_loads)
-        w_loads += [(g0, 1, 0, 3 * BANK) for g0 in range(wide, head)]
+        w_loads += [(g0, 2, 0, 3 * BANK) for g0 in range(wide, head, 2)]
         q0_load = len(w_loads)
         w_loads += [(g0, 4, 0, BANK) for g0 in range(head, PASSES, 4)]
         k0_load = len(w_loads)
@@ -101,7 +101,7 @@ def tile_dwarfattention_pa_k_kernel(
         k1_load = len(w_loads)
         w_loads += [(g0, min(4, PASSES - g0), 3 * BANK, BANK) for g0 in range(wide, PASSES, 4)]
         v_load = len(w_loads)
-        half_v = 6
+        half_v = 8
         w_loads += [(g0, 2, 2 * EMB, 2 * BANK) for g0 in range(0, half_v, 2)]
         v0_load = len(w_loads)
         w_loads += [(g0, min(4, PASSES - g0), 2 * EMB, BANK) for g0 in range(half_v, PASSES, 4)]
@@ -156,8 +156,8 @@ def tile_dwarfattention_pa_k_kernel(
 
             x_sb = setup.tile([P, D_MODEL], BF16)
             x_rows = x.rearrange("o n k -> (o n) k")
-            for c in range(2):
-                cols = slice(c * D_MODEL // 2, (c + 1) * D_MODEL // 2)
+            for c in range(4):
+                cols = slice(c * D_MODEL // 4, (c + 1) * D_MODEL // 4)
                 nc.sync.dma_start(out=x_sb[:, cols], in_=x_rows[:, cols])
             for a in range(PASSES // PLANES):
                 for quad in range(4):
@@ -393,12 +393,14 @@ def tile_dwarfattention_pa_k_kernel(
 
             bias_functions()
             for quarter in range(4):
-                qk_passes(2 * quarter, 2 * quarter + 2)
+                qk_passes(quarter, quarter + 1)
                 table_quarter(quarter)
+            qk_passes(4, 5)
             transpose_gains()
             small_tables()
+            qk_passes(5, 6)
             spread_b_qkv(0, 6)
-            qk_passes(8, q0_load)
+            qk_passes(6, q0_load)
 
         with tc.tile_pool(name="dense", bufs=2) as dense:
             toks, trs, k_ts, prods = {}, {}, {}, {}
@@ -636,75 +638,74 @@ def tile_dwarfattention_pa_k_kernel(
             exponentials(0)
             same_token_exp(0)
             exponentials(1)
+            mx_passes(k1_load, v_load - 1, [k1])
             transposes(("q", 1))
             split_q(2)
             split_q(3)
-            mx_passes(k1_load, v_load, [k1])
+            mx_passes(v_load - 1, v_load, [k1])
             clip(0)
-            same_token_clip(0)
             clip(1)
-            same_token_weigh(0)
+            same_token_clip(0)
             to_sbuf(("k", 1), k1, EMB + BANK)
+            same_token_weigh(0)
             weigh(0)
-            weigh(1)
-            same_token_sum(0)
-            same_token_products(1)
             transposes(("k", 1))
             plain_k(1)
+            weigh(1)
+            same_token_sum(0)
             add_layers(0)
             same_token_z(0)
-            add_layers(1)
+            same_token_products(1)
             scores(2)
             scores(3)
-            mx_passes(v_load, v_load + 1, v_banks)
-            same_token_dots(1)
+            mx_passes(v_load, v_load + 2, v_banks)
             exponentials(2)
+            add_layers(1)
             exponentials(3)
-            same_token_exp(1)
-            mx_passes(v_load + 1, v0_load, v_banks)
+            same_token_dots(1)
+            mx_passes(v_load + 2, v0_load, v_banks)
             clip(2)
-            same_token_clip(1)
             clip(3)
             weigh(2)
-            same_token_weigh(1)
+            same_token_exp(1)
             add_layers(2)
             mx_passes(v0_load, v1_load - 1, [v0])
             column_sums(2)
-            mx_passes(v1_load - 1, v1_load, [v0])
-            same_token_sum(1)
             weigh(3)
-            same_token_z(1)
+            same_token_clip(1)
             add_layers(3)
+            same_token_weigh(1)
+            mx_passes(v1_load - 1, v1_load, [v0])
             column_sums(3)
             biased_v(0)
+            same_token_sum(1)
             biased_v(1)
             weighted_sums(0)
+            same_token_v(0)
+            same_token_z(1)
+            same_token_v(1)
             signed_sums(of_bank(2), sums_pss[2][:, :, 0:3])
             signed_sums(of_bank(3), sums_pss[3][:, :, 0:3])
-            same_token_v(0)
-            sum_z(halves[1])
             mx_passes(v1_load, v1_load + 1, [v2, v3])
             weighted_sums(1)
-            same_token_v(1)
-            invert_z(halves[1])
             class_sums(0)
+            sum_z(halves[1])
             numerator(0)
-            scale_w(halves[1])
-            sum_z(of_bank(0))
+            invert_z(halves[1])
             mx_passes(v1_load + 1, v2_load, [v2, v3])
             class_sums(1)
-            invert_z(of_bank(0))
+            scale_w(halves[1])
+            sum_z(halves[0])
             numerator(1)
-            sum_z(of_bank(1))
-            quotient(0)
-            invert_z(of_bank(1))
+            invert_z(halves[0])
             mx_passes(v2_load, v2_load + 1, [v3])
-            biased_v(3)
             mx_passes(v2_load + 1, v2_load + 2, [v2])
+            quotient(0)
+            biased_v(3)
+            biased_v(2)
             quotient(1)
             store(0, 1)
             weighted_sums(3)
-            biased_v(2)
             same_token_v(3)
             weighted_sums(2)
             same_token_v(2)

@@ -638,11 +638,10 @@ def tile_dwarfattention_pa_k_kernel(
             exponentials(0)
             same_token_exp(0)
             exponentials(1)
-            mx_passes(k1_load, v_load - 1, [k1])
             transposes(("q", 1))
+            mx_passes(k1_load, v_load, [k1])
             split_q(2)
             split_q(3)
-            mx_passes(v_load - 1, v_load, [k1])
             clip(0)
             clip(1)
             same_token_clip(0)
@@ -686,8 +685,8 @@ def tile_dwarfattention_pa_k_kernel(
             same_token_v(1)
             signed_sums(of_bank(2), sums_pss[2][:, :, 0:3])
             signed_sums(of_bank(3), sums_pss[3][:, :, 0:3])
-            mx_passes(v1_load, v1_load + 1, [v2, v3])
             weighted_sums(1)
+            mx_passes(v1_load, v1_load + 1, [v2, v3])
             class_sums(0)
             sum_z(halves[1])
             numerator(0)

from contextlib import ExitStack

import concourse.mybir as mybir
from concourse.masks import make_identity

F32 = mybir.dt.float32
BF16 = mybir.dt.bfloat16
I32 = mybir.dt.int32
U32 = mybir.dt.uint32
U8 = mybir.dt.uint8
FP8X4 = mybir.dt.float8_e4m3fn_x4
ALU = mybir.AluOpType
ACT = mybir.ActivationFunctionType
AXIS_X = mybir.AxisListType.X

P = 128
TOKENS = 128
D_MODEL = 8192
HEADS = 16
HEAD_DIM = 64
EMB = HEADS * HEAD_DIM
SCALES = 11
TAPS = 4
D4 = [0.4829629131445341, 0.8365163037378079, 0.2241438680420134, -0.1294095225512604]
EPS = 1e-06

K_PASS = 512
PASSES = D_MODEL // K_PASS
BANK = 512
PLANES = 4

GROUP = 8
GROUPS = TOKENS // GROUP
SLOTS = P // GROUP
PAD = TOKENS - GROUP

FLOPS = 2 * TOKENS * D_MODEL * 3 * EMB


def taps_of(taus):
    return [(j, tau, tau << j) for j in range(SCALES) for tau in taus if (tau << j) < TOKENS]


LAYER_TAUS = [(1, 3), (2,)]


CLASS_WIDTH = 48
W_BUFS = 7


def tile_dwarfattention_pa_k_kernel(
    tc, x, W_qkv_words, W_qkv_scales, b_qkv, gains, pos_bias, identity_bypass, out
):
    nc = tc.nc
    n_pb = SCALES * TAPS * HEADS
    with ExitStack() as stack:
        stack.enter_context(tc.manual_schedule())
        keep = stack.enter_context(tc.tile_pool(name="keep", bufs=1))
        wpool = stack.enter_context(tc.tile_pool(name="weights", bufs=W_BUFS))
        accs = stack.enter_context(tc.psum_pool(name="accs", bufs=4))
        work = stack.enter_context(tc.psum_pool(name="work", bufs=4))

        ident_f = keep.tile([P, P], F32)
        ident_b = keep.tile([P, P], BF16)
        ones_b = keep.tile([P, P], BF16)
        ones_f = keep.tile([P, 2], F32)
        minus_one = keep.tile([P, 1], F32)
        x_codes = keep.tile([P, PASSES * TOKENS], U32, align_bytes=64)
        x_scales = keep.tile([P, PASSES * TOKENS], U8, align_bytes=64)
        w_planes = keep.tile([P, PASSES // PLANES, 3 * EMB], U8, align_bytes=64)
        bias_all = keep.tile([P, 3 * EMB], BF16)
        q_split = [keep.tile([P, 4, 2, TOKENS], F32, name="q_split%d" % i) for i in range(2)]
        base_tab = keep.tile([P, HEADS, TOKENS], BF16)
        step_tab = keep.tile([P, HEADS, TOKENS], F32)
        add_base = keep.tile([P, P], BF16)
        gain_tab = keep.tile([P, 2, HEADS, TOKENS], F32)
        tap_coef = keep.tile([P, TOKENS], F32)
        class_wide = keep.tile([P, CLASS_WIDTH], F32)
        class3 = class_wide[:, 0:4]
        sign3 = keep.tile([P, 4], F32)
        diag_bias = keep.tile([P, HEADS, SCALES + 1], F32)
        diag_gain = keep.tile([P, HEADS, SCALES + 1], F32)
        z_fixed = keep.tile([P, HEADS], F32)
        at_all = keep.tile([P, HEADS, TOKENS], F32)
        v_sb = keep.tile([P, HEADS, HEAD_DIM + 4], F32)
        w_diag = keep.tile([P, HEADS], F32)
        z_parts = keep.tile([P, HEADS, 4], F32)
        z_inv = keep.tile([P, HEADS], F32)

        w_words = W_qkv_words.rearrange("g p n t -> p g (n t)").bitcast(I32)
        wide, head = 4, PASSES - 4
        w_loads = [(g0, 1, 0, 4 * BANK) for g0 in range(wide)]
        qk_load = len(w_loads)
        w_loads += [(g0, 2, 0, 3 * BANK) for g0 in range(wide, head, 2)]
        q0_load = len(w_loads)
        w_loads += [(g0, 4, 0, BANK) for g0 in range(head, PASSES, 4)]
        k0_load = len(w_loads)
        w_loads += [(g0, 4, EMB, BANK) for g0 in range(head, PASSES, 4)]
        q1_load = len(w_loads)
        w_loads += [(g0, 4, BANK, BANK) for g0 in range(head, PASSES, 4)]
        k1_load = len(w_loads)
        w_loads += [(g0, min(4, PASSES - g0), 3 * BANK, BANK) for g0 in range(wide, PASSES, 4)]
        v_load = len(w_loads)
        half_v = 8
        w_loads += [(g0, 2, 2 * EMB, 2 * BANK) for g0 in range(0, half_v, 2)]
        v0_load = len(w_loads)
        w_loads += [(g0, min(4, PASSES - g0), 2 * EMB, BANK) for g0 in range(half_v, PASSES, 4)]
        v1_load = len(w_loads)
        w_loads += [(g0, 2, 2 * EMB + BANK, BANK) for g0 in range(half_v, PASSES - 2, 2)]
        v2_load = len(w_loads)
        w_loads += [(PASSES - 2, 2, 2 * EMB + BANK + i * BANK // 2, BANK // 2) for i in (1, 0)]
        w_tiles = []

        def load_weights_up_to(n):
            for g0, n_g, col0, n_cols in w_loads[len(w_tiles) : n]:
                w = wpool.tile([P, n_g, n_cols], U32, tag="w", align_bytes=64)
                nc.sync.dma_start(out=w[:].bitcast(I32), in_=w_words[:, g0 : g0 + n_g, col0 : col0 + n_cols])
                w_tiles.append(w)

        def mx_passes(first, last, banks):
            for t in range(first, last):
                g0, n_g, col0, n_cols = w_loads[t]
                for gi in range(n_g):
                    g = g0 + gi
                    col = 0
                    for bank in banks:
                        cols = slice(col, col + bank.shape[1])
                        nc.tensor.matmul_mx(
                            out=bank[:],
                            lhsT=x_codes[:, TOKENS * g : TOKENS * (g + 1)].bitcast(FP8X4),
                            lhsT_scale=x_scales[:, TOKENS * g : TOKENS * (g + 1)],
                            rhs=w_tiles[t][:, gi, cols].bitcast(FP8X4),
                            rhs_scale=w_planes[4 * (g % PLANES) : P, g // PLANES, col0 + cols.start : col0 + cols.stop],
                            start=(g == 0),
                            stop=(g == PASSES - 1),
                        )
                        col = cols.stop
                load_weights_up_to(t + 1 + W_BUFS)

        with tc.tile_pool(name="setup", bufs=1) as setup:
            small_row = setup.tile([P, n_pb + HEADS], BF16)
            nc.vector.memset(small_row[:], 0.0)
            nc.scalar.dma_start(out=small_row[0:1, 0:n_pb], in_=pos_bias.rearrange("(o r) h -> o (r h)", o=1))
            nc.scalar.dma_start(out=small_row[0:1, n_pb:], in_=identity_bypass.rearrange("(o h) -> o h", o=1))
            gains_hg = setup.tile([P, 2, GROUP * SCALES], BF16)
            nc.scalar.dma_start(
                out=gains_hg[:],
                in_=gains.rearrange("o h (g a) j -> (o h g) (a j)", a=GROUP).rearrange("(t p) e -> p t e", p=P),
            )
            nc.vector.memset(w_planes[:].rearrange("p a n -> p (a n)").bitcast(I32), 0)
            make_identity(nc, ident_f[:])
            make_identity(nc, ident_b[:])
            nc.gpsimd.memset(ones_b[:], 1.0)
            nc.gpsimd.memset(ones_f[:], 1.0)
            nc.gpsimd.memset(minus_one[:], -1.0)

            x_sb = setup.tile([P, D_MODEL], BF16)
            x_rows = x.rearrange("o n k -> (o n) k")
            for c in range(4):
                cols = slice(c * D_MODEL // 4, (c + 1) * D_MODEL // 4)
                nc.sync.dma_start(out=x_sb[:, cols], in_=x_rows[:, cols])
            for a in range(PASSES // PLANES):
                for quad in range(4):
                    nc.sync.dma_start(
                        out=w_planes[32 * quad : 32 * quad + 16, a, :].bitcast(I32),
                        in_=W_qkv_scales[PLANES * a : PLANES * (a + 1), 4 * quad : 4 * quad + 4, :].bitcast(I32),
                    )
            load_weights_up_to(W_BUFS)

            bias_rows = setup.tile([P, P], BF16)
            nc.gpsimd.memset(bias_rows[:], 0.0)
            nc.gpsimd.dma_start(out=bias_rows[0 : 3 * EMB // P, :], in_=b_qkv.rearrange("(r c) -> r c", c=P))
            gains_h = setup.tile([P, TOKENS * SCALES], BF16)
            nc.gpsimd.memset(gains_h[:], 0.0)
            nc.gpsimd.dma_start(out=gains_h[0:HEADS, :], in_=gains.rearrange("o h n j -> (o h) (n j)"))
            before = setup.tile([P, TAPS - 1, 8], F32)
            nc.gpsimd.memset(before[:], 0.0)
            for j, tau, o in taps_of((1, 2, 3)):
                nc.gpsimd.memset(before[0:o, tau - 1, j : j + 1], 1.0)
            for tile in q_split:
                nc.gpsimd.memset(tile[:], 0.0)

            token_of_row = setup.tile([P, GROUP], F32)
            nc.vector.tensor_reduce(
                out=token_of_row[:], in_=ident_f[:].rearrange("p (a s) -> p a s", s=SLOTS), op=ALU.add, axis=AXIS_X
            )
            slot_of_row = setup.tile([P, SLOTS], F32)
            nc.vector.tensor_reduce(
                out=slot_of_row[:], in_=ident_f[:].rearrange("p (a s) -> p s a", s=SLOTS), op=ALU.add, axis=AXIS_X
            )
            nc.vector.tensor_tensor(
                out=add_base[:], in0=ident_b[:], in1=ident_b[:, P - 1 : P].to_broadcast([P, P]), op=ALU.max
            )
            win_t = setup.tile([P, 2, GROUP, SLOTS], F32)
            nc.vector.memset(win_t[:], 0.0)
            for layer, taus in enumerate(LAYER_TAUS):
                for j, tau, o in taps_of(taus):
                    nc.vector.tensor_copy(
                        out=win_t[:, layer, :, (TAPS * j + tau - layer - 1) // 2], in_=ident_f[:, PAD - o : PAD - o + GROUP]
                    )
            win = setup.tile([P, 2, PAD + P], BF16)
            nc.vector.memset(win[:], 0.0)
            gains_pad = setup.tile([P, 2, GROUP, SLOTS], BF16)
            gains_by_j = gains_hg[:].rearrange("p t (a j) -> p t a j", j=SCALES)
            for twin in range(2):
                nc.vector.tensor_copy(out=gains_pad[:, :, :, twin:SLOTS:2], in_=gains_by_j[:, :, :, 0 : SLOTS // 2])

            nc.vector.memset(class_wide[:], 0.0)
            for c in range(3):
                nc.vector.tensor_reduce(out=class3[:, c : c + 1], in_=ident_f[:, c:TOKENS:3], op=ALU.add, axis=AXIS_X)
            nc.vector.tensor_copy(out=v_sb[:, :, HEAD_DIM:], in_=class3.unsqueeze(1).to_broadcast([P, HEADS, 4]))
            nc.vector.tensor_scalar(out=sign3[:], in0=class3, scalar1=-2.0, scalar2=1.0, op0=ALU.mult, op1=ALU.add)
            for c in range(3):
                n_c = len(range(c, TOKENS, 3))
                nc.vector.tensor_scalar(
                    out=tap_coef[:, c:TOKENS:3],
                    in0=class3[:, c : c + 1].to_broadcast([P, n_c]),
                    scalar1=D4[3] - D4[1],
                    scalar2=D4[1],
                    op0=ALU.mult,
                    op1=ALU.add,
                )

            small_all = setup.tile([P, n_pb + HEADS], F32)
            pb_all = small_all[:, 0:n_pb]
            pb_by_tau = pb_all.rearrange("p (j t h) -> p t h j", t=TAPS, h=HEADS)
            bypass_all = small_all[:, n_pb:]

            x_words = x_sb[:].bitcast(F32)
            grouped = setup.tile([P, PASSES, TOKENS, 4], BF16, align_bytes=64)
            grouped_flat = grouped[:].rearrange("p g t e -> p (g t e)")
            grouped_words = grouped_flat.bitcast(F32).rearrange("p (g t u) -> p g t u", g=PASSES, u=2)

            def transpose_x(first_pair, last_pair):
                for pair in range(first_pair, last_pair):
                    xt = work.tile([P, 2, 2, TOKENS], F32, tag="work")
                    for gi in range(2):
                        g = 2 * pair + gi
                        for u in range(2):
                            nc.tensor.transpose(xt[:, gi, u, :], x_words[:, 256 * g + u : 256 * (g + 1) : 2], ident_f[:])
                    nc.scalar.copy(
                        out=grouped_words[:, 2 * pair : 2 * pair + 2, :, :], in_=xt[:].rearrange("p g u t -> p g t u")
                    )

            transpose_x(0, PASSES // 2)
            for quarter in range(4):
                cols = slice(4 * TOKENS * quarter, 4 * TOKENS * (quarter + 1))
                nc.vector.quantize_mx(
                    out=x_codes[:, cols].bitcast(FP8X4),
                    scales=x_scales[:, cols],
                    in_=grouped_flat[:, 4 * K_PASS * quarter : 4 * K_PASS * (quarter + 1)],
                )
            half = (n_pb + HEADS) // 2
            for i in range(2):
                ps = work.tile([P, half], F32, tag="work")
                nc.tensor.matmul(out=ps[:], lhsT=ones_b[:], rhs=small_row[:, half * i : half * (i + 1)], start=True, stop=True)
                nc.vector.tensor_copy(out=small_all[:, half * i : half * (i + 1)], in_=ps[:])
            win_ps = work.tile([P, 2, P], F32, tag="work")
            for layer in range(2):
                nc.tensor.transpose(win_ps[:, layer, :], win_t[:, layer, :, :].rearrange("p a s -> p (a s)"), ident_f[:])
            nc.scalar.copy(out=win[:, :, 0:P], in_=win_ps[:])
            gains_ps = work.tile([P, 2, P], BF16, tag="work")
            for t in range(2):
                nc.tensor.transpose(gains_ps[:, t, :], gains_pad[:, t, :, :].rearrange("p a s -> p (a s)"), ident_b[:])

            bias_moving = setup.tile([P, 3, GROUP, HEADS], BF16)
            for layer in range(2):
                picked = setup.tile([P, HEADS, SLOTS], F32, tag="picked", bufs=2)
                nc.vector.tensor_tensor(
                    out=picked[:],
                    in0=pb_all.rearrange("p (r h) -> p h r", h=HEADS)[:, :, layer + 1 : layer + 2 * SLOTS : 2],
                    in1=slot_of_row[:].unsqueeze(1).to_broadcast([P, HEADS, SLOTS]),
                    op=ALU.mult,
                )
                pb_rows = setup.tile([P, HEADS], F32, tag="pb_rows", bufs=2)
                nc.vector.tensor_reduce(out=pb_rows[:], in_=picked[:], op=ALU.add, axis=AXIS_X)
                nc.vector.tensor_tensor(
                    out=bias_moving[:, layer, :, :],
                    in0=pb_rows[:].unsqueeze(1).to_broadcast([P, GROUP, HEADS]),
                    in1=token_of_row[:].unsqueeze(2).to_broadcast([P, GROUP, HEADS]),
                    op=ALU.mult,
                )
            nc.vector.tensor_scalar_mul(out=bias_moving[:, 2, :, :], in0=bias_moving[:, 0, :, :], scalar1=-1.0)
            gains_rows = setup.tile([P, GROUPS, HEADS], BF16)
            nc.vector.tensor_copy(
                out=gains_rows[:], in_=gains_ps[:].rearrange("p t c -> p (t c)").rearrange("p (h g) -> p g h", h=HEADS)
            )
            gain_moving = setup.tile([P, GROUPS, GROUP, HEADS], BF16)
            for a in range(GROUP):
                nc.vector.tensor_scalar_mul(out=gain_moving[:, :, a, :], in0=gains_rows[:], scalar1=token_of_row[:, a : a + 1])

            def table_quarter(quarter):
                cols = slice(4 * GROUP * quarter, 4 * GROUP * (quarter + 1))
                for layer in range(2):
                    bias_ps = work.tile([P, 4 * GROUP, HEADS], F32, tag="work")
                    gain_ps = work.tile([P, 4 * GROUP, HEADS], F32, tag="work")
                    for gl in range(4):
                        grp = 4 * quarter + gl
                        rows = slice(GROUP * gl, GROUP * (gl + 1))
                        wins = [win[:, i, PAD - GROUP * grp : PAD - GROUP * grp + P] for i in range(2)]
                        nc.tensor.matmul(
                            out=bias_ps[:, rows, :], lhsT=wins[layer], rhs=bias_moving[:, layer, :, :], start=True, stop=(layer == 0)
                        )
                        if layer == 1:
                            nc.tensor.matmul(
                                out=bias_ps[:, rows, :], lhsT=wins[0], rhs=bias_moving[:, 2, :, :], start=False, stop=True
                            )
                        nc.tensor.matmul(
                            out=gain_ps[:, rows, :], lhsT=wins[layer], rhs=gain_moving[:, grp, :, :], start=True, stop=True
                        )
                    bias_in = bias_ps[:].rearrange("p n h -> p h n")
                    if layer == 0:
                        nc.scalar.activation(
                            out=base_tab[:, :, cols], in_=bias_in, func=ACT.Identity, bias=ident_f[:, P - 1 : P]
                        )
                    else:
                        nc.scalar.copy(out=step_tab[:, :, cols], in_=bias_in)
                    gain_in = gain_ps[:].rearrange("p n h -> p h n")
                    if layer == 0:
                        coef = tap_coef[:, cols].unsqueeze(1).to_broadcast([P, HEADS, 4 * GROUP])
                        nc.vector.tensor_tensor(out=gain_tab[:, layer, :, cols], in0=gain_in, in1=coef, op=ALU.mult)
                    else:
                        nc.vector.tensor_scalar_mul(out=gain_tab[:, layer, :, cols], in0=gain_in, scalar1=D4[2])

            def spread_b_qkv(first, last):
                for i in range(first, last):
                    ps = work.tile([P, 4, P], F32, tag="work")
                    for j in range(4):
                        row = 4 * i + j
                        nc.tensor.matmul(
                            out=ps[:, j, :],
                            lhsT=ident_b[:, row : row + 1].to_broadcast([P, P]),
                            rhs=bias_rows[:],
                            start=True,
                            stop=True,
                        )
                    nc.scalar.copy(out=bias_all[:, BANK * i : BANK * (i + 1)], in_=ps[:].rearrange("p j c -> p (j c)"))

            gains_nt = setup.tile([P, HEADS, SCALES], F32)

            def transpose_gains():
                for j0 in range(0, SCALES, 8):
                    n_j = min(8, SCALES - j0)
                    ps = work.tile([P, 8, P], BF16, tag="work")
                    for j in range(n_j):
                        nc.tensor.transpose(ps[:, j, :], gains_h[:, j0 + j : TOKENS * SCALES : SCALES], ident_b[:])
                    nc.vector.tensor_copy(
                        out=gains_nt[:, :, j0 : j0 + n_j], in_=ps[:, 0:n_j, 0:HEADS].rearrange("p j h -> p h j")
                    )

            soft = setup.tile([P, HEADS], F32)
            n_f = TAPS * 8 * HEADS
            f_of_bias = setup.tile([P, n_f], F32)
            f_tmp = setup.tile([P, n_f], F32)

            def bias_functions():
                nc.scalar.activation(out=soft[:], in_=bypass_all, func=ACT.Abs)
                nc.scalar.activation(out=soft[:], in_=soft[:], func=ACT.Exp, scale=-1.0)
                nc.scalar.activation(out=soft[:], in_=soft[:], func=ACT.Ln, bias=ones_f[:, 0:1])
                nc.scalar.activation(out=f_of_bias[:], in_=pb_all[:, 0:n_f], func=ACT.Exp)

            def small_tables():
                nc.vector.scalar_tensor_tensor(
                    out=diag_gain[:, :, SCALES], in0=bypass_all, scalar=0.0, in1=soft[:], op0=ALU.max, op1=ALU.add
                )
                nc.vector.tensor_scalar_mul(out=diag_gain[:, :, 0:SCALES], in0=gains_nt[:], scalar1=D4[0])
                nc.vector.memset(diag_bias[:, :, SCALES], 1.0)
                nc.vector.tensor_scalar_add(out=diag_bias[:, :, 0:SCALES], in0=pb_by_tau[:, 0, :, :], scalar1=1.0)

                nc.vector.tensor_scalar(out=f_tmp[:], in0=pb_all[:, 0:n_f], scalar1=0.0, scalar2=1.0, op0=ALU.max, op1=ALU.add)
                nc.vector.tensor_tensor(out=f_of_bias[:], in0=f_of_bias[:], in1=f_tmp[:], op=ALU.min)
                for tau in range(1, TAPS):
                    nc.vector.tensor_scalar_mul(out=before[:, tau - 1, :], in0=before[:, tau - 1, :], scalar1=abs(D4[tau]))
                gf = setup.tile([P, HEADS, TAPS - 1, 8], F32)
                nc.vector.tensor_tensor(
                    out=gf[:],
                    in0=f_of_bias[:].rearrange("p (j t h) -> p h t j", t=TAPS, h=HEADS)[:, :, 1:TAPS, :],
                    in1=gains_nt[:, :, 0:8].unsqueeze(2).to_broadcast([P, HEADS, TAPS - 1, 8]),
                    op=ALU.mult,
                )
                nc.vector.tensor_tensor(
                    out=gf[:], in0=gf[:], in1=before[:].unsqueeze(1).to_broadcast([P, HEADS, TAPS - 1, 8]), op=ALU.mult
                )
                gf_sum = setup.tile([P, HEADS], F32)
                nc.vector.tensor_reduce(out=gf_sum[:], in_=gf[:].rearrange("p h t j -> p h (t j)"), op=ALU.add, axis=AXIS_X)
                nc.vector.tensor_scalar_add(out=z_fixed[:], in0=gf_sum[:], scalar1=EPS)

            q0, k0, q1, k1 = [accs.tile([P, BANK], F32, tag="acc", name="acc_%s" % n) for n in ("q0", "k0", "q1", "k1")]

            def qk_passes(first, last):
                mx_passes(first, min(last, qk_load), [q0, q1, k0, k1])
                mx_passes(max(first, qk_load), last, [q0, q1, k0])

            bias_functions()
            for quarter in range(4):
                qk_passes(quarter, quarter + 1)
                table_quarter(quarter)
            qk_passes(4, 5)
            transpose_gains()
            small_tables()
            qk_passes(5, 6)
            spread_b_qkv(0, 6)
            qk_passes(6, q0_load)

        with tc.tile_pool(name="dense", bufs=2) as dense:
            toks, trs, k_ts, prods = {}, {}, {}, {}
            sts, us, fs = {}, {}, {}

            def to_sbuf(key, bank, col0):
                width = bank.shape[1]
                tok = dense.tile([P, width], F32, tag="tok", bufs=4)
                nc.vector.tensor_tensor(out=tok[:], in0=bank[:], in1=bias_all[:, col0 : col0 + width], op=ALU.add)
                toks[key] = tok

            def transposes(key):
                n_pairs = toks[key].shape[1] // P
                tr = work.tile([P, n_pairs, TOKENS], F32, tag="work")
                for pair in range(n_pairs):
                    nc.tensor.transpose(tr[:, pair, :], toks[key][:, P * pair : P * (pair + 1)], ident_f[:])
                trs[key] = tr

            for half_i in range(2):
                k_t = dense.tile([P, 4, TOKENS], F32, tag="k_t")
                k_ts[half_i] = k_t

            def plain_k(half_i):
                for two in (slice(0, 2), slice(2, 4)):
                    nc.scalar.copy(out=k_ts[half_i][:, two, :], in_=trs["k", half_i][:, two, :])

            def split_q(b):
                two = slice(2 * (b % 2), 2 * (b % 2) + 2)
                for hd in range(2):
                    rows = slice(HEAD_DIM * hd, HEAD_DIM * (hd + 1))
                    nc.scalar.copy(out=q_split[b // 2][rows, two, hd, :], in_=trs["q", b // 2][rows, two, :])

            def scores(b):
                st = work.tile([P, 4, TOKENS], F32, tag="work")
                for i in range(2):
                    pair = 2 * (b % 2) + i
                    out_i = st[:, 2 * i : 2 * i + 2, :]
                    nc.tensor.matmul(
                        out=out_i,
                        lhsT=add_base[:],
                        rhs=base_tab[:, 4 * b + 2 * i : 4 * b + 2 * i + 2, :],
                        start=True,
                        stop=False,
                    )
                    nc.tensor.matmul(
                        out=out_i, lhsT=k_ts[b // 2][:, pair, :], rhs=q_split[b // 2][:, pair, :, :], start=False, stop=True
                    )
                sts[b] = st

            dots = dense.tile([P, HEADS], F32, bufs=1)

            def same_token_products(half_i):
                prod = dense.tile([P, BANK], F32, tag="prod")
                nc.vector.tensor_tensor(out=prod[:], in0=toks["q", half_i][:], in1=toks["k", half_i][:], op=ALU.mult)
                prods[half_i] = prod

            def same_token_dots(half_i):
                for i in range(8):
                    cols = slice(HEAD_DIM * i, HEAD_DIM * (i + 1))
                    nc.scalar.activation(
                        out=prods[half_i][:, cols],
                        in_=prods[half_i][:, cols],
                        func=ACT.Identity,
                        accum_out=dots[:, 8 * half_i + i : 8 * half_i + i + 1],
                    )

            def exponentials(b):
                u = dense.tile([P, 4, TOKENS], F32, tag="u", bufs=3)
                nc.vector.tensor_tensor(out=u[:], in0=sts[b][:], in1=step_tab[:, 4 * b : 4 * b + 4, :], op=ALU.add)
                f = dense.tile([P, 2, 4, TOKENS], F32, tag="f", bufs=3)
                us[b] = (sts[b], u)
                for layer in range(2):
                    nc.scalar.activation(out=f[:, layer, :, :], in_=us[b][layer][:], func=ACT.Exp, bias=minus_one[:])
                fs[b] = f

            def clip(b):
                for layer in range(2):
                    f = fs[b][:, layer, :, :]
                    nc.vector.scalar_tensor_tensor(out=f, in0=us[b][layer][:], scalar=1.0, in1=f, op0=ALU.max, op1=ALU.min)

            def weigh(b):
                nc.vector.tensor_tensor(
                    out=fs[b][:].rearrange("p l h n -> p l (h n)"),
                    in0=fs[b][:].rearrange("p l h n -> p l (h n)"),
                    in1=gain_tab[:, :, 4 * b : 4 * b + 4, :].rearrange("p l h n -> p l (h n)"),
                    op=ALU.mult,
                )

            def add_layers(b):
                nc.vector.tensor_tensor(
                    out=at_all[:, 4 * b : 4 * b + 4, :], in0=fs[b][:, 0, :, :], in1=fs[b][:, 1, :, :], op=ALU.add
                )

            n_t = SCALES + 1
            u_diag = dense.tile([P, HEADS, n_t], F32, bufs=1)
            f_diag = dense.tile([P, HEADS, n_t], F32, bufs=1)
            halves = [slice(0, 8), slice(8, 16)]

            def same_token_exp(half_i):
                heads = halves[half_i]
                nc.vector.tensor_tensor(
                    out=u_diag[:, heads, :],
                    in0=dots[:, heads].unsqueeze(2).to_broadcast([P, 8, n_t]),
                    in1=diag_bias[:, heads, :],
                    op=ALU.add,
                )
                nc.scalar.activation(out=f_diag[:, heads, :], in_=u_diag[:, heads, :], func=ACT.Exp, bias=minus_one[:])

            def same_token_clip(half_i):
                f = f_diag[:, halves[half_i], :]
                nc.vector.scalar_tensor_tensor(
                    out=f, in0=u_diag[:, halves[half_i], :], scalar=1.0, in1=f, op0=ALU.max, op1=ALU.min
                )

            def same_token_weigh(half_i):
                f = f_diag[:, halves[half_i], :]
                nc.vector.tensor_tensor(out=f, in0=f, in1=diag_gain[:, halves[half_i], :], op=ALU.mult)

            def same_token_sum(half_i):
                nc.vector.tensor_reduce(
                    out=w_diag[:, halves[half_i]], in_=f_diag[:, halves[half_i], :], op=ALU.add, axis=AXIS_X
                )

            def same_token_z(half_i):
                heads = halves[half_i]
                nc.vector.tensor_tensor(out=z_parts[:, heads, 3], in0=w_diag[:, heads], in1=z_fixed[:, heads], op=ALU.add)

            v_diag = dense.tile([P, HEADS, HEAD_DIM], F32, bufs=1)
            o_sb = dense.tile([P, HEADS, HEAD_DIM], F32, bufs=1)
            z_sum = dense.tile([P, HEADS], F32, bufs=1)
            out_rows = out.rearrange("o n e -> (o n) e")
            o_pss, sums_pss = {}, {}

            def of_bank(b):
                return slice(4 * b, 4 * b + 4)

            def biased_v(b):
                nc.vector.tensor_tensor(
                    out=v_sb[:, of_bank(b), 0:HEAD_DIM],
                    in0=v_of_bank[b].rearrange("p (h d) -> p h d", d=HEAD_DIM),
                    in1=bias_all[:, 2 * EMB :].rearrange("p (h d) -> p h d", d=HEAD_DIM)[:, of_bank(b), :],
                    op=ALU.add,
                )

            def weighted_sums(b):
                o_ps = work.tile([P, 4, HEAD_DIM + 4], F32, tag="work")
                for i in range(4):
                    h = 4 * b + i
                    nc.tensor.matmul(out=o_ps[:, i, :], lhsT=at_all[:, h, :], rhs=v_sb[:, h, :], start=True, stop=True)
                o_pss[b] = o_ps

            def same_token_v(b):
                nc.vector.tensor_tensor(
                    out=v_diag[:, of_bank(b), :],
                    in0=v_sb[:, of_bank(b), 0:HEAD_DIM],
                    in1=w_diag[:, of_bank(b)].unsqueeze(2).to_broadcast([P, 4, HEAD_DIM]),
                    op=ALU.mult,
                )

            def signed_sums(heads, sums):
                nc.vector.tensor_tensor(
                    out=z_parts[:, heads, 0:3],
                    in0=sums,
                    in1=sign3[:, 0:3].unsqueeze(1).to_broadcast([P, heads.stop - heads.start, 3]),
                    op=ALU.mult,
                )

            def class_sums(b):
                signed_sums(of_bank(b), o_pss[b][:, :, HEAD_DIM : HEAD_DIM + 3])

            def column_sums(b):
                sums_ps = work.tile([P, 4, CLASS_WIDTH], F32, tag="work")
                for i in range(4):
                    nc.tensor.matmul(out=sums_ps[:, i, :], lhsT=at_all[:, 4 * b + i, :], rhs=class_wide[:], start=True, stop=True)
                sums_pss[b] = sums_ps

            def numerator(b):
                nc.vector.tensor_tensor(
                    out=v_diag[:, of_bank(b), :], in0=o_pss[b][:, :, 0:HEAD_DIM], in1=v_diag[:, of_bank(b), :], op=ALU.add
                )

            def sum_z(heads):
                nc.vector.tensor_reduce(out=z_sum[:, heads], in_=z_parts[:, heads, :], op=ALU.add, axis=AXIS_X)

            def invert_z(heads):
                nc.vector.reciprocal(out=z_inv[:, heads], in_=z_sum[:, heads])

            def quotient(b):
                nc.vector.tensor_tensor(
                    out=o_sb[:, of_bank(b), :],
                    in0=v_diag[:, of_bank(b), :],
                    in1=z_inv[:, of_bank(b)].unsqueeze(2).to_broadcast([P, 4, HEAD_DIM]),
                    op=ALU.mult,
                )

            def scale_w(heads):
                nc.vector.tensor_tensor(out=w_diag[:, heads], in0=w_diag[:, heads], in1=z_inv[:, heads], op=ALU.mult)

            def finish(b):
                for i in range(4):
                    h = 4 * b + i
                    nc.vector.scalar_tensor_tensor(
                        out=o_sb[:, h, :],
                        in0=o_pss[b][:, i, 0:HEAD_DIM],
                        scalar=z_inv[:, h : h + 1],
                        in1=v_diag[:, h, :],
                        op0=ALU.mult,
                        op1=ALU.add,
                    )

            def store(first, last):
                cols = slice(4 * HEAD_DIM * first, 4 * HEAD_DIM * (last + 1))
                nc.sync.dma_start(out=out_rows[:, cols], in_=o_sb[:].rearrange("p h d -> p (h d)")[:, cols])

            v0 = accs.tile([P, BANK], F32, tag="acc")
            v2, v3 = [accs.tile([P, BANK // 2], F32, tag="acc", name="acc_v%d" % b) for b in (2, 3)]
            v_banks = [v0, v2, v3]
            v_of_bank = [v0[:, 0 : BANK // 2], v0[:, BANK // 2 :], v2[:], v3[:]]

            mx_passes(q0_load, k0_load, [q0])
            to_sbuf(("q", 0), q0, 0)
            transposes(("q", 0))
            split_q(0)
            split_q(1)
            mx_passes(k0_load, q1_load, [k0])
            to_sbuf(("k", 0), k0, EMB)
            transposes(("k", 0))
            plain_k(0)
            same_token_products(0)
            mx_passes(q1_load, k1_load, [q1])
            scores(0)
            scores(1)
            to_sbuf(("q", 1), q1, BANK)
            same_token_dots(0)
            exponentials(0)
            same_token_exp(0)
            exponentials(1)
            transposes(("q", 1))
            mx_passes(k1_load, v_load, [k1])
            split_q(2)
            split_q(3)
            clip(0)
            clip(1)
            same_token_clip(0)
            to_sbuf(("k", 1), k1, EMB + BANK)
            same_token_weigh(0)
            weigh(0)
            transposes(("k", 1))
            plain_k(1)
            weigh(1)
            same_token_sum(0)
            add_layers(0)
            same_token_z(0)
            same_token_products(1)
            scores(2)
            scores(3)
            mx_passes(v_load, v_load + 2, v_banks)
            exponentials(2)
            add_layers(1)
            exponentials(3)
            same_token_dots(1)
            mx_passes(v_load + 2, v0_load, v_banks)
            clip(2)
            clip(3)
            weigh(2)
            same_token_exp(1)
            add_layers(2)
            mx_passes(v0_load, v1_load - 1, [v0])
            column_sums(2)
            weigh(3)
            same_token_clip(1)
            add_layers(3)
            same_token_weigh(1)
            mx_passes(v1_load - 1, v1_load, [v0])
            column_sums(3)
            biased_v(0)
            same_token_sum(1)
            biased_v(1)
            weighted_sums(0)
            same_token_v(0)
            same_token_z(1)
            same_token_v(1)
            signed_sums(of_bank(2), sums_pss[2][:, :, 0:3])
            signed_sums(of_bank(3), sums_pss[3][:, :, 0:3])
            weighted_sums(1)
            mx_passes(v1_load, v1_load + 1, [v2, v3])
            class_sums(0)
            sum_z(halves[1])
            numerator(0)
            invert_z(halves[1])
            mx_passes(v1_load + 1, v2_load, [v2, v3])
            class_sums(1)
            scale_w(halves[1])
            sum_z(halves[0])
            numerator(1)
            invert_z(halves[0])
            mx_passes(v2_load, v2_load + 1, [v3])
            mx_passes(v2_load + 1, v2_load + 2, [v2])
            quotient(0)
            biased_v(3)
            biased_v(2)
            quotient(1)
            store(0, 1)
            weighted_sums(3)
            same_token_v(3)
            weighted_sums(2)
            same_token_v(2)
            finish(3)
            store(3, 3)
            finish(2)
            store(2, 2)
